import numpy as np
import ml_dtypes


def mxq(x, axis, fmt="e4m3"):
    dtype, down = {"e4m3": (ml_dtypes.float8_e4m3fn, 7), "e5m2": (ml_dtypes.float8_e5m2, 14)}[fmt]
    v = np.moveaxis(np.asarray(x, np.float32).astype(ml_dtypes.bfloat16).astype(np.float64), axis, -1)
    blocks = v.reshape(v.shape[:-1] + (-1, 32))
    amax = np.abs(blocks).max(-1, keepdims=True)
    byte = np.maximum(np.where(amax > 0, np.frexp(amax)[1] - 1 + 127, 0) - down, 1)
    scale = np.exp2(byte - 127.0)
    codes = (blocks / scale).astype(np.float32).astype(dtype).astype(np.float64)
    return np.moveaxis((codes * scale).reshape(v.shape), -1, axis)


WIDE = False


def mx_kscale(k):
    if not WIDE:
        return np.ones(k)
    levels = np.array([10, -10, 5, -5, 0])
    a = np.random.permutation(np.resize(levels, k // 512 * 4)).reshape(k // 512, 4)
    idx = np.arange(k)
    return np.exp2(a[idx // 512, idx % 128 // 32])


BF16 = ml_dtypes.bfloat16


def bf(x):
    return np.asarray(x, np.float32).astype(BF16)


def f64(x):
    return np.asarray(x).astype(np.float64)


N, F, U, G, P = 1024, 512, 512, 3, 3
C = G + P
T = G + 2 * P + 1
LO, HI = -1.0, 1.0
LN_EPS = 0.001


def b_splines(x, grid):
    xe = x[..., None]
    bases = np.where((xe >= grid[..., :-1]) & (xe < grid[..., 1:]), 1.0, 0.0)
    for k in range(1, P + 1):
        left = (xe - grid[..., :-(k + 1)]) / (grid[..., k:-1] - grid[..., :-(k + 1)])
        right = (grid[..., k + 1:] - xe) / (grid[..., k + 1:] - grid[..., 1:-k])
        bases = left * bases[..., :-1] + right * bases[..., 1:]
    return bases.reshape(x.shape[0], -1)


def setup_inputs():
    t = mx_kscale(F)
    h = (HI - LO) / G
    knots = np.linspace(LO - P * h, LO + (G + P) * h, T)
    grid = knots[None, None, :] + (np.random.random_sample((1, F, T)) - 0.5) * 0.25 * h
    return {
        "x": bf(np.random.standard_normal((N, F)) * 0.1 + np.random.standard_normal((N, 1)) * 0.1),
        "ln_gamma": bf((1.0 + 0.1 * np.random.standard_normal(F)) * t),
        "ln_beta": bf(0.1 * np.random.standard_normal(F) * t),
        "base_weight": bf(np.random.standard_normal((F, U)) / np.sqrt(F) / t[:, None]),
        "base_bias": bf(0.25 * np.random.standard_normal(U)),
        "spline_weight": bf(np.random.standard_normal((F * C, U)) / np.sqrt(F)),
        "grid": bf(grid * t[None, :, None]),
    }


def reference(x, ln_gamma, ln_beta, base_weight, base_bias, spline_weight, grid):
    x = f64(x)
    mean = x.mean(-1, keepdims=True)
    var = x.var(-1, keepdims=True)
    xn = (x - mean) / np.sqrt(var + LN_EPS) * f64(ln_gamma) + f64(ln_beta)
    base_out = (mxq(np.maximum(xn, 0.0), 1, "e4m3") @ mxq(f64(base_weight), 0, "e4m3")) + f64(base_bias)
    spline_out = mxq(b_splines(xn, f64(grid)), 1, "e4m3") @ mxq(f64(spline_weight), 0, "e4m3")
    return base_out + spline_out

@@ -1,0 +1,250 @@
+from contextlib import ExitStack
+
+import concourse.mybir as mybir
+from concourse.masks import make_identity
+
+F32 = mybir.dt.float32
+BF16 = mybir.dt.bfloat16
+U32 = mybir.dt.uint32
+U8 = mybir.dt.uint8
+FP8X4 = mybir.dt.float8_e4m3fn_x4
+ALU = mybir.AluOpType
+ACT = mybir.ActivationFunctionType
+
+P = 128
+PACK = 4
+ROWS = 1024
+FEATURES = 512
+UNITS = 512
+KNOTS = 10
+BASES = 6
+CHUNKS = FEATURES // P
+HALF = 512
+HALVES = ROWS // HALF
+ROW_TILES = HALF // P
+PLANES = CHUNKS * BASES
+SPLINE_PASSES = PLANES // PACK
+LN_EPS = 0.001
+
+FLOPS = 2 * ROWS * (FEATURES + FEATURES * BASES) * UNITS
+
+
+def tile_kanlinear_pa_kernel(tc, x, ln_gamma, ln_beta, base_weight, base_bias, spline_weight, grid, out):
+    nc = tc.nc
+    with ExitStack() as ctx:
+        const = ctx.enter_context(tc.tile_pool(name="const", bufs=1))
+        keep = ctx.enter_context(tc.tile_pool(name="keep", bufs=1))
+        work = ctx.enter_context(tc.tile_pool(name="work", bufs=2))
+        psum_t = ctx.enter_context(tc.psum_pool(name="psum_t", bufs=2))
+        psum_acc = ctx.enter_context(tc.psum_pool(name="psum_acc", bufs=6))
+
+        grid_bf = const.tile([P, CHUNKS, KNOTS], BF16, name="grid_bf")
+        nc.sync.dma_start(out=grid_bf[:], in_=grid.rearrange("o (c p) t -> p (o c) t", p=P))
+        gamma_bf = const.tile([P, CHUNKS], BF16, name="gamma_bf")
+        beta_bf = const.tile([P, CHUNKS], BF16, name="beta_bf")
+        with nc.allow_non_contiguous_dma(reason="512 two-byte elements, one to a partition and chunk"):
+            nc.sync.dma_start(out=gamma_bf[:], in_=ln_gamma.rearrange("(c p) -> p c", p=P))
+            nc.sync.dma_start(out=beta_bf[:], in_=ln_beta.rearrange("(c p) -> p c", p=P))
+        x_bf = []
+        for h in range(HALVES):
+            x_half = keep.tile([P, ROW_TILES, FEATURES], BF16, name="x_half%d" % h)
+            nc.sync.dma_start(
+                out=x_half[:], in_=x[h * HALF : (h + 1) * HALF, :].rearrange("(t p) f -> p t f", p=P)
+            )
+            x_bf.append(x_half)
+        base_raw = keep.tile([P, PACK, UNITS], BF16, name="base_raw")
+        nc.sync.dma_start(out=base_raw[:], in_=base_weight.rearrange("(c p) u -> p c u", p=P))
+        bias_bc = const.tile([P, UNITS], BF16, name="bias_bc")
+        nc.sync.dma_start(out=bias_bc[:], in_=base_bias.partition_broadcast(P))
+        spline_raw = keep.tile([P, PLANES, UNITS], BF16, name="spline_raw")
+        for c in range(CHUNKS):
+            nc.sync.dma_start(
+                out=spline_raw[:, c * BASES : (c + 1) * BASES, :].rearrange("p j u -> p (j u)"),
+                in_=spline_weight[c * P * BASES : (c + 1) * P * BASES, :].rearrange("(p j) u -> p (j u)", j=BASES),
+            )
+
+        ident = const.tile([P, P], F32, name="ident")
+        make_identity(nc, ident[:])
+        one = const.tile([P, 1], F32, name="one")
+        nc.vector.memset(one[:], 1.0)
+        warm = const.tile([P, 1], F32, name="warm")
+        nc.scalar.activation(out=warm[:], in_=one[:], func=ACT.Sqrt)
+
+        gamma = const.tile([P, CHUNKS], F32, name="gamma")
+        beta = const.tile([P, CHUNKS], F32, name="beta")
+        nc.vector.tensor_copy(out=gamma[:], in_=gamma_bf[:])
+        nc.vector.tensor_copy(out=beta[:], in_=beta_bf[:])
+
+        g = const.tile([P, CHUNKS, KNOTS], F32, name="g")
+        neg_g = const.tile([P, CHUNKS, KNOTS], F32, name="neg_g")
+        nc.vector.tensor_copy(out=g[:], in_=grid_bf[:])
+        nc.vector.tensor_scalar_mul(out=neg_g[:], in0=g[:], scalar1=-1.0)
+        den = const.tile([P, CHUNKS, 23], F32, name="den")
+        d1 = den[:, :, 14:23]
+        d2 = const.tile([P, CHUNKS, KNOTS - 2], F32, name="d2")
+        d3 = const.tile([P, CHUNKS, KNOTS - 3], F32, name="d3")
+        d4 = const.tile([P, CHUNKS, KNOTS - 4], F32, name="d4")
+        neg_d4 = const.tile([P, CHUNKS, KNOTS - 4], F32, name="neg_d4")
+        nc.vector.tensor_sub(out=d1, in0=g[:, :, 1:10], in1=g[:, :, 0:9])
+        nc.vector.tensor_sub(out=d2[:], in0=g[:, :, 2:10], in1=g[:, :, 0:8])
+        nc.vector.tensor_sub(out=d3[:], in0=g[:, :, 3:10], in1=g[:, :, 0:7])
+        nc.vector.tensor_sub(out=d4[:], in0=g[:, :, 4:10], in1=g[:, :, 0:6])
+        nc.vector.tensor_sub(out=neg_d4[:], in0=g[:, :, 0:6], in1=g[:, :, 4:10])
+        prod_a = const.tile([P, CHUNKS, 7], F32, name="prod_a")
+        prod_b = const.tile([P, CHUNKS, 7], F32, name="prod_b")
+        nc.vector.tensor_mul(out=prod_a[:], in0=den[:, :, 14:21], in1=d2[:, :, 0:7])
+        nc.vector.tensor_mul(out=prod_b[:], in0=den[:, :, 16:23], in1=d2[:, :, 1:8])
+        nc.vector.tensor_mul(out=den[:, :, 0:7], in0=prod_a[:], in1=d3[:])
+        nc.vector.tensor_mul(out=den[:, :, 7:14], in0=prod_b[:], in1=d3[:])
+        inv = const.tile([P, CHUNKS, 23], F32, name="inv")
+        nc.vector.reciprocal(out=inv[:], in_=den[:])
+        a0 = inv[:, :, 0:6]
+        a1 = const.tile([P, CHUNKS, BASES], F32, name="a1")
+        neg_c3 = const.tile([P, CHUNKS, BASES], F32, name="neg_c3")
+        neg_c4 = const.tile([P, CHUNKS, BASES], F32, name="neg_c4")
+        nc.vector.tensor_mul(out=a1[:], in0=d4[:], in1=inv[:, :, 14:20])
+        nc.vector.tensor_mul(out=a1[:], in0=a1[:], in1=inv[:, :, 1:7])
+        nc.vector.tensor_mul(out=neg_c3[:], in0=neg_d4[:], in1=inv[:, :, 17:23])
+        nc.vector.tensor_mul(out=neg_c3[:], in0=neg_c3[:], in1=inv[:, :, 7:13])
+        nc.vector.tensor_scalar_mul(out=neg_c4[:], in0=inv[:, :, 8:14], scalar1=-1.0)
+
+        def layer_norm(h):
+            stats = work.tile([P, ROW_TILES, 6], F32, name="stats")
+            mean_var = work.tile([P, ROW_TILES, 2], F32, name="mean_var")
+            for t in range(ROW_TILES):
+                nc.vector.bn_stats(out=stats[:, t, :], in_=x_bf[h][:, t, :])
+                nc.vector.bn_aggr(out=mean_var[:, t, :], in_=stats[:, t, :])
+            var_eps = work.tile([P, ROW_TILES], F32, name="var_eps")
+            nc.vector.tensor_scalar_add(out=var_eps[:], in0=mean_var[:, :, 1], scalar1=LN_EPS)
+            std = work.tile([P, ROW_TILES], F32, name="std")
+            nc.scalar.activation(out=std[:], in_=var_eps[:], func=ACT.Sqrt)
+            guess = work.tile([P, ROW_TILES], F32, name="guess")
+            nc.vector.reciprocal(out=guess[:], in_=std[:])
+            corr = work.tile([P, ROW_TILES], F32, name="corr")
+            nc.vector.tensor_mul(out=corr[:], in0=guess[:], in1=guess[:])
+            nc.vector.tensor_mul(out=corr[:], in0=corr[:], in1=var_eps[:])
+            nc.vector.tensor_scalar(out=corr[:], in0=corr[:], scalar1=-0.5, scalar2=1.5, op0=ALU.mult, op1=ALU.add)
+            rstd = work.tile([P, ROW_TILES], F32, name="rstd")
+            nc.vector.tensor_mul(out=rstd[:], in0=guess[:], in1=corr[:])
+            z_tiles = []
+            for t in range(ROW_TILES):
+                z = work.tile([P, FEATURES], F32, name="z", bufs=2 * ROW_TILES)
+                nc.vector.tensor_scalar(
+                    out=z[:],
+                    in0=x_bf[h][:, t, :],
+                    scalar1=mean_var[:, t, 0:1],
+                    scalar2=rstd[:, t : t + 1],
+                    op0=ALU.subtract,
+                    op1=ALU.mult,
+                )
+                z_tiles.append(z)
+            xn = keep.tile([P, CHUNKS, HALF], F32, name="xn%d" % h)
+            for c in range(CHUNKS):
+                z_t = psum_t.tile([P, HALF], F32, name="z_t")
+                for t in range(ROW_TILES):
+                    nc.tensor.transpose(z_t[:, t * P : (t + 1) * P], z_tiles[t][:, c * P : (c + 1) * P], ident[:])
+                nc.scalar.activation(
+                    out=xn[:, c, :], in_=z_t[:], func=ACT.Identity, scale=gamma[:, c : c + 1], bias=beta[:, c : c + 1]
+                )
+            return xn
+
+        w_codes = keep.tile([P, SPLINE_PASSES + 1, UNITS], U32, name="w_codes", align_bytes=64)
+        w_scales = keep.tile([P, SPLINE_PASSES + 1, UNITS], U8, name="w_scales", align_bytes=64)
+        BASE_PASS = SPLINE_PASSES
+
+        def quantise_weight(s, four_rows):
+            grouped_w = work.tile([P, UNITS, PACK], BF16, name="grouped_w", align_bytes=64)
+            nc.scalar.copy(out=grouped_w[:], in_=four_rows.rearrange("p t u -> p u t"))
+            nc.vector.quantize_mx(
+                out=w_codes[:, s, :].bitcast(FP8X4),
+                scales=w_scales[:, s, :],
+                in_=grouped_w[:].rearrange("p u t -> p (u t)"),
+            )
+
+        def multiply(s, acc, grouped, start, stop):
+            codes = work.tile([P, HALF], U32, name="codes", align_bytes=64, bufs=3)
+            scales = work.tile([P, HALF], U8, name="scales", align_bytes=64, bufs=3)
+            nc.vector.quantize_mx(
+                out=codes[:].bitcast(FP8X4), scales=scales[:], in_=grouped[:].rearrange("p n t -> p (n t)")
+            )
+            for m in range(ROW_TILES):
+                nc.tensor.matmul_mx(
+                    out=acc[m][:],
+                    lhsT=codes[:, m * P : (m + 1) * P].bitcast(FP8X4),
+                    lhsT_scale=scales[:, m * P : (m + 1) * P],
+                    rhs=w_codes[:, s, :].bitcast(FP8X4),
+                    rhs_scale=w_scales[:, s, :],
+                    start=start,
+                    stop=stop,
+                )
+
+        xn_halves = [layer_norm(h) for h in range(HALVES)]
+        quantise_weight(BASE_PASS, base_raw[:])
+
+        for h in range(HALVES):
+            xn = xn_halves[h]
+            acc = [psum_acc.tile([P, UNITS], F32, name="acc") for m in range(ROW_TILES)]
+            grouped = work.tile([P, HALF, PACK], BF16, name="grouped", align_bytes=64)
+            nc.vector.tensor_scalar_max(out=grouped[:], in0=xn[:].rearrange("p c n -> p n c"), scalar1=0.0)
+            multiply(BASE_PASS, acc, grouped, True, False)
+
+            left4 = None
+            right4 = None
+            for c in range(CHUNKS):
+                v = xn[:, c, :]
+                cubes = []
+                for i in range(KNOTS):
+                    square = work.tile([P, HALF], F32, name="square", bufs=4)
+                    nc.scalar.activation(out=square[:], in_=v, func=ACT.Square, bias=neg_g[:, c, i : i + 1])
+                    cube = work.tile([P, HALF], F32, name="cube", bufs=8)
+                    nc.vector.scalar_tensor_tensor(
+                        out=cube[:], in0=v, scalar=g[:, c, i : i + 1], in1=square[:], op0=ALU.subtract, op1=ALU.mult
+                    )
+                    cubes.append(cube)
+                    j = i - 4
+                    if j < 0:
+                        continue
+                    q = c * BASES + j
+                    s = q // PACK
+                    slot = q % PACK
+                    if slot == 0:
+                        left4 = work.tile([P, PACK, HALF], BF16, name="left4", bufs=3)
+                        right4 = work.tile([P, PACK, HALF], BF16, name="right4", bufs=3)
+                        if h == 0:
+                            quantise_weight(s, spline_raw[:, s * PACK : (s + 1) * PACK, :])
+                    inner_l = work.tile([P, HALF], F32, name="inner_l", bufs=3)
+                    nc.scalar.activation(out=inner_l[:], in_=cubes[j + 1][:], func=ACT.Relu, scale=a1[:, c, j : j + 1])
+                    nc.vector.scalar_tensor_tensor(
+                        out=left4[:, slot, :],
+                        in0=cubes[j][:],
+                        scalar=a0[:, c, j : j + 1],
+                        in1=inner_l[:],
+                        op0=ALU.mult,
+                        op1=ALU.subtract,
+                    )
+                    inner_r = work.tile([P, HALF], F32, name="inner_r", bufs=3)
+                    nc.scalar.activation(
+                        out=inner_r[:], in_=cubes[j + 3][:], func=ACT.Relu, scale=neg_c3[:, c, j : j + 1]
+                    )
+                    nc.vector.scalar_tensor_tensor(
+                        out=right4[:, slot, :],
+                        in0=cubes[j + 4][:],
+                        scalar=neg_c4[:, c, j : j + 1],
+                        in1=inner_r[:],
+                        op0=ALU.mult,
+                        op1=ALU.subtract,
+                    )
+                    if slot == PACK - 1:
+                        larger = work.tile([P, PACK, HALF], BF16, name="larger")
+                        nc.vector.tensor_max(out=larger[:], in0=left4[:], in1=right4[:])
+                        grouped = work.tile([P, HALF, PACK], BF16, name="grouped", align_bytes=64)
+                        nc.vector.tensor_scalar_max(
+                            out=grouped[:], in0=larger[:].rearrange("p t n -> p n t"), scalar1=0.0
+                        )
+                        multiply(s, acc, grouped, False, s == SPLINE_PASSES - 1)
+
+            for m in range(ROW_TILES):
+                result = work.tile([P, UNITS], F32, name="result", bufs=4)
+                nc.vector.tensor_add(out=result[:], in0=acc[m][:], in1=bias_bc[:])
+                row0 = h * HALF + m * P
+                nc.sync.dma_start(out=out[row0 : row0 + P, :], in_=result[:])

@@ -24,7 +24,10 @@ HALVES = ROWS // HALF
 ROW_TILES = HALF // P
 PLANES = CHUNKS * BASES
 SPLINE_PASSES = PLANES // PACK
+BASE_PASS = SPLINE_PASSES
 LN_EPS = 0.001
+RUN = 4
+VECTOR_COLS = 256
 
 FLOPS = 2 * ROWS * (FEATURES + FEATURES * BASES) * UNITS
 
@@ -35,16 +38,9 @@ def tile_kanlinear_pa_kernel(tc, x, ln_gamma, ln_beta, base_weight, base_bias, s
         const = ctx.enter_context(tc.tile_pool(name="const", bufs=1))
         keep = ctx.enter_context(tc.tile_pool(name="keep", bufs=1))
         work = ctx.enter_context(tc.tile_pool(name="work", bufs=2))
-        psum_t = ctx.enter_context(tc.psum_pool(name="psum_t", bufs=2))
-        psum_acc = ctx.enter_context(tc.psum_pool(name="psum_acc", bufs=6))
+        psum = ctx.enter_context(tc.psum_pool(name="psum", bufs=8))
+        ctx.enter_context(tc.manual_schedule())
 
-        grid_bf = const.tile([P, CHUNKS, KNOTS], BF16, name="grid_bf")
-        nc.sync.dma_start(out=grid_bf[:], in_=grid.rearrange("o (c p) t -> p (o c) t", p=P))
-        gamma_bf = const.tile([P, CHUNKS], BF16, name="gamma_bf")
-        beta_bf = const.tile([P, CHUNKS], BF16, name="beta_bf")
-        with nc.allow_non_contiguous_dma(reason="512 two-byte elements, one to a partition and chunk"):
-            nc.sync.dma_start(out=gamma_bf[:], in_=ln_gamma.rearrange("(c p) -> p c", p=P))
-            nc.sync.dma_start(out=beta_bf[:], in_=ln_beta.rearrange("(c p) -> p c", p=P))
         x_bf = []
         for h in range(HALVES):
             x_half = keep.tile([P, ROW_TILES, FEATURES], BF16, name="x_half%d" % h)
@@ -52,16 +48,22 @@ def tile_kanlinear_pa_kernel(tc, x, ln_gamma, ln_beta, base_weight, base_bias, s
                 out=x_half[:], in_=x[h * HALF : (h + 1) * HALF, :].rearrange("(t p) f -> p t f", p=P)
             )
             x_bf.append(x_half)
-        base_raw = keep.tile([P, PACK, UNITS], BF16, name="base_raw")
-        nc.sync.dma_start(out=base_raw[:], in_=base_weight.rearrange("(c p) u -> p c u", p=P))
-        bias_bc = const.tile([P, UNITS], BF16, name="bias_bc")
-        nc.sync.dma_start(out=bias_bc[:], in_=base_bias.partition_broadcast(P))
-        spline_raw = keep.tile([P, PLANES, UNITS], BF16, name="spline_raw")
+        grid_bf = const.tile([P, CHUNKS, KNOTS], BF16, name="grid_bf")
+        nc.scalar.dma_start(out=grid_bf[:], in_=grid.rearrange("o (c p) t -> p (o c) t", p=P))
+        gamma_bf = const.tile([P, CHUNKS], BF16, name="gamma_bf")
+        beta_bf = const.tile([P, CHUNKS], BF16, name="beta_bf")
+        with nc.allow_non_contiguous_dma(reason="512 two-byte elements, one to a partition and chunk"):
+            nc.scalar.dma_start(out=gamma_bf[:], in_=ln_gamma.rearrange("(c p) -> p c", p=P))
+            nc.scalar.dma_start(out=beta_bf[:], in_=ln_beta.rearrange("(c p) -> p c", p=P))
+        raw = keep.tile([P, PLANES + PACK, UNITS], BF16, name="raw")
+        nc.sync.dma_start(out=raw[:, PLANES:, :], in_=base_weight.rearrange("(c p) u -> p c u", p=P))
         for c in range(CHUNKS):
             nc.sync.dma_start(
-                out=spline_raw[:, c * BASES : (c + 1) * BASES, :].rearrange("p j u -> p (j u)"),
+                out=raw[:, c * BASES : (c + 1) * BASES, :].rearrange("p j u -> p (j u)"),
                 in_=spline_weight[c * P * BASES : (c + 1) * P * BASES, :].rearrange("(p j) u -> p (j u)", j=BASES),
             )
+        bias_bc = const.tile([P, UNITS], BF16, name="bias_bc")
+        nc.sync.dma_start(out=bias_bc[:], in_=base_bias.partition_broadcast(P))
 
         ident = const.tile([P, P], F32, name="ident")
         make_identity(nc, ident[:])
@@ -72,179 +74,295 @@ def tile_kanlinear_pa_kernel(tc, x, ln_gamma, ln_beta, base_weight, base_bias, s
 
         gamma = const.tile([P, CHUNKS], F32, name="gamma")
         beta = const.tile([P, CHUNKS], F32, name="beta")
-        nc.vector.tensor_copy(out=gamma[:], in_=gamma_bf[:])
-        nc.vector.tensor_copy(out=beta[:], in_=beta_bf[:])
-
         g = const.tile([P, CHUNKS, KNOTS], F32, name="g")
         neg_g = const.tile([P, CHUNKS, KNOTS], F32, name="neg_g")
-        nc.vector.tensor_copy(out=g[:], in_=grid_bf[:])
-        nc.vector.tensor_scalar_mul(out=neg_g[:], in0=g[:], scalar1=-1.0)
         den = const.tile([P, CHUNKS, 23], F32, name="den")
-        d1 = den[:, :, 14:23]
-        d2 = const.tile([P, CHUNKS, KNOTS - 2], F32, name="d2")
-        d3 = const.tile([P, CHUNKS, KNOTS - 3], F32, name="d3")
-        d4 = const.tile([P, CHUNKS, KNOTS - 4], F32, name="d4")
-        neg_d4 = const.tile([P, CHUNKS, KNOTS - 4], F32, name="neg_d4")
-        nc.vector.tensor_sub(out=d1, in0=g[:, :, 1:10], in1=g[:, :, 0:9])
-        nc.vector.tensor_sub(out=d2[:], in0=g[:, :, 2:10], in1=g[:, :, 0:8])
-        nc.vector.tensor_sub(out=d3[:], in0=g[:, :, 3:10], in1=g[:, :, 0:7])
-        nc.vector.tensor_sub(out=d4[:], in0=g[:, :, 4:10], in1=g[:, :, 0:6])
-        nc.vector.tensor_sub(out=neg_d4[:], in0=g[:, :, 0:6], in1=g[:, :, 4:10])
-        prod_a = const.tile([P, CHUNKS, 7], F32, name="prod_a")
-        prod_b = const.tile([P, CHUNKS, 7], F32, name="prod_b")
-        nc.vector.tensor_mul(out=prod_a[:], in0=den[:, :, 14:21], in1=d2[:, :, 0:7])
-        nc.vector.tensor_mul(out=prod_b[:], in0=den[:, :, 16:23], in1=d2[:, :, 1:8])
-        nc.vector.tensor_mul(out=den[:, :, 0:7], in0=prod_a[:], in1=d3[:])
-        nc.vector.tensor_mul(out=den[:, :, 7:14], in0=prod_b[:], in1=d3[:])
         inv = const.tile([P, CHUNKS, 23], F32, name="inv")
-        nc.vector.reciprocal(out=inv[:], in_=den[:])
         a0 = inv[:, :, 0:6]
         a1 = const.tile([P, CHUNKS, BASES], F32, name="a1")
         neg_c3 = const.tile([P, CHUNKS, BASES], F32, name="neg_c3")
         neg_c4 = const.tile([P, CHUNKS, BASES], F32, name="neg_c4")
-        nc.vector.tensor_mul(out=a1[:], in0=d4[:], in1=inv[:, :, 14:20])
-        nc.vector.tensor_mul(out=a1[:], in0=a1[:], in1=inv[:, :, 1:7])
-        nc.vector.tensor_mul(out=neg_c3[:], in0=neg_d4[:], in1=inv[:, :, 17:23])
-        nc.vector.tensor_mul(out=neg_c3[:], in0=neg_c3[:], in1=inv[:, :, 7:13])
-        nc.vector.tensor_scalar_mul(out=neg_c4[:], in0=inv[:, :, 8:14], scalar1=-1.0)
 
-        def layer_norm(h):
+        def knot_casts():
+            nc.vector.tensor_copy(out=g[:], in_=grid_bf[:])
+            nc.vector.tensor_scalar_mul(out=neg_g[:], in0=g[:], scalar1=-1.0)
+            nc.vector.tensor_copy(out=gamma[:], in_=gamma_bf[:])
+            nc.vector.tensor_copy(out=beta[:], in_=beta_bf[:])
+
+        def knot_coefficients():
+            d2 = const.tile([P, CHUNKS, KNOTS - 2], F32, name="d2")
+            d3 = const.tile([P, CHUNKS, KNOTS - 3], F32, name="d3")
+            d4 = const.tile([P, CHUNKS, KNOTS - 4], F32, name="d4")
+            neg_d4 = const.tile([P, CHUNKS, KNOTS - 4], F32, name="neg_d4")
+            nc.vector.tensor_sub(out=den[:, :, 14:23], in0=g[:, :, 1:10], in1=g[:, :, 0:9])
+            nc.vector.tensor_sub(out=d2[:], in0=g[:, :, 2:10], in1=g[:, :, 0:8])
+            nc.vector.tensor_sub(out=d3[:], in0=g[:, :, 3:10], in1=g[:, :, 0:7])
+            nc.vector.tensor_sub(out=d4[:], in0=g[:, :, 4:10], in1=g[:, :, 0:6])
+            nc.vector.tensor_sub(out=neg_d4[:], in0=g[:, :, 0:6], in1=g[:, :, 4:10])
+            prod_a = const.tile([P, CHUNKS, 7], F32, name="prod_a")
+            prod_b = const.tile([P, CHUNKS, 7], F32, name="prod_b")
+            nc.vector.tensor_mul(out=prod_a[:], in0=den[:, :, 14:21], in1=d2[:, :, 0:7])
+            nc.vector.tensor_mul(out=prod_b[:], in0=den[:, :, 16:23], in1=d2[:, :, 1:8])
+            nc.vector.tensor_mul(out=den[:, :, 0:7], in0=prod_a[:], in1=d3[:])
+            nc.vector.tensor_mul(out=den[:, :, 7:14], in0=prod_b[:], in1=d3[:])
+            nc.vector.reciprocal(out=inv[:], in_=den[:])
+            nc.vector.tensor_mul(out=a1[:], in0=d4[:], in1=inv[:, :, 14:20])
+            nc.vector.tensor_mul(out=neg_c3[:], in0=neg_d4[:], in1=inv[:, :, 17:23])
+            nc.vector.tensor_scalar_mul(out=neg_c4[:], in0=inv[:, :, 8:14], scalar1=-1.0)
+            nc.vector.tensor_mul(out=a1[:], in0=a1[:], in1=inv[:, :, 1:7])
+            nc.vector.tensor_mul(out=neg_c3[:], in0=neg_c3[:], in1=inv[:, :, 7:13])
+
+        xn = keep.tile([P, HALVES, CHUNKS, HALF], F32, name="xn")
+        neg_mean = keep.tile([P, HALVES, ROW_TILES], F32, name="neg_mean")
+        var_eps = keep.tile([P, HALVES, ROW_TILES], F32, name="var_eps")
+        std = keep.tile([P, HALVES, ROW_TILES], F32, name="std")
+        rstd = keep.tile([P, HALVES, ROW_TILES], F32, name="rstd")
+        shift = keep.tile([P, HALVES, ROW_TILES], F32, name="shift")
+        z_tiles = {}
+
+        def moments_on_vector(h):
             stats = work.tile([P, ROW_TILES, 6], F32, name="stats")
             mean_var = work.tile([P, ROW_TILES, 2], F32, name="mean_var")
             for t in range(ROW_TILES):
                 nc.vector.bn_stats(out=stats[:, t, :], in_=x_bf[h][:, t, :])
+            for t in range(ROW_TILES):
                 nc.vector.bn_aggr(out=mean_var[:, t, :], in_=stats[:, t, :])
-            var_eps = work.tile([P, ROW_TILES], F32, name="var_eps")
-            nc.vector.tensor_scalar_add(out=var_eps[:], in0=mean_var[:, :, 1], scalar1=LN_EPS)
-            std = work.tile([P, ROW_TILES], F32, name="std")
-            nc.scalar.activation(out=std[:], in_=var_eps[:], func=ACT.Sqrt)
+            nc.vector.tensor_scalar_add(out=var_eps[:, h, :], in0=mean_var[:, :, 1], scalar1=LN_EPS)
+            nc.vector.tensor_scalar_mul(out=neg_mean[:, h, :], in0=mean_var[:, :, 0], scalar1=-1.0)
+
+        sums = keep.tile([P, 2, ROW_TILES], F32, name="sums")
+
+        def sums_on_scalar(h):
+            for t in range(ROW_TILES):
+                unread = work.tile([P, FEATURES], BF16, name="unread", bufs=ROW_TILES)
+                nc.scalar.activation(
+                    out=unread[:], in_=x_bf[h][:, t, :], func=ACT.Identity, accum_out=sums[:, 0, t : t + 1]
+                )
+
+        def mean_of_sums(h):
+            nc.vector.tensor_scalar_mul(out=neg_mean[:, h, :], in0=sums[:, 0, :], scalar1=-1.0 / FEATURES)
+
+        def deviations_on_scalar(h):
+            for t in range(ROW_TILES):
+                unread = work.tile([P, FEATURES], BF16, name="unread", bufs=ROW_TILES)
+                nc.scalar.activation(
+                    out=unread[:],
+                    in_=x_bf[h][:, t, :],
+                    func=ACT.Square,
+                    bias=neg_mean[:, h, t : t + 1],
+                    accum_out=sums[:, 1, t : t + 1],
+                )
+
+        def variance_of_sums(h):
+            nc.vector.tensor_scalar(
+                out=var_eps[:, h, :], in0=sums[:, 1, :], scalar1=1.0 / FEATURES, scalar2=LN_EPS, op0=ALU.mult, op1=ALU.add
+            )
+
+        def root(h):
+            nc.scalar.activation(out=std[:, h, :], in_=var_eps[:, h, :], func=ACT.Sqrt)
+
+        def reciprocal_root(h):
             guess = work.tile([P, ROW_TILES], F32, name="guess")
-            nc.vector.reciprocal(out=guess[:], in_=std[:])
+            nc.vector.reciprocal(out=guess[:], in_=std[:, h, :])
             corr = work.tile([P, ROW_TILES], F32, name="corr")
             nc.vector.tensor_mul(out=corr[:], in0=guess[:], in1=guess[:])
-            nc.vector.tensor_mul(out=corr[:], in0=corr[:], in1=var_eps[:])
+            nc.vector.tensor_mul(out=corr[:], in0=corr[:], in1=var_eps[:, h, :])
             nc.vector.tensor_scalar(out=corr[:], in0=corr[:], scalar1=-0.5, scalar2=1.5, op0=ALU.mult, op1=ALU.add)
-            rstd = work.tile([P, ROW_TILES], F32, name="rstd")
-            nc.vector.tensor_mul(out=rstd[:], in0=guess[:], in1=corr[:])
-            z_tiles = []
+            nc.vector.tensor_mul(out=rstd[:, h, :], in0=guess[:], in1=corr[:])
+            nc.vector.tensor_mul(out=shift[:, h, :], in0=neg_mean[:, h, :], in1=rstd[:, h, :])
+
+        def normalise(h, engine):
             for t in range(ROW_TILES):
                 z = work.tile([P, FEATURES], F32, name="z", bufs=2 * ROW_TILES)
-                nc.vector.tensor_scalar(
-                    out=z[:],
-                    in0=x_bf[h][:, t, :],
-                    scalar1=mean_var[:, t, 0:1],
-                    scalar2=rstd[:, t : t + 1],
-                    op0=ALU.subtract,
-                    op1=ALU.mult,
-                )
-                z_tiles.append(z)
-            xn = keep.tile([P, CHUNKS, HALF], F32, name="xn%d" % h)
-            for c in range(CHUNKS):
-                z_t = psum_t.tile([P, HALF], F32, name="z_t")
-                for t in range(ROW_TILES):
-                    nc.tensor.transpose(z_t[:, t * P : (t + 1) * P], z_tiles[t][:, c * P : (c + 1) * P], ident[:])
-                nc.scalar.activation(
-                    out=xn[:, c, :], in_=z_t[:], func=ACT.Identity, scale=gamma[:, c : c + 1], bias=beta[:, c : c + 1]
-                )
-            return xn
+                if engine == "vector":
+                    nc.vector.tensor_scalar(
+                        out=z[:],
+                        in0=x_bf[h][:, t, :],
+                        scalar1=rstd[:, h, t : t + 1],
+                        scalar2=shift[:, h, t : t + 1],
+                        op0=ALU.mult,
+                        op1=ALU.add,
+                    )
+                else:
+                    nc.scalar.activation(
+                        out=z[:],
+                        in_=x_bf[h][:, t, :],
+                        func=ACT.Identity,
+                        scale=rstd[:, h, t : t + 1],
+                        bias=shift[:, h, t : t + 1],
+                    )
+                z_tiles[(h, t)] = z
+
+        def turn(h, c):
+            z_t = psum.tile([P, HALF], F32, name="z_t", tag="bank")
+            for t in range(ROW_TILES):
+                nc.tensor.transpose(z_t[:, t * P : (t + 1) * P], z_tiles[(h, t)][:, c * P : (c + 1) * P], ident[:])
+            nc.scalar.activation(
+                out=xn[:, h, c, :], in_=z_t[:], func=ACT.Identity, scale=gamma[:, c : c + 1], bias=beta[:, c : c + 1]
+            )
+
+        def regroup(planes, relu):
+            grouped = work.tile([P, HALF, PACK], BF16, name="grouped", align_bytes=64, bufs=4)
+            dst = grouped[:].rearrange("p (c i) t -> p c t i", i=RUN)
+            src = planes.rearrange("p t (c i) -> p c t i", i=RUN)
+            cut = VECTOR_COLS // RUN
+            if relu:
+                nc.vector.tensor_scalar_max(out=dst[:, :cut], in0=src[:, :cut], scalar1=0.0)
+                nc.scalar.activation(out=dst[:, cut:], in_=src[:, cut:], func=ACT.Relu)
+            else:
+                nc.vector.tensor_copy(out=dst[:, :cut], in_=src[:, :cut])
+                nc.scalar.copy(out=dst[:, cut:], in_=src[:, cut:])
+            return grouped
 
         w_codes = keep.tile([P, SPLINE_PASSES + 1, UNITS], U32, name="w_codes", align_bytes=64)
         w_scales = keep.tile([P, SPLINE_PASSES + 1, UNITS], U8, name="w_scales", align_bytes=64)
-        BASE_PASS = SPLINE_PASSES
 
-        def quantise_weight(s, four_rows):
-            grouped_w = work.tile([P, UNITS, PACK], BF16, name="grouped_w", align_bytes=64)
-            nc.scalar.copy(out=grouped_w[:], in_=four_rows.rearrange("p t u -> p u t"))
+        def quantise_weight(s, grouped):
             nc.vector.quantize_mx(
                 out=w_codes[:, s, :].bitcast(FP8X4),
                 scales=w_scales[:, s, :],
-                in_=grouped_w[:].rearrange("p u t -> p (u t)"),
+                in_=grouped[:].rearrange("p u t -> p (u t)"),
             )
 
-        def multiply(s, acc, grouped, start, stop):
+        acc = {}
+
+        def multiply(s, h, grouped):
             codes = work.tile([P, HALF], U32, name="codes", align_bytes=64, bufs=3)
             scales = work.tile([P, HALF], U8, name="scales", align_bytes=64, bufs=3)
             nc.vector.quantize_mx(
                 out=codes[:].bitcast(FP8X4), scales=scales[:], in_=grouped[:].rearrange("p n t -> p (n t)")
             )
             for m in range(ROW_TILES):
+                if s == 0:
+                    acc[(h, m)] = psum.tile([P, UNITS], F32, name="acc", tag="bank")
                 nc.tensor.matmul_mx(
-                    out=acc[m][:],
+                    out=acc[(h, m)][:],
                     lhsT=codes[:, m * P : (m + 1) * P].bitcast(FP8X4),
                     lhsT_scale=scales[:, m * P : (m + 1) * P],
                     rhs=w_codes[:, s, :].bitcast(FP8X4),
                     rhs_scale=w_scales[:, s, :],
-                    start=start,
-                    stop=stop,
+                    start=(s == 0),
+                    stop=(s == SPLINE_PASSES - 1),
                 )
+            if s == SPLINE_PASSES - 1:
+                for m in range(ROW_TILES):
+                    result = work.tile([P, UNITS], F32, name="result", bufs=4)
+                    nc.vector.tensor_add(out=result[:], in0=acc[(h, m)][:], in1=bias_bc[:])
+                    row0 = h * HALF + m * P
+                    nc.sync.dma_start(out=out[row0 : row0 + P, :], in_=result[:])
 
-        xn_halves = [layer_norm(h) for h in range(HALVES)]
-        quantise_weight(BASE_PASS, base_raw[:])
+        def emit_squares(h, c):
+            squares = []
+            for i in range(KNOTS):
+                square = work.tile([P, HALF], F32, name="square", bufs=KNOTS)
+                nc.scalar.activation(out=square[:], in_=xn[:, h, c, :], func=ACT.Square, bias=neg_g[:, c, i : i + 1])
+                squares.append(square)
+            return squares
 
-        for h in range(HALVES):
-            xn = xn_halves[h]
-            acc = [psum_acc.tile([P, UNITS], F32, name="acc") for m in range(ROW_TILES)]
-            grouped = work.tile([P, HALF, PACK], BF16, name="grouped", align_bytes=64)
-            nc.vector.tensor_scalar_max(out=grouped[:], in0=xn[:].rearrange("p c n -> p n c"), scalar1=0.0)
-            multiply(BASE_PASS, acc, grouped, True, False)
+        def emit_cubes(h, c, squares):
+            cubes = []
+            for i in range(KNOTS):
+                cube = work.tile([P, HALF], F32, name="cube", bufs=KNOTS + 2)
+                nc.vector.scalar_tensor_tensor(
+                    out=cube[:],
+                    in0=xn[:, h, c, :],
+                    scalar=g[:, c, i : i + 1],
+                    in1=squares[i][:],
+                    op0=ALU.subtract,
+                    op1=ALU.mult,
+                )
+                cubes.append(cube)
+            return cubes
 
-            left4 = None
-            right4 = None
-            for c in range(CHUNKS):
-                v = xn[:, c, :]
-                cubes = []
-                for i in range(KNOTS):
-                    square = work.tile([P, HALF], F32, name="square", bufs=4)
-                    nc.scalar.activation(out=square[:], in_=v, func=ACT.Square, bias=neg_g[:, c, i : i + 1])
-                    cube = work.tile([P, HALF], F32, name="cube", bufs=8)
-                    nc.vector.scalar_tensor_tensor(
-                        out=cube[:], in0=v, scalar=g[:, c, i : i + 1], in1=square[:], op0=ALU.subtract, op1=ALU.mult
-                    )
-                    cubes.append(cube)
-                    j = i - 4
-                    if j < 0:
-                        continue
-                    q = c * BASES + j
-                    s = q // PACK
-                    slot = q % PACK
-                    if slot == 0:
-                        left4 = work.tile([P, PACK, HALF], BF16, name="left4", bufs=3)
-                        right4 = work.tile([P, PACK, HALF], BF16, name="right4", bufs=3)
-                        if h == 0:
-                            quantise_weight(s, spline_raw[:, s * PACK : (s + 1) * PACK, :])
-                    inner_l = work.tile([P, HALF], F32, name="inner_l", bufs=3)
-                    nc.scalar.activation(out=inner_l[:], in_=cubes[j + 1][:], func=ACT.Relu, scale=a1[:, c, j : j + 1])
-                    nc.vector.scalar_tensor_tensor(
-                        out=left4[:, slot, :],
-                        in0=cubes[j][:],
-                        scalar=a0[:, c, j : j + 1],
-                        in1=inner_l[:],
-                        op0=ALU.mult,
-                        op1=ALU.subtract,
-                    )
-                    inner_r = work.tile([P, HALF], F32, name="inner_r", bufs=3)
-                    nc.scalar.activation(
-                        out=inner_r[:], in_=cubes[j + 3][:], func=ACT.Relu, scale=neg_c3[:, c, j : j + 1]
-                    )
-                    nc.vector.scalar_tensor_tensor(
-                        out=right4[:, slot, :],
-                        in0=cubes[j + 4][:],
-                        scalar=neg_c4[:, c, j : j + 1],
-                        in1=inner_r[:],
-                        op0=ALU.mult,
-                        op1=ALU.subtract,
-                    )
-                    if slot == PACK - 1:
-                        larger = work.tile([P, PACK, HALF], BF16, name="larger")
-                        nc.vector.tensor_max(out=larger[:], in0=left4[:], in1=right4[:])
-                        grouped = work.tile([P, HALF, PACK], BF16, name="grouped", align_bytes=64)
-                        nc.vector.tensor_scalar_max(
-                            out=grouped[:], in0=larger[:].rearrange("p t n -> p n t"), scalar1=0.0
-                        )
-                        multiply(s, acc, grouped, False, s == SPLINE_PASSES - 1)
+        def emit_inners(c, cubes):
+            inners = []
+            for j in range(BASES):
+                inner_l = work.tile([P, HALF], F32, name="inner_l", bufs=BASES)
+                nc.scalar.activation(out=inner_l[:], in_=cubes[j + 1][:], func=ACT.Relu, scale=a1[:, c, j : j + 1])
+                inner_r = work.tile([P, HALF], F32, name="inner_r", bufs=BASES)
+                nc.scalar.activation(out=inner_r[:], in_=cubes[j + 3][:], func=ACT.Relu, scale=neg_c3[:, c, j : j + 1])
+                inners.append((inner_l, inner_r))
+            return inners
 
-            for m in range(ROW_TILES):
-                result = work.tile([P, UNITS], F32, name="result", bufs=4)
-                nc.vector.tensor_add(out=result[:], in0=acc[m][:], in1=bias_bc[:])
-                row0 = h * HALF + m * P
-                nc.sync.dma_start(out=out[row0 : row0 + P, :], in_=result[:])
+        sides = {}
+
+        def emit_sides(h, c, cubes, inners):
+            complete = []
+            for j in range(BASES):
+                q = c * BASES + j
+                s = q // PACK
+                if q % PACK == 0:
+                    left4 = work.tile([P, PACK, HALF], BF16, name="left4", bufs=3)
+                    right4 = work.tile([P, PACK, HALF], BF16, name="right4", bufs=3)
+                    sides[s] = (left4, right4)
+                left4, right4 = sides[s]
+                nc.vector.scalar_tensor_tensor(
+                    out=left4[:, q % PACK, :],
+                    in0=cubes[j][:],
+                    scalar=a0[:, c, j : j + 1],
+                    in1=inners[j][0][:],
+                    op0=ALU.mult,
+                    op1=ALU.subtract,
+                )
+                nc.vector.scalar_tensor_tensor(
+                    out=right4[:, q % PACK, :],
+                    in0=cubes[j + 4][:],
+                    scalar=neg_c4[:, c, j : j + 1],
+                    in1=inners[j][1][:],
+                    op0=ALU.mult,
+                    op1=ALU.subtract,
+                )
+                if q % PACK == PACK - 1:
+                    complete.append(s)
+            for s in complete:
+                nc.vector.tensor_max(out=sides[s][0][:], in0=sides[s][0][:], in1=sides[s][1][:])
+            return complete
+
+        moments_on_vector(0)
+        root(0)
+        knot_casts()
+        reciprocal_root(0)
+        normalise(0, "vector")
+        turn(0, 0)
+        squares = emit_squares(0, 0)
+        knot_coefficients()
+        waiting = []
+        blocks = [(h, c) for h in range(HALVES) for c in range(CHUNKS)]
+        for b in range(len(blocks)):
+            h, c = blocks[b]
+            cubes = emit_cubes(h, c, squares)
+            inners = emit_inners(c, cubes)
+            if b == 1:
+                mean_of_sums(1)
+            if b == 2:
+                variance_of_sums(1)
+            if b == 3:
+                reciprocal_root(1)
+                normalise(1, "scalar")
+            if b + 1 < len(blocks):
+                turn(blocks[b + 1][0], blocks[b + 1][1])
+                squares = emit_squares(blocks[b + 1][0], blocks[b + 1][1])
+            if b == 0:
+                sums_on_scalar(1)
+            if b == 1:
+                deviations_on_scalar(1)
+            if b == 2:
+                root(1)
+            for s, half, grouped in waiting:
+                if half is None:
+                    quantise_weight(s, grouped)
+                else:
+                    multiply(s, half, grouped)
+            waiting = []
+            complete = emit_sides(h, c, cubes, inners)
+            if c == CHUNKS - 2:
+                complete.append(BASE_PASS)
+            for s in complete:
+                if h == 0:
+                    waiting.append((s, None, regroup(raw[:, s * PACK : (s + 1) * PACK, :], False)))
+                if s == BASE_PASS:
+                    waiting.append((s, h, regroup(xn[:, h], True)))
+                else:
+                    waiting.append((s, h, regroup(sides[s][0][:], True)))
+        for s, half, grouped in waiting:
+            multiply(s, half, grouped)

@@ -27,7 +27,8 @@ SPLINE_PASSES = PLANES // PACK
 BASE_PASS = SPLINE_PASSES
 LN_EPS = 0.001
 RUN = 4
-VECTOR_COLS = 256
+WEIGHT_VECTOR_COLS = 384
+VALUE_VECTOR_COLS = 64
 
 FLOPS = 2 * ROWS * (FEATURES + FEATURES * BASES) * UNITS
 
@@ -44,9 +45,9 @@ def tile_kanlinear_pa_kernel(tc, x, ln_gamma, ln_beta, base_weight, base_bias, s
         x_bf = []
         for h in range(HALVES):
             x_half = keep.tile([P, ROW_TILES, FEATURES], BF16, name="x_half%d" % h)
-            nc.sync.dma_start(
-                out=x_half[:], in_=x[h * HALF : (h + 1) * HALF, :].rearrange("(t p) f -> p t f", p=P)
-            )
+            rows = x[h * HALF : (h + 1) * HALF, :].rearrange("(t p) f -> p t f", p=P)
+            for t in range(0, ROW_TILES, 2):
+                nc.sync.dma_start(out=x_half[:, t : t + 2, :], in_=rows[:, t : t + 2, :])
             x_bf.append(x_half)
         grid_bf = const.tile([P, CHUNKS, KNOTS], BF16, name="grid_bf")
         nc.scalar.dma_start(out=grid_bf[:], in_=grid.rearrange("o (c p) t -> p (o c) t", p=P))
@@ -166,9 +167,12 @@ def tile_kanlinear_pa_kernel(tc, x, ln_gamma, ln_beta, base_weight, base_bias, s
             nc.vector.reciprocal(out=guess[:], in_=std[:, h, :])
             corr = work.tile([P, ROW_TILES], F32, name="corr")
             nc.vector.tensor_mul(out=corr[:], in0=guess[:], in1=guess[:])
-            nc.vector.tensor_mul(out=corr[:], in0=corr[:], in1=var_eps[:, h, :])
-            nc.vector.tensor_scalar(out=corr[:], in0=corr[:], scalar1=-0.5, scalar2=1.5, op0=ALU.mult, op1=ALU.add)
-            nc.vector.tensor_mul(out=rstd[:, h, :], in0=guess[:], in1=corr[:])
+            nc.vector.scalar_tensor_tensor(
+                out=corr[:], in0=corr[:], scalar=-0.5, in1=var_eps[:, h, :], op0=ALU.mult, op1=ALU.mult
+            )
+            nc.vector.scalar_tensor_tensor(
+                out=rstd[:, h, :], in0=corr[:], scalar=1.5, in1=guess[:], op0=ALU.add, op1=ALU.mult
+            )
             nc.vector.tensor_mul(out=shift[:, h, :], in0=neg_mean[:, h, :], in1=rstd[:, h, :])
 
         def normalise(h, engine):
@@ -178,10 +182,10 @@ def tile_kanlinear_pa_kernel(tc, x, ln_gamma, ln_beta, base_weight, base_bias, s
                     nc.vector.tensor_scalar(
                         out=z[:],
                         in0=x_bf[h][:, t, :],
-                        scalar1=rstd[:, h, t : t + 1],
-                        scalar2=shift[:, h, t : t + 1],
-                        op0=ALU.mult,
-                        op1=ALU.add,
+                        scalar1=neg_mean[:, h, t : t + 1],
+                        scalar2=rstd[:, h, t : t + 1],
+                        op0=ALU.add,
+                        op1=ALU.mult,
                     )
                 else:
                     nc.scalar.activation(
@@ -205,11 +209,12 @@ def tile_kanlinear_pa_kernel(tc, x, ln_gamma, ln_beta, base_weight, base_bias, s
             grouped = work.tile([P, HALF, PACK], BF16, name="grouped", align_bytes=64, bufs=4)
             dst = grouped[:].rearrange("p (c i) t -> p c t i", i=RUN)
             src = planes.rearrange("p t (c i) -> p c t i", i=RUN)
-            cut = VECTOR_COLS // RUN
             if relu:
+                cut = VALUE_VECTOR_COLS // RUN
                 nc.vector.tensor_scalar_max(out=dst[:, :cut], in0=src[:, :cut], scalar1=0.0)
                 nc.scalar.activation(out=dst[:, cut:], in_=src[:, cut:], func=ACT.Relu)
             else:
+                cut = WEIGHT_VECTOR_COLS // RUN
                 nc.vector.tensor_copy(out=dst[:, :cut], in_=src[:, :cut])
                 nc.scalar.copy(out=dst[:, cut:], in_=src[:, cut:])
             return grouped
@@ -251,6 +256,37 @@ def tile_kanlinear_pa_kernel(tc, x, ln_gamma, ln_beta, base_weight, base_bias, s
                     row0 = h * HALF + m * P
                     nc.sync.dma_start(out=out[row0 : row0 + P, :], in_=result[:])
 
+        waiting = []
+
+        sides = {}
+        half_now = [0]
+
+        def regroup_pass(s, h):
+            if h == 0:
+                waiting.append((s, None, regroup(raw[:, s * PACK : (s + 1) * PACK, :], False)))
+            if s == BASE_PASS:
+                waiting.append((s, h, regroup(xn[:, h], True)))
+            else:
+                waiting.append((s, h, regroup(sides[s][0][:], True)))
+
+        def multiply_waiting():
+            for s, half, grouped in waiting:
+                if half is None:
+                    quantise_weight(s, grouped)
+                else:
+                    multiply(s, half, grouped)
+            waiting[:] = []
+
+        stage = {"complete": [], "larger": []}
+
+        def finish_step():
+            for s in stage["larger"]:
+                regroup_pass(s, half_now[0])
+            stage["larger"] = stage["complete"]
+            stage["complete"] = []
+            for s in stage["larger"]:
+                nc.vector.tensor_max(out=sides[s][0][:], in0=sides[s][0][:], in1=sides[s][1][:])
+
         def emit_squares(h, c):
             squares = []
             for i in range(KNOTS):
@@ -272,6 +308,8 @@ def tile_kanlinear_pa_kernel(tc, x, ln_gamma, ln_beta, base_weight, base_bias, s
                     op1=ALU.mult,
                 )
                 cubes.append(cube)
+                if i % 2 == 1:
+                    finish_step()
             return cubes
 
         def emit_inners(c, cubes):
@@ -284,85 +322,72 @@ def tile_kanlinear_pa_kernel(tc, x, ln_gamma, ln_beta, base_weight, base_bias, s
                 inners.append((inner_l, inner_r))
             return inners
 
-        sides = {}
-
-        def emit_sides(h, c, cubes, inners):
-            complete = []
-            for j in range(BASES):
-                q = c * BASES + j
-                s = q // PACK
-                if q % PACK == 0:
-                    left4 = work.tile([P, PACK, HALF], BF16, name="left4", bufs=3)
-                    right4 = work.tile([P, PACK, HALF], BF16, name="right4", bufs=3)
-                    sides[s] = (left4, right4)
-                left4, right4 = sides[s]
-                nc.vector.scalar_tensor_tensor(
-                    out=left4[:, q % PACK, :],
-                    in0=cubes[j][:],
-                    scalar=a0[:, c, j : j + 1],
-                    in1=inners[j][0][:],
-                    op0=ALU.mult,
-                    op1=ALU.subtract,
-                )
-                nc.vector.scalar_tensor_tensor(
-                    out=right4[:, q % PACK, :],
-                    in0=cubes[j + 4][:],
-                    scalar=neg_c4[:, c, j : j + 1],
-                    in1=inners[j][1][:],
-                    op0=ALU.mult,
-                    op1=ALU.subtract,
-                )
-                if q % PACK == PACK - 1:
-                    complete.append(s)
-            for s in complete:
-                nc.vector.tensor_max(out=sides[s][0][:], in0=sides[s][0][:], in1=sides[s][1][:])
-            return complete
+        def emit_sides(c, j, cubes, inners):
+            q = c * BASES + j
+            s = q // PACK
+            if q % PACK == 0:
+                left4 = work.tile([P, PACK, HALF], BF16, name="left4", bufs=3)
+                right4 = work.tile([P, PACK, HALF], BF16, name="right4", bufs=3)
+                sides[s] = (left4, right4)
+            left4, right4 = sides[s]
+            nc.vector.scalar_tensor_tensor(
+                out=left4[:, q % PACK, :],
+                in0=cubes[j][:],
+                scalar=a0[:, c, j : j + 1],
+                in1=inners[j][0][:],
+                op0=ALU.mult,
+                op1=ALU.subtract,
+            )
+            nc.vector.scalar_tensor_tensor(
+                out=right4[:, q % PACK, :],
+                in0=cubes[j + 4][:],
+                scalar=neg_c4[:, c, j : j + 1],
+                in1=inners[j][1][:],
+                op0=ALU.mult,
+                op1=ALU.subtract,
+            )
+            if q % PACK == PACK - 1:
+                stage["complete"].append(s)
 
         moments_on_vector(0)
         root(0)
+        sums_on_scalar(1)
         knot_casts()
         reciprocal_root(0)
         normalise(0, "vector")
         turn(0, 0)
-        squares = emit_squares(0, 0)
         knot_coefficients()
-        waiting = []
+        mean_of_sums(1)
+        squares = emit_squares(0, 0)
         blocks = [(h, c) for h in range(HALVES) for c in range(CHUNKS)]
         for b in range(len(blocks)):
             h, c = blocks[b]
+            last_block = b == len(blocks) - 1
+            if not last_block:
+                turn(blocks[b + 1][0], blocks[b + 1][1])
             cubes = emit_cubes(h, c, squares)
+            half_now[0] = h
             inners = emit_inners(c, cubes)
             if b == 1:
-                mean_of_sums(1)
-            if b == 2:
                 variance_of_sums(1)
-            if b == 3:
+            if b == 2:
                 reciprocal_root(1)
-                normalise(1, "scalar")
-            if b + 1 < len(blocks):
-                turn(blocks[b + 1][0], blocks[b + 1][1])
+            if not last_block:
                 squares = emit_squares(blocks[b + 1][0], blocks[b + 1][1])
             if b == 0:
-                sums_on_scalar(1)
-            if b == 1:
                 deviations_on_scalar(1)
-            if b == 2:
+            if b == 1:
                 root(1)
-            for s, half, grouped in waiting:
-                if half is None:
-                    quantise_weight(s, grouped)
-                else:
-                    multiply(s, half, grouped)
-            waiting = []
-            complete = emit_sides(h, c, cubes, inners)
+            if b == 2:
+                normalise(1, "scalar")
+            multiply_waiting()
+            for j in range(BASES):
+                emit_sides(c, j, cubes, inners)
+                finish_step()
+                if last_block and j == BASES - 2:
+                    multiply_waiting()
             if c == CHUNKS - 2:
-                complete.append(BASE_PASS)
-            for s in complete:
-                if h == 0:
-                    waiting.append((s, None, regroup(raw[:, s * PACK : (s + 1) * PACK, :], False)))
-                if s == BASE_PASS:
-                    waiting.append((s, h, regroup(xn[:, h], True)))
-                else:
-                    waiting.append((s, h, regroup(sides[s][0][:], True)))
-        for s, half, grouped in waiting:
-            multiply(s, half, grouped)
+                regroup_pass(BASE_PASS, h)
+        finish_step()
+        finish_step()
+        multiply_waiting()

@@ -27,8 +27,11 @@ SPLINE_PASSES = PLANES // PACK
 BASE_PASS = SPLINE_PASSES
 LN_EPS = 0.001
 RUN = 4
-WEIGHT_VECTOR_COLS = 384
-VALUE_VECTOR_COLS = 64
+VALUE_SCALAR_COLS = 320
+TAIL_SCALAR_COLS = 192
+GPSIMD_LEFTS = (0, 1, 2, 3)
+COMPLETE = [[0], [1, 2], [3], [4, 5]]
+REGROUP_WEIGHTS = [[0, 1], [2, 6], [3, 4], [5], [], [], [], []]
 
 FLOPS = 2 * ROWS * (FEATURES + FEATURES * BASES) * UNITS
 
@@ -39,7 +42,7 @@ def tile_kanlinear_pa_kernel(tc, x, ln_gamma, ln_beta, base_weight, base_bias, s
         const = ctx.enter_context(tc.tile_pool(name="const", bufs=1))
         keep = ctx.enter_context(tc.tile_pool(name="keep", bufs=1))
         work = ctx.enter_context(tc.tile_pool(name="work", bufs=2))
-        psum = ctx.enter_context(tc.psum_pool(name="psum", bufs=8))
+        psum = ctx.enter_context(tc.psum_pool(name="psum", bufs=2))
         ctx.enter_context(tc.manual_schedule())
 
         x_bf = []
@@ -57,8 +60,9 @@ def tile_kanlinear_pa_kernel(tc, x, ln_gamma, ln_beta, base_weight, base_bias, s
             nc.scalar.dma_start(out=gamma_bf[:], in_=ln_gamma.rearrange("(c p) -> p c", p=P))
             nc.scalar.dma_start(out=beta_bf[:], in_=ln_beta.rearrange("(c p) -> p c", p=P))
         raw = keep.tile([P, PLANES + PACK, UNITS], BF16, name="raw")
-        nc.sync.dma_start(out=raw[:, PLANES:, :], in_=base_weight.rearrange("(c p) u -> p c u", p=P))
         for c in range(CHUNKS):
+            if c == 2:
+                nc.sync.dma_start(out=raw[:, PLANES:, :], in_=base_weight.rearrange("(c p) u -> p c u", p=P))
             nc.sync.dma_start(
                 out=raw[:, c * BASES : (c + 1) * BASES, :].rearrange("p j u -> p (j u)"),
                 in_=spline_weight[c * P * BASES : (c + 1) * P * BASES, :].rearrange("(p j) u -> p (j u)", j=BASES),
@@ -76,17 +80,18 @@ def tile_kanlinear_pa_kernel(tc, x, ln_gamma, ln_beta, base_weight, base_bias, s
         gamma = const.tile([P, CHUNKS], F32, name="gamma")
         beta = const.tile([P, CHUNKS], F32, name="beta")
         g = const.tile([P, CHUNKS, KNOTS], F32, name="g")
-        neg_g = const.tile([P, CHUNKS, KNOTS], F32, name="neg_g")
         den = const.tile([P, CHUNKS, 23], F32, name="den")
         inv = const.tile([P, CHUNKS, 23], F32, name="inv")
-        a0 = inv[:, :, 0:6]
-        a1 = const.tile([P, CHUNKS, BASES], F32, name="a1")
-        neg_c3 = const.tile([P, CHUNKS, BASES], F32, name="neg_c3")
-        neg_c4 = const.tile([P, CHUNKS, BASES], F32, name="neg_c4")
+        sq_scale = const.tile([P, CHUNKS, KNOTS], F32, name="sq_scale")
+        sq_bias = const.tile([P, CHUNKS, KNOTS], F32, name="sq_bias")
+        l_inner = const.tile([P, CHUNKS, BASES], F32, name="l_inner")
+        r_inner = const.tile([P, CHUNKS, BASES], F32, name="r_inner")
+        r_first = const.tile([P, CHUNKS, 3], F32, name="r_first")
+        factor = const.tile([P, CHUNKS, KNOTS], F32, name="factor")
+        root_guess = const.tile([P, CHUNKS, KNOTS], F32, name="root_guess")
 
         def knot_casts():
             nc.vector.tensor_copy(out=g[:], in_=grid_bf[:])
-            nc.vector.tensor_scalar_mul(out=neg_g[:], in0=g[:], scalar1=-1.0)
             nc.vector.tensor_copy(out=gamma[:], in_=gamma_bf[:])
             nc.vector.tensor_copy(out=beta[:], in_=beta_bf[:])
 
@@ -107,11 +112,27 @@ def tile_kanlinear_pa_kernel(tc, x, ln_gamma, ln_beta, base_weight, base_bias, s
             nc.vector.tensor_mul(out=den[:, :, 0:7], in0=prod_a[:], in1=d3[:])
             nc.vector.tensor_mul(out=den[:, :, 7:14], in0=prod_b[:], in1=d3[:])
             nc.vector.reciprocal(out=inv[:], in_=den[:])
-            nc.vector.tensor_mul(out=a1[:], in0=d4[:], in1=inv[:, :, 14:20])
-            nc.vector.tensor_mul(out=neg_c3[:], in0=neg_d4[:], in1=inv[:, :, 17:23])
-            nc.vector.tensor_scalar_mul(out=neg_c4[:], in0=inv[:, :, 8:14], scalar1=-1.0)
-            nc.vector.tensor_mul(out=a1[:], in0=a1[:], in1=inv[:, :, 1:7])
-            nc.vector.tensor_mul(out=neg_c3[:], in0=neg_c3[:], in1=inv[:, :, 7:13])
+            nc.vector.tensor_copy(out=factor[:, :, 0:7], in_=inv[:, :, 0:7])
+            nc.vector.tensor_copy(out=factor[:, :, 7:10], in_=inv[:, :, 11:14])
+            nc.scalar.activation(out=root_guess[:], in_=factor[:], func=ACT.Sqrt)
+            ratio = const.tile([P, CHUNKS, 4], F32, name="ratio")
+            nc.vector.tensor_mul(out=ratio[:], in0=inv[:, :, 7:11], in1=den[:, :, 3:7])
+            nc.vector.tensor_mul(out=l_inner[:], in0=d4[:], in1=inv[:, :, 14:20])
+            nc.vector.tensor_mul(out=r_inner[:], in0=neg_d4[:], in1=inv[:, :, 17:23])
+            nc.vector.tensor_scalar_mul(out=r_first[:], in0=ratio[:, :, 1:4], scalar1=-1.0)
+            nc.vector.tensor_mul(out=r_inner[:, :, 0:4], in0=r_inner[:, :, 0:4], in1=ratio[:])
+            quotient = const.tile([P, CHUNKS, KNOTS], F32, name="quotient")
+            inv_guess = const.tile([P, CHUNKS, KNOTS], F32, name="inv_guess")
+            nc.vector.reciprocal(out=inv_guess[:], in_=root_guess[:])
+            nc.vector.scalar_tensor_tensor(
+                out=quotient[:], in0=factor[:], scalar=0.5, in1=inv_guess[:], op0=ALU.mult, op1=ALU.mult
+            )
+            nc.vector.scalar_tensor_tensor(
+                out=sq_scale[:], in0=root_guess[:], scalar=0.5, in1=quotient[:], op0=ALU.mult, op1=ALU.add
+            )
+            nc.vector.scalar_tensor_tensor(
+                out=sq_bias[:], in0=g[:], scalar=-1.0, in1=sq_scale[:], op0=ALU.mult, op1=ALU.mult
+            )
 
         xn = keep.tile([P, HALVES, CHUNKS, HALF], F32, name="xn")
         neg_mean = keep.tile([P, HALVES, ROW_TILES], F32, name="neg_mean")
@@ -135,7 +156,7 @@ def tile_kanlinear_pa_kernel(tc, x, ln_gamma, ln_beta, base_weight, base_bias, s
 
         def sums_on_scalar(h):
             for t in range(ROW_TILES):
-                unread = work.tile([P, FEATURES], BF16, name="unread", bufs=ROW_TILES)
+                unread = work.tile([P, FEATURES], BF16, name="unread", bufs=2)
                 nc.scalar.activation(
                     out=unread[:], in_=x_bf[h][:, t, :], func=ACT.Identity, accum_out=sums[:, 0, t : t + 1]
                 )
@@ -145,7 +166,7 @@ def tile_kanlinear_pa_kernel(tc, x, ln_gamma, ln_beta, base_weight, base_bias, s
 
         def deviations_on_scalar(h):
             for t in range(ROW_TILES):
-                unread = work.tile([P, FEATURES], BF16, name="unread", bufs=ROW_TILES)
+                unread = work.tile([P, FEATURES], BF16, name="unread", bufs=2)
                 nc.scalar.activation(
                     out=unread[:],
                     in_=x_bf[h][:, t, :],
@@ -177,7 +198,7 @@ def tile_kanlinear_pa_kernel(tc, x, ln_gamma, ln_beta, base_weight, base_bias, s
 
         def normalise(h, engine):
             for t in range(ROW_TILES):
-                z = work.tile([P, FEATURES], F32, name="z", bufs=2 * ROW_TILES)
+                z = work.tile([P, FEATURES], F32, name="z", bufs=ROW_TILES)
                 if engine == "vector":
                     nc.vector.tensor_scalar(
                         out=z[:],
@@ -197,26 +218,35 @@ def tile_kanlinear_pa_kernel(tc, x, ln_gamma, ln_beta, base_weight, base_bias, s
                     )
                 z_tiles[(h, t)] = z
 
+        v_banks = {}
+
         def turn(h, c):
-            z_t = psum.tile([P, HALF], F32, name="z_t", tag="bank")
+            z_t = psum.tile([P, HALF], F32, name="z_t", tag="z_t")
             for t in range(ROW_TILES):
                 nc.tensor.transpose(z_t[:, t * P : (t + 1) * P], z_tiles[(h, t)][:, c * P : (c + 1) * P], ident[:])
             nc.scalar.activation(
                 out=xn[:, h, c, :], in_=z_t[:], func=ACT.Identity, scale=gamma[:, c : c + 1], bias=beta[:, c : c + 1]
             )
+            if (h, c) != (0, 0):
+                v = psum.tile([P, HALF], F32, name="v", tag="v")
+                nc.tensor.matmul(v[:], lhsT=ident[:], rhs=xn[:, h, c, :], start=True, stop=True)
+                v_banks[(h, c)] = v
 
-        def regroup(planes, relu):
-            grouped = work.tile([P, HALF, PACK], BF16, name="grouped", align_bytes=64, bufs=4)
-            dst = grouped[:].rearrange("p (c i) t -> p c t i", i=RUN)
-            src = planes.rearrange("p t (c i) -> p c t i", i=RUN)
-            if relu:
-                cut = VALUE_VECTOR_COLS // RUN
-                nc.vector.tensor_scalar_max(out=dst[:, :cut], in0=src[:, :cut], scalar1=0.0)
-                nc.scalar.activation(out=dst[:, cut:], in_=src[:, cut:], func=ACT.Relu)
-            else:
-                cut = WEIGHT_VECTOR_COLS // RUN
-                nc.vector.tensor_copy(out=dst[:, :cut], in_=src[:, :cut])
-                nc.scalar.copy(out=dst[:, cut:], in_=src[:, cut:])
+        def regroup(planes, relu, shares):
+            grouped = work.tile([P, HALF, PACK], BF16, name="grouped", align_bytes=64, bufs=5)
+            dst_all = grouped[:].rearrange("p (c i) t -> p c t i", i=RUN)
+            src_all = planes.rearrange("p t (c i) -> p c t i", i=RUN)
+            for engine, col0, col1 in shares:
+                dst = dst_all[:, col0 // RUN : col1 // RUN]
+                src = src_all[:, col0 // RUN : col1 // RUN]
+                if engine == "vector" and relu:
+                    nc.vector.tensor_scalar_max(out=dst, in0=src, scalar1=0.0)
+                elif engine == "vector":
+                    nc.vector.tensor_copy(out=dst, in_=src)
+                elif relu:
+                    nc.scalar.activation(out=dst, in_=src, func=ACT.Relu)
+                else:
+                    nc.scalar.copy(out=dst, in_=src)
             return grouped
 
         w_codes = keep.tile([P, SPLINE_PASSES + 1, UNITS], U32, name="w_codes", align_bytes=64)
@@ -239,7 +269,7 @@ def tile_kanlinear_pa_kernel(tc, x, ln_gamma, ln_beta, base_weight, base_bias, s
             )
             for m in range(ROW_TILES):
                 if s == 0:
-                    acc[(h, m)] = psum.tile([P, UNITS], F32, name="acc", tag="bank")
+                    acc[(h, m)] = psum.tile([P, UNITS], F32, name="acc", tag="acc%d" % m, bufs=1)
                 nc.tensor.matmul_mx(
                     out=acc[(h, m)][:],
                     lhsT=codes[:, m * P : (m + 1) * P].bitcast(FP8X4),
@@ -251,103 +281,87 @@ def tile_kanlinear_pa_kernel(tc, x, ln_gamma, ln_beta, base_weight, base_bias, s
                 )
             if s == SPLINE_PASSES - 1:
                 for m in range(ROW_TILES):
-                    result = work.tile([P, UNITS], F32, name="result", bufs=4)
+                    result = work.tile([P, UNITS], F32, name="result", bufs=2)
                     nc.vector.tensor_add(out=result[:], in0=acc[(h, m)][:], in1=bias_bc[:])
                     row0 = h * HALF + m * P
                     nc.sync.dma_start(out=out[row0 : row0 + P, :], in_=result[:])
 
-        waiting = []
-
         sides = {}
-        half_now = [0]
+        values = {}
+        weights = {}
 
-        def regroup_pass(s, h):
-            if h == 0:
-                waiting.append((s, None, regroup(raw[:, s * PACK : (s + 1) * PACK, :], False)))
-            if s == BASE_PASS:
-                waiting.append((s, h, regroup(xn[:, h], True)))
-            else:
-                waiting.append((s, h, regroup(sides[s][0][:], True)))
+        def regroup_weight(s, shares):
+            weights[s] = regroup(raw[:, s * PACK : (s + 1) * PACK, :], False, shares)
 
-        def multiply_waiting():
-            for s, half, grouped in waiting:
-                if half is None:
-                    quantise_weight(s, grouped)
-                else:
-                    multiply(s, half, grouped)
-            waiting[:] = []
+        def regroup_values(s, h, shares):
+            planes = xn[:, h] if s == BASE_PASS else sides[s][0][:]
+            values[(s, h)] = regroup(planes, True, shares)
 
-        stage = {"complete": [], "larger": []}
+        def larger_side(s, cols=slice(0, HALF)):
+            nc.vector.tensor_max(out=sides[s][0][:, :, cols], in0=sides[s][0][:, :, cols], in1=sides[s][1][:, :, cols])
 
-        def finish_step():
-            for s in stage["larger"]:
-                regroup_pass(s, half_now[0])
-            stage["larger"] = stage["complete"]
-            stage["complete"] = []
-            for s in stage["larger"]:
-                nc.vector.tensor_max(out=sides[s][0][:], in0=sides[s][0][:], in1=sides[s][1][:])
-
-        def emit_squares(h, c):
-            squares = []
-            for i in range(KNOTS):
+        def emit_squares(h, c, knots, squares):
+            for i in knots:
                 square = work.tile([P, HALF], F32, name="square", bufs=KNOTS)
-                nc.scalar.activation(out=square[:], in_=xn[:, h, c, :], func=ACT.Square, bias=neg_g[:, c, i : i + 1])
+                nc.scalar.activation(
+                    out=square[:],
+                    in_=xn[:, h, c, :],
+                    func=ACT.Square,
+                    scale=sq_scale[:, c, i : i + 1],
+                    bias=sq_bias[:, c, i : i + 1],
+                )
                 squares.append(square)
-            return squares
 
         def emit_cubes(h, c, squares):
             cubes = []
             for i in range(KNOTS):
-                cube = work.tile([P, HALF], F32, name="cube", bufs=KNOTS + 2)
+                cube = work.tile([P, HALF], F32, name="cube", bufs=KNOTS + 6)
                 nc.vector.scalar_tensor_tensor(
                     out=cube[:],
-                    in0=xn[:, h, c, :],
+                    in0=xn[:, h, c, :] if (h, c) == (0, 0) else v_banks[(h, c)][:],
                     scalar=g[:, c, i : i + 1],
                     in1=squares[i][:],
                     op0=ALU.subtract,
                     op1=ALU.mult,
                 )
                 cubes.append(cube)
-                if i % 2 == 1:
-                    finish_step()
             return cubes
 
         def emit_inners(c, cubes):
             inners = []
             for j in range(BASES):
-                inner_l = work.tile([P, HALF], F32, name="inner_l", bufs=BASES)
-                nc.scalar.activation(out=inner_l[:], in_=cubes[j + 1][:], func=ACT.Relu, scale=a1[:, c, j : j + 1])
+                inner_l = work.tile([P, HALF], F32, name="inner_l", bufs=BASES + 4)
+                nc.scalar.activation(
+                    out=inner_l[:], in_=cubes[j + 1][:], func=ACT.Relu, scale=l_inner[:, c, j : j + 1]
+                )
                 inner_r = work.tile([P, HALF], F32, name="inner_r", bufs=BASES)
-                nc.scalar.activation(out=inner_r[:], in_=cubes[j + 3][:], func=ACT.Relu, scale=neg_c3[:, c, j : j + 1])
+                nc.scalar.activation(
+                    out=inner_r[:], in_=cubes[j + 3][:], func=ACT.Relu, scale=r_inner[:, c, j : j + 1]
+                )
                 inners.append((inner_l, inner_r))
             return inners
 
-        def emit_sides(c, j, cubes, inners):
+        def side_slot(c, j, side):
             q = c * BASES + j
             s = q // PACK
-            if q % PACK == 0:
-                left4 = work.tile([P, PACK, HALF], BF16, name="left4", bufs=3)
-                right4 = work.tile([P, PACK, HALF], BF16, name="right4", bufs=3)
+            if side == 1 and q % PACK == 0:
+                left4 = work.tile([P, PACK, HALF], BF16, name="left4", bufs=4)
+                right4 = work.tile([P, PACK, HALF], BF16, name="right4", bufs=4)
                 sides[s] = (left4, right4)
-            left4, right4 = sides[s]
+            return sides[s][side][:, q % PACK, :]
+
+        def emit_left(c, j, cubes, inners, engine):
+            engine.tensor_sub(out=side_slot(c, j, 0), in0=cubes[j][:], in1=inners[j][0][:])
+
+        def emit_right(c, j, cubes, inners):
             nc.vector.scalar_tensor_tensor(
-                out=left4[:, q % PACK, :],
-                in0=cubes[j][:],
-                scalar=a0[:, c, j : j + 1],
-                in1=inners[j][0][:],
-                op0=ALU.mult,
-                op1=ALU.subtract,
-            )
-            nc.vector.scalar_tensor_tensor(
-                out=right4[:, q % PACK, :],
+                out=side_slot(c, j, 1),
                 in0=cubes[j + 4][:],
-                scalar=neg_c4[:, c, j : j + 1],
+                scalar=r_first[:, c, j : j + 1] if j < 3 else -1.0,
                 in1=inners[j][1][:],
                 op0=ALU.mult,
                 op1=ALU.subtract,
             )
-            if q % PACK == PACK - 1:
-                stage["complete"].append(s)
 
         moments_on_vector(0)
         root(0)
@@ -358,36 +372,73 @@ def tile_kanlinear_pa_kernel(tc, x, ln_gamma, ln_beta, base_weight, base_bias, s
         turn(0, 0)
         knot_coefficients()
         mean_of_sums(1)
-        squares = emit_squares(0, 0)
+        squares = []
+        emit_squares(0, 0, range(KNOTS), squares)
         blocks = [(h, c) for h in range(HALVES) for c in range(CHUNKS)]
+        value_shares = [("scalar", 0, VALUE_SCALAR_COLS), ("vector", VALUE_SCALAR_COLS, HALF)]
+        previous = None
         for b in range(len(blocks)):
             h, c = blocks[b]
             last_block = b == len(blocks) - 1
             if not last_block:
                 turn(blocks[b + 1][0], blocks[b + 1][1])
+            ready = []
+            if b > 0:
+                pc, p_cubes, p_inners = previous
+                for j in GPSIMD_LEFTS:
+                    emit_left(pc, j, p_cubes, p_inners, nc.gpsimd)
+                ready = [(s, blocks[b - 1][0]) for s in COMPLETE[pc]]
+                if pc == 2:
+                    ready.append((BASE_PASS, blocks[b - 1][0]))
             cubes = emit_cubes(h, c, squares)
-            half_now[0] = h
             inners = emit_inners(c, cubes)
+            for s, vh in ready:
+                if s != BASE_PASS:
+                    larger_side(s)
             if b == 1:
                 variance_of_sums(1)
             if b == 2:
                 reciprocal_root(1)
+            squares = []
             if not last_block:
-                squares = emit_squares(blocks[b + 1][0], blocks[b + 1][1])
+                emit_squares(blocks[b + 1][0], blocks[b + 1][1], range(0, 3), squares)
+            emit_right(c, 0, cubes, inners)
+            for s, vh in ready:
+                regroup_values(s, vh, value_shares)
+            emit_right(c, 1, cubes, inners)
+            if not last_block:
+                emit_squares(blocks[b + 1][0], blocks[b + 1][1], range(3, KNOTS), squares)
             if b == 0:
                 deviations_on_scalar(1)
             if b == 1:
                 root(1)
             if b == 2:
                 normalise(1, "scalar")
-            multiply_waiting()
-            for j in range(BASES):
-                emit_sides(c, j, cubes, inners)
-                finish_step()
-                if last_block and j == BASES - 2:
-                    multiply_waiting()
-            if c == CHUNKS - 2:
-                regroup_pass(BASE_PASS, h)
-        finish_step()
-        finish_step()
-        multiply_waiting()
+            for s in REGROUP_WEIGHTS[b]:
+                regroup_weight(s, [("vector", 0, UNITS)])
+            emit_right(c, 2, cubes, inners)
+            emit_right(c, 3, cubes, inners)
+            for s, vh in ready:
+                multiply(s, vh, values[(s, vh)])
+            if last_block:
+                for j in (0, 1):
+                    emit_left(c, j, cubes, inners, nc.vector)
+                emit_right(c, 4, cubes, inners)
+                larger_side(4)
+                regroup_values(4, h, [("scalar", 0, HALF)])
+                emit_right(c, 5, cubes, inners)
+                for j in (2, 3, 4, 5):
+                    emit_left(c, j, cubes, inners, nc.vector)
+            else:
+                emit_right(c, 4, cubes, inners)
+                emit_right(c, 5, cubes, inners)
+                for j in range(BASES):
+                    if j not in GPSIMD_LEFTS:
+                        emit_left(c, j, cubes, inners, nc.vector)
+            for s in REGROUP_WEIGHTS[b]:
+                quantise_weight(s, weights[s])
+            previous = (c, cubes, inners)
+        larger_side(5)
+        multiply(4, 1, values[(4, 1)])
+        regroup_values(5, 1, [("scalar", 0, TAIL_SCALAR_COLS), ("vector", TAIL_SCALAR_COLS, HALF)])
+        multiply(5, 1, values[(5, 1)])

@@ -27,9 +27,11 @@ SPLINE_PASSES = PLANES // PACK
 BASE_PASS = SPLINE_PASSES
 LN_EPS = 0.001
 RUN = 4
-VALUE_SCALAR_COLS = 320
+VALUE_SCALAR_COLS = {0: 0, 1: 320, 2: 256}
+LAST_SCALAR_COLS = 448
 TAIL_SCALAR_COLS = 192
-GPSIMD_LEFTS = (0, 1, 2, 3)
+GPSIMD_LEFTS = (0, 1, 2, 3, 4)
+COPIED_CUBES = (4, 5)
 COMPLETE = [[0], [1, 2], [3], [4, 5]]
 REGROUP_WEIGHTS = [[0, 1], [2, 6], [3, 4], [5], [], [], [], []]
 
@@ -42,7 +44,7 @@ def tile_kanlinear_pa_kernel(tc, x, ln_gamma, ln_beta, base_weight, base_bias, s
         const = ctx.enter_context(tc.tile_pool(name="const", bufs=1))
         keep = ctx.enter_context(tc.tile_pool(name="keep", bufs=1))
         work = ctx.enter_context(tc.tile_pool(name="work", bufs=2))
-        psum = ctx.enter_context(tc.psum_pool(name="psum", bufs=2))
+        psum = ctx.enter_context(tc.psum_pool(name="psum", bufs=1))
         ctx.enter_context(tc.manual_schedule())
 
         x_bf = []
@@ -90,37 +92,32 @@ def tile_kanlinear_pa_kernel(tc, x, ln_gamma, ln_beta, base_weight, base_bias, s
         factor = const.tile([P, CHUNKS, KNOTS], F32, name="factor")
         root_guess = const.tile([P, CHUNKS, KNOTS], F32, name="root_guess")
 
-        def knot_casts():
-            nc.vector.tensor_copy(out=g[:], in_=grid_bf[:])
-            nc.vector.tensor_copy(out=gamma[:], in_=gamma_bf[:])
-            nc.vector.tensor_copy(out=beta[:], in_=beta_bf[:])
+        d4 = const.tile([P, CHUNKS, KNOTS - 4], F32, name="d4")
+        neg_d4 = const.tile([P, CHUNKS, KNOTS - 4], F32, name="neg_d4")
 
-        def knot_coefficients():
+        def knot_differences():
+            nc.gpsimd.tensor_copy(out=g[:], in_=grid_bf[:])
             d2 = const.tile([P, CHUNKS, KNOTS - 2], F32, name="d2")
             d3 = const.tile([P, CHUNKS, KNOTS - 3], F32, name="d3")
-            d4 = const.tile([P, CHUNKS, KNOTS - 4], F32, name="d4")
-            neg_d4 = const.tile([P, CHUNKS, KNOTS - 4], F32, name="neg_d4")
-            nc.vector.tensor_sub(out=den[:, :, 14:23], in0=g[:, :, 1:10], in1=g[:, :, 0:9])
-            nc.vector.tensor_sub(out=d2[:], in0=g[:, :, 2:10], in1=g[:, :, 0:8])
-            nc.vector.tensor_sub(out=d3[:], in0=g[:, :, 3:10], in1=g[:, :, 0:7])
-            nc.vector.tensor_sub(out=d4[:], in0=g[:, :, 4:10], in1=g[:, :, 0:6])
-            nc.vector.tensor_sub(out=neg_d4[:], in0=g[:, :, 0:6], in1=g[:, :, 4:10])
+            nc.gpsimd.tensor_sub(out=den[:, :, 14:23], in0=g[:, :, 1:10], in1=g[:, :, 0:9])
+            nc.gpsimd.tensor_sub(out=d2[:], in0=g[:, :, 2:10], in1=g[:, :, 0:8])
+            nc.gpsimd.tensor_sub(out=d3[:], in0=g[:, :, 3:10], in1=g[:, :, 0:7])
+            nc.gpsimd.tensor_sub(out=d4[:], in0=g[:, :, 4:10], in1=g[:, :, 0:6])
+            nc.gpsimd.tensor_sub(out=neg_d4[:], in0=g[:, :, 0:6], in1=g[:, :, 4:10])
             prod_a = const.tile([P, CHUNKS, 7], F32, name="prod_a")
             prod_b = const.tile([P, CHUNKS, 7], F32, name="prod_b")
-            nc.vector.tensor_mul(out=prod_a[:], in0=den[:, :, 14:21], in1=d2[:, :, 0:7])
-            nc.vector.tensor_mul(out=prod_b[:], in0=den[:, :, 16:23], in1=d2[:, :, 1:8])
-            nc.vector.tensor_mul(out=den[:, :, 0:7], in0=prod_a[:], in1=d3[:])
-            nc.vector.tensor_mul(out=den[:, :, 7:14], in0=prod_b[:], in1=d3[:])
+            nc.gpsimd.tensor_mul(out=prod_a[:], in0=den[:, :, 14:21], in1=d2[:, :, 0:7])
+            nc.gpsimd.tensor_mul(out=prod_b[:], in0=den[:, :, 16:23], in1=d2[:, :, 1:8])
+            nc.gpsimd.tensor_mul(out=den[:, :, 0:7], in0=prod_a[:], in1=d3[:])
+            nc.gpsimd.tensor_mul(out=den[:, :, 7:14], in0=prod_b[:], in1=d3[:])
+
+        def knot_factors():
             nc.vector.reciprocal(out=inv[:], in_=den[:])
             nc.vector.tensor_copy(out=factor[:, :, 0:7], in_=inv[:, :, 0:7])
             nc.vector.tensor_copy(out=factor[:, :, 7:10], in_=inv[:, :, 11:14])
             nc.scalar.activation(out=root_guess[:], in_=factor[:], func=ACT.Sqrt)
-            ratio = const.tile([P, CHUNKS, 4], F32, name="ratio")
-            nc.vector.tensor_mul(out=ratio[:], in0=inv[:, :, 7:11], in1=den[:, :, 3:7])
-            nc.vector.tensor_mul(out=l_inner[:], in0=d4[:], in1=inv[:, :, 14:20])
-            nc.vector.tensor_mul(out=r_inner[:], in0=neg_d4[:], in1=inv[:, :, 17:23])
-            nc.vector.tensor_scalar_mul(out=r_first[:], in0=ratio[:, :, 1:4], scalar1=-1.0)
-            nc.vector.tensor_mul(out=r_inner[:, :, 0:4], in0=r_inner[:, :, 0:4], in1=ratio[:])
+
+        def knot_coefficients():
             quotient = const.tile([P, CHUNKS, KNOTS], F32, name="quotient")
             inv_guess = const.tile([P, CHUNKS, KNOTS], F32, name="inv_guess")
             nc.vector.reciprocal(out=inv_guess[:], in_=root_guess[:])
@@ -133,6 +130,12 @@ def tile_kanlinear_pa_kernel(tc, x, ln_gamma, ln_beta, base_weight, base_bias, s
             nc.vector.scalar_tensor_tensor(
                 out=sq_bias[:], in0=g[:], scalar=-1.0, in1=sq_scale[:], op0=ALU.mult, op1=ALU.mult
             )
+            ratio = const.tile([P, CHUNKS, 4], F32, name="ratio")
+            nc.gpsimd.tensor_mul(out=ratio[:], in0=inv[:, :, 7:11], in1=den[:, :, 3:7])
+            nc.gpsimd.tensor_mul(out=l_inner[:], in0=d4[:], in1=inv[:, :, 14:20])
+            nc.gpsimd.tensor_mul(out=r_inner[:], in0=neg_d4[:], in1=inv[:, :, 17:23])
+            nc.gpsimd.tensor_scalar_mul(out=r_first[:], in0=ratio[:, :, 1:4], scalar1=-1.0)
+            nc.gpsimd.tensor_mul(out=r_inner[:, :, 0:4], in0=r_inner[:, :, 0:4], in1=ratio[:])
 
         xn = keep.tile([P, HALVES, CHUNKS, HALF], F32, name="xn")
         neg_mean = keep.tile([P, HALVES, ROW_TILES], F32, name="neg_mean")
@@ -154,8 +157,8 @@ def tile_kanlinear_pa_kernel(tc, x, ln_gamma, ln_beta, base_weight, base_bias, s
 
         sums = keep.tile([P, 2, ROW_TILES], F32, name="sums")
 
-        def sums_on_scalar(h):
-            for t in range(ROW_TILES):
+        def sums_on_scalar(h, tiles):
+            for t in tiles:
                 unread = work.tile([P, FEATURES], BF16, name="unread", bufs=2)
                 nc.scalar.activation(
                     out=unread[:], in_=x_bf[h][:, t, :], func=ACT.Identity, accum_out=sums[:, 0, t : t + 1]
@@ -164,8 +167,8 @@ def tile_kanlinear_pa_kernel(tc, x, ln_gamma, ln_beta, base_weight, base_bias, s
         def mean_of_sums(h):
             nc.vector.tensor_scalar_mul(out=neg_mean[:, h, :], in0=sums[:, 0, :], scalar1=-1.0 / FEATURES)
 
-        def deviations_on_scalar(h):
-            for t in range(ROW_TILES):
+        def deviations_on_scalar(h, tiles):
+            for t in tiles:
                 unread = work.tile([P, FEATURES], BF16, name="unread", bufs=2)
                 nc.scalar.activation(
                     out=unread[:],
@@ -196,8 +199,8 @@ def tile_kanlinear_pa_kernel(tc, x, ln_gamma, ln_beta, base_weight, base_bias, s
             )
             nc.vector.tensor_mul(out=shift[:, h, :], in0=neg_mean[:, h, :], in1=rstd[:, h, :])
 
-        def normalise(h, engine):
-            for t in range(ROW_TILES):
+        def normalise(h, tiles, engine):
+            for t in tiles:
                 z = work.tile([P, FEATURES], F32, name="z", bufs=ROW_TILES)
                 if engine == "vector":
                     nc.vector.tensor_scalar(
@@ -220,23 +223,35 @@ def tile_kanlinear_pa_kernel(tc, x, ln_gamma, ln_beta, base_weight, base_bias, s
 
         v_banks = {}
 
+        turned = {}
+
         def turn(h, c):
             z_t = psum.tile([P, HALF], F32, name="z_t", tag="z_t")
             for t in range(ROW_TILES):
                 nc.tensor.transpose(z_t[:, t * P : (t + 1) * P], z_tiles[(h, t)][:, c * P : (c + 1) * P], ident[:])
+            turned[(h, c)] = z_t
+
+        def scale_and_shift(h, c):
             nc.scalar.activation(
-                out=xn[:, h, c, :], in_=z_t[:], func=ACT.Identity, scale=gamma[:, c : c + 1], bias=beta[:, c : c + 1]
+                out=xn[:, h, c, :],
+                in_=turned[(h, c)][:],
+                func=ACT.Identity,
+                scale=gamma[:, c : c + 1],
+                bias=beta[:, c : c + 1],
             )
-            if (h, c) != (0, 0):
-                v = psum.tile([P, HALF], F32, name="v", tag="v")
-                nc.tensor.matmul(v[:], lhsT=ident[:], rhs=xn[:, h, c, :], start=True, stop=True)
-                v_banks[(h, c)] = v
+
+        def copy_to_psum(h, c):
+            v = psum.tile([P, HALF], F32, name="v", tag="v")
+            nc.tensor.matmul(v[:], lhsT=ident[:], rhs=xn[:, h, c, :], start=True, stop=True)
+            v_banks[(h, c)] = v
 
         def regroup(planes, relu, shares):
             grouped = work.tile([P, HALF, PACK], BF16, name="grouped", align_bytes=64, bufs=5)
             dst_all = grouped[:].rearrange("p (c i) t -> p c t i", i=RUN)
             src_all = planes.rearrange("p t (c i) -> p c t i", i=RUN)
             for engine, col0, col1 in shares:
+                if col0 == col1:
+                    continue
                 dst = dst_all[:, col0 // RUN : col1 // RUN]
                 src = src_all[:, col0 // RUN : col1 // RUN]
                 if engine == "vector" and relu:
@@ -281,7 +296,7 @@ def tile_kanlinear_pa_kernel(tc, x, ln_gamma, ln_beta, base_weight, base_bias, s
                 )
             if s == SPLINE_PASSES - 1:
                 for m in range(ROW_TILES):
-                    result = work.tile([P, UNITS], F32, name="result", bufs=2)
+                    result = work.tile([P, UNITS], F32, name="result", bufs=4)
                     nc.vector.tensor_add(out=result[:], in0=acc[(h, m)][:], in1=bias_bc[:])
                     row0 = h * HALF + m * P
                     nc.sync.dma_start(out=out[row0 : row0 + P, :], in_=result[:])
@@ -312,10 +327,12 @@ def tile_kanlinear_pa_kernel(tc, x, ln_gamma, ln_beta, base_weight, base_bias, s
                 )
                 squares.append(square)
 
+        cube_banks = {}
+
         def emit_cubes(h, c, squares):
             cubes = []
             for i in range(KNOTS):
-                cube = work.tile([P, HALF], F32, name="cube", bufs=KNOTS + 6)
+                cube = work.tile([P, HALF], F32, name="cube", bufs=2 * KNOTS)
                 nc.vector.scalar_tensor_tensor(
                     out=cube[:],
                     in0=xn[:, h, c, :] if (h, c) == (0, 0) else v_banks[(h, c)][:],
@@ -325,21 +342,21 @@ def tile_kanlinear_pa_kernel(tc, x, ln_gamma, ln_beta, base_weight, base_bias, s
                     op1=ALU.mult,
                 )
                 cubes.append(cube)
+                if (h, c) != (0, 0) and i in COPIED_CUBES:
+                    copy = psum.tile([P, HALF], F32, name="copy", tag="cube%d" % i)
+                    nc.tensor.matmul(copy[:], lhsT=ident[:], rhs=cube[:], start=True, stop=True)
+                    cube_banks[i] = copy
             return cubes
 
-        def emit_inners(c, cubes):
-            inners = []
-            for j in range(BASES):
-                inner_l = work.tile([P, HALF], F32, name="inner_l", bufs=BASES + 4)
-                nc.scalar.activation(
-                    out=inner_l[:], in_=cubes[j + 1][:], func=ACT.Relu, scale=l_inner[:, c, j : j + 1]
-                )
-                inner_r = work.tile([P, HALF], F32, name="inner_r", bufs=BASES)
-                nc.scalar.activation(
-                    out=inner_r[:], in_=cubes[j + 3][:], func=ACT.Relu, scale=r_inner[:, c, j : j + 1]
-                )
-                inners.append((inner_l, inner_r))
-            return inners
+        def emit_inner_left(c, j, cubes):
+            inner = work.tile([P, HALF], F32, name="inner_l", bufs=BASES)
+            nc.scalar.activation(out=inner[:], in_=cubes[j + 1][:], func=ACT.Relu, scale=l_inner[:, c, j : j + 1])
+            return inner
+
+        def emit_inner_right(c, j, cubes):
+            inner = work.tile([P, HALF], F32, name="inner_r", bufs=BASES)
+            nc.scalar.activation(out=inner[:], in_=cubes[j + 3][:], func=ACT.Relu, scale=r_inner[:, c, j : j + 1])
+            return inner
 
         def side_slot(c, j, side):
             q = c * BASES + j
@@ -350,94 +367,105 @@ def tile_kanlinear_pa_kernel(tc, x, ln_gamma, ln_beta, base_weight, base_bias, s
                 sides[s] = (left4, right4)
             return sides[s][side][:, q % PACK, :]
 
-        def emit_left(c, j, cubes, inners, engine):
-            engine.tensor_sub(out=side_slot(c, j, 0), in0=cubes[j][:], in1=inners[j][0][:])
+        def emit_left(c, j, cubes, inner, engine):
+            first = cubes[j] if engine is nc.gpsimd or j not in cube_banks else cube_banks[j]
+            engine.tensor_sub(out=side_slot(c, j, 0), in0=first[:], in1=inner[:])
 
-        def emit_right(c, j, cubes, inners):
+        def emit_right(c, j, cubes, inner):
             nc.vector.scalar_tensor_tensor(
                 out=side_slot(c, j, 1),
-                in0=cubes[j + 4][:],
+                in0=cube_banks[j + 4][:] if j + 4 in cube_banks else cubes[j + 4][:],
                 scalar=r_first[:, c, j : j + 1] if j < 3 else -1.0,
-                in1=inners[j][1][:],
+                in1=inner[:],
                 op0=ALU.mult,
                 op1=ALU.subtract,
             )
 
+        knot_differences()
         moments_on_vector(0)
+        sums_on_scalar(1, (0,))
         root(0)
-        sums_on_scalar(1)
-        knot_casts()
+        knot_factors()
         reciprocal_root(0)
-        normalise(0, "vector")
+        nc.vector.tensor_copy(out=gamma[:], in_=gamma_bf[:])
+        nc.vector.tensor_copy(out=beta[:], in_=beta_bf[:])
+        normalise(0, (0, 1, 2), "vector")
+        normalise(0, (3,), "scalar")
         turn(0, 0)
+        sums_on_scalar(1, (1, 2, 3))
+        scale_and_shift(0, 0)
+        turn(0, 1)
         knot_coefficients()
         mean_of_sums(1)
+        blocks = [(h, c) for h in range(HALVES) for c in range(CHUNKS)]
         squares = []
         emit_squares(0, 0, range(KNOTS), squares)
-        blocks = [(h, c) for h in range(HALVES) for c in range(CHUNKS)]
-        value_shares = [("scalar", 0, VALUE_SCALAR_COLS), ("vector", VALUE_SCALAR_COLS, HALF)]
+        gate = const.tile([P, 1], F32, name="gate")
+        passed = const.tile([P, 1], F32, name="passed")
         previous = None
         for b in range(len(blocks)):
             h, c = blocks[b]
             last_block = b == len(blocks) - 1
-            if not last_block:
-                turn(blocks[b + 1][0], blocks[b + 1][1])
+            lefts_by_gpsimd = () if last_block else GPSIMD_LEFTS
             ready = []
             if b > 0:
-                pc, p_cubes, p_inners = previous
+                pc, p_cubes, p_lefts = previous
                 for j in GPSIMD_LEFTS:
-                    emit_left(pc, j, p_cubes, p_inners, nc.gpsimd)
+                    emit_left(pc, j, p_cubes, p_lefts[j], nc.gpsimd)
                 ready = [(s, blocks[b - 1][0]) for s in COMPLETE[pc]]
                 if pc == 2:
                     ready.append((BASE_PASS, blocks[b - 1][0]))
+            if not last_block:
+                scale_and_shift(*blocks[b + 1])
             cubes = emit_cubes(h, c, squares)
-            inners = emit_inners(c, cubes)
+            if not last_block:
+                copy_to_psum(*blocks[b + 1])
+            if b + 2 < len(blocks):
+                turn(*blocks[b + 2])
+            rights = [emit_inner_right(c, j, cubes) for j in range(2)]
+            emit_right(c, 0, cubes, rights[0])
+            emit_right(c, 1, cubes, rights[1])
+            rights = rights + [emit_inner_right(c, j, cubes) for j in range(2, BASES)]
+            lefts = {}
+            for j in [j for j in range(BASES) if j not in lefts_by_gpsimd] + list(lefts_by_gpsimd):
+                lefts[j] = emit_inner_left(c, j, cubes)
             for s, vh in ready:
                 if s != BASE_PASS:
                     larger_side(s)
             if b == 1:
-                variance_of_sums(1)
-            if b == 2:
                 reciprocal_root(1)
             squares = []
-            if not last_block:
-                emit_squares(blocks[b + 1][0], blocks[b + 1][1], range(0, 3), squares)
-            emit_right(c, 0, cubes, inners)
-            for s, vh in ready:
-                regroup_values(s, vh, value_shares)
-            emit_right(c, 1, cubes, inners)
-            if not last_block:
-                emit_squares(blocks[b + 1][0], blocks[b + 1][1], range(3, KNOTS), squares)
             if b == 0:
-                deviations_on_scalar(1)
+                deviations_on_scalar(1, range(ROW_TILES))
             if b == 1:
-                root(1)
-            if b == 2:
-                normalise(1, "scalar")
+                normalise(1, range(ROW_TILES), "scalar")
+            emit_right(c, 2, cubes, rights[2])
+            share = LAST_SCALAR_COLS if last_block else VALUE_SCALAR_COLS[len(ready)]
+            for s, vh in ready:
+                regroup_values(s, vh, [("scalar", 0, share), ("vector", share, HALF)])
+            for j in range(3, BASES):
+                emit_right(c, j, cubes, rights[j])
+            if not last_block:
+                emit_squares(*blocks[b + 1], range(KNOTS), squares)
             for s in REGROUP_WEIGHTS[b]:
                 regroup_weight(s, [("vector", 0, UNITS)])
-            emit_right(c, 2, cubes, inners)
-            emit_right(c, 3, cubes, inners)
+            for j in range(BASES):
+                if j not in lefts_by_gpsimd:
+                    emit_left(c, j, cubes, lefts[j], nc.vector)
+                if last_block and j == 1:
+                    larger_side(4)
+                    regroup_values(4, h, [("scalar", 0, HALF)])
             for s, vh in ready:
                 multiply(s, vh, values[(s, vh)])
-            if last_block:
-                for j in (0, 1):
-                    emit_left(c, j, cubes, inners, nc.vector)
-                emit_right(c, 4, cubes, inners)
-                larger_side(4)
-                regroup_values(4, h, [("scalar", 0, HALF)])
-                emit_right(c, 5, cubes, inners)
-                for j in (2, 3, 4, 5):
-                    emit_left(c, j, cubes, inners, nc.vector)
-            else:
-                emit_right(c, 4, cubes, inners)
-                emit_right(c, 5, cubes, inners)
-                for j in range(BASES):
-                    if j not in GPSIMD_LEFTS:
-                        emit_left(c, j, cubes, inners, nc.vector)
             for s in REGROUP_WEIGHTS[b]:
                 quantise_weight(s, weights[s])
-            previous = (c, cubes, inners)
+            if b == 0:
+                variance_of_sums(1)
+                root(1)
+            if not last_block:
+                nc.vector.memset(gate[:], float(b))
+                nc.gpsimd.tensor_copy(out=passed[:], in_=gate[:])
+            previous = (c, cubes, lefts)
         larger_side(5)
         multiply(4, 1, values[(4, 1)])
         regroup_values(5, 1, [("scalar", 0, TAIL_SCALAR_COLS), ("vector", TAIL_SCALAR_COLS, HALF)])

@@ -27,13 +27,13 @@ SPLINE_PASSES = PLANES // PACK
 BASE_PASS = SPLINE_PASSES
 LN_EPS = 0.001
 RUN = 4
-VALUE_SCALAR_COLS = {0: 0, 1: 320, 2: 256}
-LAST_SCALAR_COLS = 448
-TAIL_SCALAR_COLS = 192
+VALUE_SCALAR_COLS = 256
+LAST_SCALAR_COLS = 384
+TAIL_SCALAR_COLS = 96
 GPSIMD_LEFTS = (0, 1, 2, 3, 4)
 COPIED_CUBES = (4, 5)
 COMPLETE = [[0], [1, 2], [3], [4, 5]]
-REGROUP_WEIGHTS = [[0, 1], [2, 6], [3, 4], [5], [], [], [], []]
+REGROUP_WEIGHTS = [[0, 1, 2], [6, 3], [4], [5], [], [], [], []]
 
 FLOPS = 2 * ROWS * (FEATURES + FEATURES * BASES) * UNITS
 
@@ -89,7 +89,7 @@ def tile_kanlinear_pa_kernel(tc, x, ln_gamma, ln_beta, base_weight, base_bias, s
         l_inner = const.tile([P, CHUNKS, BASES], F32, name="l_inner")
         r_inner = const.tile([P, CHUNKS, BASES], F32, name="r_inner")
         r_first = const.tile([P, CHUNKS, 3], F32, name="r_first")
-        factor = const.tile([P, CHUNKS, KNOTS], F32, name="factor")
+        factor = inv[:, :, 0:KNOTS]
         root_guess = const.tile([P, CHUNKS, KNOTS], F32, name="root_guess")
 
         d4 = const.tile([P, CHUNKS, KNOTS - 4], F32, name="d4")
@@ -97,6 +97,8 @@ def tile_kanlinear_pa_kernel(tc, x, ln_gamma, ln_beta, base_weight, base_bias, s
 
         def knot_differences():
             nc.gpsimd.tensor_copy(out=g[:], in_=grid_bf[:])
+            nc.gpsimd.tensor_copy(out=gamma[:], in_=gamma_bf[:])
+            nc.gpsimd.tensor_copy(out=beta[:], in_=beta_bf[:])
             d2 = const.tile([P, CHUNKS, KNOTS - 2], F32, name="d2")
             d3 = const.tile([P, CHUNKS, KNOTS - 3], F32, name="d3")
             nc.gpsimd.tensor_sub(out=den[:, :, 14:23], in0=g[:, :, 1:10], in1=g[:, :, 0:9])
@@ -109,20 +111,19 @@ def tile_kanlinear_pa_kernel(tc, x, ln_gamma, ln_beta, base_weight, base_bias, s
             nc.gpsimd.tensor_mul(out=prod_a[:], in0=den[:, :, 14:21], in1=d2[:, :, 0:7])
             nc.gpsimd.tensor_mul(out=prod_b[:], in0=den[:, :, 16:23], in1=d2[:, :, 1:8])
             nc.gpsimd.tensor_mul(out=den[:, :, 0:7], in0=prod_a[:], in1=d3[:])
-            nc.gpsimd.tensor_mul(out=den[:, :, 7:14], in0=prod_b[:], in1=d3[:])
+            nc.gpsimd.tensor_mul(out=den[:, :, 7:10], in0=prod_b[:, :, 4:7], in1=d3[:, :, 4:7])
+            nc.gpsimd.tensor_mul(out=den[:, :, 10:14], in0=prod_b[:, :, 0:4], in1=d3[:, :, 0:4])
 
         def knot_factors():
             nc.vector.reciprocal(out=inv[:], in_=den[:])
-            nc.vector.tensor_copy(out=factor[:, :, 0:7], in_=inv[:, :, 0:7])
-            nc.vector.tensor_copy(out=factor[:, :, 7:10], in_=inv[:, :, 11:14])
-            nc.scalar.activation(out=root_guess[:], in_=factor[:], func=ACT.Sqrt)
+            nc.scalar.activation(out=root_guess[:], in_=factor, func=ACT.Sqrt)
 
-        def knot_coefficients():
+        def knot_roots():
             quotient = const.tile([P, CHUNKS, KNOTS], F32, name="quotient")
             inv_guess = const.tile([P, CHUNKS, KNOTS], F32, name="inv_guess")
             nc.vector.reciprocal(out=inv_guess[:], in_=root_guess[:])
             nc.vector.scalar_tensor_tensor(
-                out=quotient[:], in0=factor[:], scalar=0.5, in1=inv_guess[:], op0=ALU.mult, op1=ALU.mult
+                out=quotient[:], in0=factor, scalar=0.5, in1=inv_guess[:], op0=ALU.mult, op1=ALU.mult
             )
             nc.vector.scalar_tensor_tensor(
                 out=sq_scale[:], in0=root_guess[:], scalar=0.5, in1=quotient[:], op0=ALU.mult, op1=ALU.add
@@ -130,8 +131,10 @@ def tile_kanlinear_pa_kernel(tc, x, ln_gamma, ln_beta, base_weight, base_bias, s
             nc.vector.scalar_tensor_tensor(
                 out=sq_bias[:], in0=g[:], scalar=-1.0, in1=sq_scale[:], op0=ALU.mult, op1=ALU.mult
             )
+
+        def knot_coefficients():
             ratio = const.tile([P, CHUNKS, 4], F32, name="ratio")
-            nc.gpsimd.tensor_mul(out=ratio[:], in0=inv[:, :, 7:11], in1=den[:, :, 3:7])
+            nc.gpsimd.tensor_mul(out=ratio[:], in0=inv[:, :, 10:14], in1=den[:, :, 3:7])
             nc.gpsimd.tensor_mul(out=l_inner[:], in0=d4[:], in1=inv[:, :, 14:20])
             nc.gpsimd.tensor_mul(out=r_inner[:], in0=neg_d4[:], in1=inv[:, :, 17:23])
             nc.gpsimd.tensor_scalar_mul(out=r_first[:], in0=ratio[:, :, 1:4], scalar1=-1.0)
@@ -276,15 +279,22 @@ def tile_kanlinear_pa_kernel(tc, x, ln_gamma, ln_beta, base_weight, base_bias, s
 
         acc = {}
 
-        def multiply(s, h, grouped):
+        def quantise_values(grouped, codes, scales, rows):
+            nc.vector.quantize_mx(
+                out=codes[:, rows].bitcast(FP8X4),
+                scales=scales[:, rows],
+                in_=grouped[:, rows, :].rearrange("p n t -> p (n t)"),
+            )
+
+        def codes_and_scales():
             codes = work.tile([P, HALF], U32, name="codes", align_bytes=64, bufs=3)
             scales = work.tile([P, HALF], U8, name="scales", align_bytes=64, bufs=3)
-            nc.vector.quantize_mx(
-                out=codes[:].bitcast(FP8X4), scales=scales[:], in_=grouped[:].rearrange("p n t -> p (n t)")
-            )
-            for m in range(ROW_TILES):
+            return codes, scales
+
+        def accumulate(s, h, codes, scales, row_tiles):
+            for m in row_tiles:
                 if s == 0:
-                    acc[(h, m)] = psum.tile([P, UNITS], F32, name="acc", tag="acc%d" % m, bufs=1)
+                    acc[(h, m)] = psum.tile([P, UNITS], F32, name="acc", tag="acc%d" % m)
                 nc.tensor.matmul_mx(
                     out=acc[(h, m)][:],
                     lhsT=codes[:, m * P : (m + 1) * P].bitcast(FP8X4),
@@ -294,12 +304,18 @@ def tile_kanlinear_pa_kernel(tc, x, ln_gamma, ln_beta, base_weight, base_bias, s
                     start=(s == 0),
                     stop=(s == SPLINE_PASSES - 1),
                 )
-            if s == SPLINE_PASSES - 1:
-                for m in range(ROW_TILES):
-                    result = work.tile([P, UNITS], F32, name="result", bufs=4)
-                    nc.vector.tensor_add(out=result[:], in0=acc[(h, m)][:], in1=bias_bc[:])
-                    row0 = h * HALF + m * P
-                    nc.sync.dma_start(out=out[row0 : row0 + P, :], in_=result[:])
+
+        def store(h, row_tiles):
+            for m in row_tiles:
+                result = work.tile([P, UNITS], F32, name="result", bufs=4)
+                nc.vector.tensor_add(out=result[:], in0=acc[(h, m)][:], in1=bias_bc[:])
+                row0 = h * HALF + m * P
+                nc.sync.dma_start(out=out[row0 : row0 + P, :], in_=result[:])
+
+        def multiply(s, h, grouped):
+            codes, scales = codes_and_scales()
+            quantise_values(grouped, codes, scales, slice(0, HALF))
+            accumulate(s, h, codes, scales, range(ROW_TILES))
 
         sides = {}
         values = {}
@@ -385,16 +401,16 @@ def tile_kanlinear_pa_kernel(tc, x, ln_gamma, ln_beta, base_weight, base_bias, s
         moments_on_vector(0)
         sums_on_scalar(1, (0,))
         root(0)
-        knot_factors()
+        sums_on_scalar(1, (1, 2))
         reciprocal_root(0)
-        nc.vector.tensor_copy(out=gamma[:], in_=gamma_bf[:])
-        nc.vector.tensor_copy(out=beta[:], in_=beta_bf[:])
+        knot_factors()
         normalise(0, (0, 1, 2), "vector")
         normalise(0, (3,), "scalar")
         turn(0, 0)
-        sums_on_scalar(1, (1, 2, 3))
+        sums_on_scalar(1, (3,))
         scale_and_shift(0, 0)
         turn(0, 1)
+        knot_roots()
         knot_coefficients()
         mean_of_sums(1)
         blocks = [(h, c) for h in range(HALVES) for c in range(CHUNKS)]
@@ -440,7 +456,7 @@ def tile_kanlinear_pa_kernel(tc, x, ln_gamma, ln_beta, base_weight, base_bias, s
             if b == 1:
                 normalise(1, range(ROW_TILES), "scalar")
             emit_right(c, 2, cubes, rights[2])
-            share = LAST_SCALAR_COLS if last_block else VALUE_SCALAR_COLS[len(ready)]
+            share = LAST_SCALAR_COLS if last_block else VALUE_SCALAR_COLS
             for s, vh in ready:
                 regroup_values(s, vh, [("scalar", 0, share), ("vector", share, HALF)])
             for j in range(3, BASES):
@@ -457,6 +473,8 @@ def tile_kanlinear_pa_kernel(tc, x, ln_gamma, ln_beta, base_weight, base_bias, s
                     regroup_values(4, h, [("scalar", 0, HALF)])
             for s, vh in ready:
                 multiply(s, vh, values[(s, vh)])
+                if s == SPLINE_PASSES - 1:
+                    store(vh, range(ROW_TILES))
             for s in REGROUP_WEIGHTS[b]:
                 quantise_weight(s, weights[s])
             if b == 0:
@@ -466,7 +484,17 @@ def tile_kanlinear_pa_kernel(tc, x, ln_gamma, ln_beta, base_weight, base_bias, s
                 nc.vector.memset(gate[:], float(b))
                 nc.gpsimd.tensor_copy(out=passed[:], in_=gate[:])
             previous = (c, cubes, lefts)
-        larger_side(5)
+        parts = [slice(0, HALF // 2), slice(HALF // 2, HALF)]
+        for rows in parts:
+            larger_side(5, rows)
+        shares = []
+        for rows in parts:
+            cut = rows.start + TAIL_SCALAR_COLS
+            shares = shares + [("scalar", rows.start, cut), ("vector", cut, rows.stop)]
         multiply(4, 1, values[(4, 1)])
-        regroup_values(5, 1, [("scalar", 0, TAIL_SCALAR_COLS), ("vector", TAIL_SCALAR_COLS, HALF)])
-        multiply(5, 1, values[(5, 1)])
+        codes, scales = codes_and_scales()
+        regroup_values(5, 1, shares)
+        for rows in parts:
+            quantise_values(values[(5, 1)], codes, scales, rows)
+            accumulate(5, 1, codes, scales, range(rows.start // P, rows.stop // P))
+        store(1, range(ROW_TILES))

@@ -27,11 +27,14 @@ SPLINE_PASSES = PLANES // PACK
 BASE_PASS = SPLINE_PASSES
 LN_EPS = 0.001
 RUN = 4
-VALUE_SCALAR_COLS = 256
-LAST_SCALAR_COLS = 384
+VALUE_SCALAR_COLS = 272
+LAST_SCALAR_COLS = 448
 TAIL_SCALAR_COLS = 96
-GPSIMD_LEFTS = (0, 1, 2, 3, 4)
-COPIED_CUBES = (4, 5)
+INNER_RIGHTS = (2, 4, 0, 1)
+EARLY_RIGHTS = (3, 2, 5, 4)
+GPSIMD_LEFTS = (0, 1, 2, 3, 4, 5)
+COPIED_CUBES = (6, 8)
+PAIRED_RIGHTS = (3, 5)
 COMPLETE = [[0], [1, 2], [3], [4, 5]]
 REGROUP_WEIGHTS = [[0, 1, 2], [6, 3], [4], [5], [], [], [], []]
 
@@ -82,13 +85,13 @@ def tile_kanlinear_pa_kernel(tc, x, ln_gamma, ln_beta, base_weight, base_bias, s
         gamma = const.tile([P, CHUNKS], F32, name="gamma")
         beta = const.tile([P, CHUNKS], F32, name="beta")
         g = const.tile([P, CHUNKS, KNOTS], F32, name="g")
-        den = const.tile([P, CHUNKS, 23], F32, name="den")
-        inv = const.tile([P, CHUNKS, 23], F32, name="inv")
+        den = const.tile([P, CHUNKS, 25], F32, name="den")
+        inv = const.tile([P, CHUNKS, 25], F32, name="inv")
         sq_scale = const.tile([P, CHUNKS, KNOTS], F32, name="sq_scale")
         sq_bias = const.tile([P, CHUNKS, KNOTS], F32, name="sq_bias")
         l_inner = const.tile([P, CHUNKS, BASES], F32, name="l_inner")
         r_inner = const.tile([P, CHUNKS, BASES], F32, name="r_inner")
-        r_first = const.tile([P, CHUNKS, 3], F32, name="r_first")
+        r_first = const.tile([P, CHUNKS, 5], F32, name="r_first")
         factor = inv[:, :, 0:KNOTS]
         root_guess = const.tile([P, CHUNKS, KNOTS], F32, name="root_guess")
 
@@ -101,21 +104,25 @@ def tile_kanlinear_pa_kernel(tc, x, ln_gamma, ln_beta, base_weight, base_bias, s
             nc.gpsimd.tensor_copy(out=beta[:], in_=beta_bf[:])
             d2 = const.tile([P, CHUNKS, KNOTS - 2], F32, name="d2")
             d3 = const.tile([P, CHUNKS, KNOTS - 3], F32, name="d3")
-            nc.gpsimd.tensor_sub(out=den[:, :, 14:23], in0=g[:, :, 1:10], in1=g[:, :, 0:9])
+            nc.gpsimd.tensor_sub(out=den[:, :, 13:22], in0=g[:, :, 1:10], in1=g[:, :, 0:9])
             nc.gpsimd.tensor_sub(out=d2[:], in0=g[:, :, 2:10], in1=g[:, :, 0:8])
             nc.gpsimd.tensor_sub(out=d3[:], in0=g[:, :, 3:10], in1=g[:, :, 0:7])
             nc.gpsimd.tensor_sub(out=d4[:], in0=g[:, :, 4:10], in1=g[:, :, 0:6])
-            nc.gpsimd.tensor_sub(out=neg_d4[:], in0=g[:, :, 0:6], in1=g[:, :, 4:10])
+            nc.gpsimd.tensor_sub(out=den[:, :, 23:25], in0=g[:, :, 7:10:2], in1=g[:, :, 3:6:2])
             prod_a = const.tile([P, CHUNKS, 7], F32, name="prod_a")
             prod_b = const.tile([P, CHUNKS, 7], F32, name="prod_b")
-            nc.gpsimd.tensor_mul(out=prod_a[:], in0=den[:, :, 14:21], in1=d2[:, :, 0:7])
-            nc.gpsimd.tensor_mul(out=prod_b[:], in0=den[:, :, 16:23], in1=d2[:, :, 1:8])
-            nc.gpsimd.tensor_mul(out=den[:, :, 0:7], in0=prod_a[:], in1=d3[:])
-            nc.gpsimd.tensor_mul(out=den[:, :, 7:10], in0=prod_b[:, :, 4:7], in1=d3[:, :, 4:7])
-            nc.gpsimd.tensor_mul(out=den[:, :, 10:14], in0=prod_b[:, :, 0:4], in1=d3[:, :, 0:4])
+            nc.gpsimd.tensor_mul(out=prod_b[:], in0=den[:, :, 15:22], in1=d2[:, :, 1:8])
+            nc.gpsimd.tensor_mul(out=prod_b[:], in0=prod_b[:], in1=d3[:])
+            nc.gpsimd.tensor_mul(out=prod_a[:], in0=den[:, :, 13:20], in1=d2[:, :, 0:7])
+            nc.gpsimd.tensor_mul(out=den[:, :, 0:6], in0=prod_a[:, :, 0:6], in1=d3[:, :, 0:6])
+            nc.gpsimd.tensor_mul(out=den[:, :, 6:9:2], in0=prod_b[:, :, 3:6:2], in1=den[:, :, 19:22:2])
+            nc.gpsimd.tensor_copy(out=den[:, :, 7:10:2], in_=prod_b[:, :, 4:7:2])
+            nc.gpsimd.tensor_copy(out=den[:, :, 10:13], in_=prod_b[:, :, 0:3])
+            nc.gpsimd.tensor_mul(out=den[:, :, 22:23], in0=prod_a[:, :, 6:7], in1=d3[:, :, 6:7])
 
         def knot_factors():
             nc.vector.reciprocal(out=inv[:], in_=den[:])
+            nc.vector.tensor_mul(out=inv[:, :, 6:9:2], in0=inv[:, :, 6:9:2], in1=d4[:, :, 3:6:2])
             nc.scalar.activation(out=root_guess[:], in_=factor, func=ACT.Sqrt)
 
         def knot_roots():
@@ -133,12 +140,19 @@ def tile_kanlinear_pa_kernel(tc, x, ln_gamma, ln_beta, base_weight, base_bias, s
             )
 
         def knot_coefficients():
-            ratio = const.tile([P, CHUNKS, 4], F32, name="ratio")
-            nc.gpsimd.tensor_mul(out=ratio[:], in0=inv[:, :, 10:14], in1=den[:, :, 3:7])
-            nc.gpsimd.tensor_mul(out=l_inner[:], in0=d4[:], in1=inv[:, :, 14:20])
-            nc.gpsimd.tensor_mul(out=r_inner[:], in0=neg_d4[:], in1=inv[:, :, 17:23])
-            nc.gpsimd.tensor_scalar_mul(out=r_first[:], in0=ratio[:, :, 1:4], scalar1=-1.0)
-            nc.gpsimd.tensor_mul(out=r_inner[:, :, 0:4], in0=r_inner[:, :, 0:4], in1=ratio[:])
+            ratio = const.tile([P, CHUNKS, 3], F32, name="ratio")
+            nc.gpsimd.tensor_mul(out=ratio[:], in0=inv[:, :, 10:13], in1=den[:, :, 3:6])
+            nc.gpsimd.tensor_sub(out=neg_d4[:], in0=g[:, :, 0:6], in1=g[:, :, 4:10])
+            nc.gpsimd.tensor_mul(out=r_inner[:], in0=neg_d4[:], in1=inv[:, :, 16:22])
+            nc.gpsimd.tensor_mul(out=r_inner[:, :, 0:3], in0=r_inner[:, :, 0:3], in1=ratio[:])
+            nc.gpsimd.tensor_scalar_mul(out=r_first[:, :, 0:2], in0=ratio[:, :, 1:3], scalar1=-1.0)
+            nc.gpsimd.tensor_mul(out=r_first[:, :, 2:5:2], in0=den[:, :, 19:22:2], in1=inv[:, :, 23:25])
+            nc.gpsimd.tensor_scalar_mul(out=r_first[:, :, 2:5:2], in0=r_first[:, :, 2:5:2], scalar1=-1.0)
+            nc.gpsimd.tensor_mul(out=l_inner[:], in0=d4[:], in1=inv[:, :, 13:19])
+            to_a6 = const.tile([P, CHUNKS, 1], F32, name="to_a6")
+            nc.gpsimd.tensor_mul(out=to_a6[:], in0=den[:, :, 6:7], in1=inv[:, :, 22:23])
+            nc.gpsimd.tensor_mul(out=to_a6[:], in0=to_a6[:], in1=inv[:, :, 23:24])
+            nc.gpsimd.tensor_mul(out=l_inner[:, :, 5:6], in0=l_inner[:, :, 5:6], in1=to_a6[:])
 
         xn = keep.tile([P, HALVES, CHUNKS, HALF], F32, name="xn")
         neg_mean = keep.tile([P, HALVES, ROW_TILES], F32, name="neg_mean")
@@ -370,29 +384,38 @@ def tile_kanlinear_pa_kernel(tc, x, ln_gamma, ln_beta, base_weight, base_bias, s
             return inner
 
         def emit_inner_right(c, j, cubes):
-            inner = work.tile([P, HALF], F32, name="inner_r", bufs=BASES)
+            inner = work.tile([P, HALF], F32, name="inner_r", bufs=4)
             nc.scalar.activation(out=inner[:], in_=cubes[j + 3][:], func=ACT.Relu, scale=r_inner[:, c, j : j + 1])
             return inner
+
+        def open_sides(c):
+            for s in range(SPLINE_PASSES):
+                if s * PACK // BASES == c:
+                    left4 = work.tile([P, PACK, HALF], BF16, name="left4", bufs=4)
+                    right4 = work.tile([P, PACK, HALF], BF16, name="right4", bufs=4)
+                    sides[s] = (left4, right4)
 
         def side_slot(c, j, side):
             q = c * BASES + j
             s = q // PACK
-            if side == 1 and q % PACK == 0:
-                left4 = work.tile([P, PACK, HALF], BF16, name="left4", bufs=4)
-                right4 = work.tile([P, PACK, HALF], BF16, name="right4", bufs=4)
-                sides[s] = (left4, right4)
             return sides[s][side][:, q % PACK, :]
 
         def emit_left(c, j, cubes, inner, engine):
             first = cubes[j] if engine is nc.gpsimd or j not in cube_banks else cube_banks[j]
             engine.tensor_sub(out=side_slot(c, j, 0), in0=first[:], in1=inner[:])
 
-        def emit_right(c, j, cubes, inner):
+        def emit_right(c, j, cubes, inners):
+            if j in PAIRED_RIGHTS:
+                inner_cube = cube_banks[j + 3] if j + 3 in cube_banks else cubes[j + 3]
+                nc.vector.scalar_tensor_tensor(
+                    out=side_slot(c, j, 1), in0=inner_cube[:], scalar=0.0, in1=cubes[j + 4][:], op0=ALU.min, op1=ALU.subtract
+                )
+                return
             nc.vector.scalar_tensor_tensor(
                 out=side_slot(c, j, 1),
                 in0=cube_banks[j + 4][:] if j + 4 in cube_banks else cubes[j + 4][:],
-                scalar=r_first[:, c, j : j + 1] if j < 3 else -1.0,
-                in1=inner[:],
+                scalar=r_first[:, c, j : j + 1],
+                in1=inners[j][:],
                 op0=ALU.mult,
                 op1=ALU.subtract,
             )
@@ -418,6 +441,14 @@ def tile_kanlinear_pa_kernel(tc, x, ln_gamma, ln_beta, base_weight, base_bias, s
         emit_squares(0, 0, range(KNOTS), squares)
         gate = const.tile([P, 1], F32, name="gate")
         passed = const.tile([P, 1], F32, name="passed")
+        pending = []
+
+        def multiply_all(passes):
+            for s, vh in passes:
+                multiply(s, vh, values[(s, vh)])
+                if s == SPLINE_PASSES - 1:
+                    store(vh, range(ROW_TILES))
+
         previous = None
         for b in range(len(blocks)):
             h, c = blocks[b]
@@ -433,21 +464,24 @@ def tile_kanlinear_pa_kernel(tc, x, ln_gamma, ln_beta, base_weight, base_bias, s
                     ready.append((BASE_PASS, blocks[b - 1][0]))
             if not last_block:
                 scale_and_shift(*blocks[b + 1])
+            open_sides(c)
             cubes = emit_cubes(h, c, squares)
             if not last_block:
                 copy_to_psum(*blocks[b + 1])
             if b + 2 < len(blocks):
                 turn(*blocks[b + 2])
-            rights = [emit_inner_right(c, j, cubes) for j in range(2)]
-            emit_right(c, 0, cubes, rights[0])
-            emit_right(c, 1, cubes, rights[1])
-            rights = rights + [emit_inner_right(c, j, cubes) for j in range(2, BASES)]
+            rights = {}
+            for j in INNER_RIGHTS:
+                rights[j] = emit_inner_right(c, j, cubes)
+            for j in EARLY_RIGHTS:
+                emit_right(c, j, cubes, rights)
             lefts = {}
             for j in [j for j in range(BASES) if j not in lefts_by_gpsimd] + list(lefts_by_gpsimd):
                 lefts[j] = emit_inner_left(c, j, cubes)
             for s, vh in ready:
                 if s != BASE_PASS:
                     larger_side(s)
+            multiply_all(pending)
             if b == 1:
                 reciprocal_root(1)
             squares = []
@@ -455,12 +489,11 @@ def tile_kanlinear_pa_kernel(tc, x, ln_gamma, ln_beta, base_weight, base_bias, s
                 deviations_on_scalar(1, range(ROW_TILES))
             if b == 1:
                 normalise(1, range(ROW_TILES), "scalar")
-            emit_right(c, 2, cubes, rights[2])
+            emit_right(c, 0, cubes, rights)
             share = LAST_SCALAR_COLS if last_block else VALUE_SCALAR_COLS
             for s, vh in ready:
                 regroup_values(s, vh, [("scalar", 0, share), ("vector", share, HALF)])
-            for j in range(3, BASES):
-                emit_right(c, j, cubes, rights[j])
+            emit_right(c, 1, cubes, rights)
             if not last_block:
                 emit_squares(*blocks[b + 1], range(KNOTS), squares)
             for s in REGROUP_WEIGHTS[b]:
@@ -471,10 +504,9 @@ def tile_kanlinear_pa_kernel(tc, x, ln_gamma, ln_beta, base_weight, base_bias, s
                 if last_block and j == 1:
                     larger_side(4)
                     regroup_values(4, h, [("scalar", 0, HALF)])
-            for s, vh in ready:
-                multiply(s, vh, values[(s, vh)])
-                if s == SPLINE_PASSES - 1:
-                    store(vh, range(ROW_TILES))
+            if last_block:
+                multiply_all(ready)
+            pending = ready
             for s in REGROUP_WEIGHTS[b]:
                 quantise_weight(s, weights[s])
             if b == 0:

@@ -27,16 +27,18 @@ SPLINE_PASSES = PLANES // PACK
 BASE_PASS = SPLINE_PASSES
 LN_EPS = 0.001
 RUN = 4
-VALUE_SCALAR_COLS = 272
-LAST_SCALAR_COLS = 448
+VALUE_SCALAR_COLS = 256
+LAST_SCALAR_COLS = HALF
 TAIL_SCALAR_COLS = 96
-INNER_RIGHTS = (2, 4, 0, 1)
-EARLY_RIGHTS = (3, 2, 5, 4)
-GPSIMD_LEFTS = (0, 1, 2, 3, 4, 5)
+CUBE_ORDER = (6, 8, 7, 5, 9, 4, 3, 2, 1, 0)
+INNER_TERMS = (("right", 4), ("right", 2), ("left", 5), ("left", 4), ("right", 1), ("right", 0), ("left", 3), ("left", 2), ("left", 1), ("left", 0))
+LAST_INNER_TERMS = (("right", 4), ("right", 2), ("left", 5), ("left", 4), ("right", 1), ("right", 0), ("left", 1), ("left", 0), ("left", 3), ("left", 2))
+EARLY_RIGHTS = (3, 5, 2, 4)
+GPSIMD_LEFTS = (5, 4, 3, 2, 1, 0)
 COPIED_CUBES = (6, 8)
 PAIRED_RIGHTS = (3, 5)
 COMPLETE = [[0], [1, 2], [3], [4, 5]]
-REGROUP_WEIGHTS = [[0, 1, 2], [6, 3], [4], [5], [], [], [], []]
+REGROUP_WEIGHTS = [[0, 1, 2], [3, 6], [4], [5], [], [], [], []]
 
 FLOPS = 2 * ROWS * (FEATURES + FEATURES * BASES) * UNITS
 
@@ -80,84 +82,85 @@ def tile_kanlinear_pa_kernel(tc, x, ln_gamma, ln_beta, base_weight, base_bias, s
         one = const.tile([P, 1], F32, name="one")
         nc.vector.memset(one[:], 1.0)
         warm = const.tile([P, 1], F32, name="warm")
-        nc.scalar.activation(out=warm[:], in_=one[:], func=ACT.Sqrt)
+        nc.scalar.activation(out=warm[:], in_=one[:], func=ACT.Abs_reciprocal_sqrt)
 
         gamma = const.tile([P, CHUNKS], F32, name="gamma")
         beta = const.tile([P, CHUNKS], F32, name="beta")
         g = const.tile([P, CHUNKS, KNOTS], F32, name="g")
-        den = const.tile([P, CHUNKS, 25], F32, name="den")
-        inv = const.tile([P, CHUNKS, 25], F32, name="inv")
+        cube_den = const.tile([P, CHUNKS, KNOTS], F32, name="cube_den")
+        root = const.tile([P, CHUNKS, KNOTS], F32, name="root")
+        root_corr = const.tile([P, CHUNKS, KNOTS], F32, name="root_corr")
         sq_scale = const.tile([P, CHUNKS, KNOTS], F32, name="sq_scale")
         sq_bias = const.tile([P, CHUNKS, KNOTS], F32, name="sq_bias")
+        rest = const.tile([P, CHUNKS, 13], F32, name="rest")
+        inv = const.tile([P, CHUNKS, 13], F32, name="inv")
+        d2 = const.tile([P, CHUNKS, KNOTS - 2], F32, name="d2")
+        d3 = const.tile([P, CHUNKS, KNOTS - 3], F32, name="d3")
+        d4 = const.tile([P, CHUNKS, KNOTS - 4], F32, name="d4")
+        neg_d4 = const.tile([P, CHUNKS, KNOTS - 4], F32, name="neg_d4")
+        inv_d4 = const.tile([P, CHUNKS, 2], F32, name="inv_d4")
+        d1_by_d4 = const.tile([P, CHUNKS, 2], F32, name="d1_by_d4")
+        d1d2 = const.tile([P, CHUNKS, 7], F32, name="d1d2")
+        d1d2_b = const.tile([P, CHUNKS, 7], F32, name="d1d2_b")
+        b_paired = const.tile([P, CHUNKS, 2], F32, name="b_paired")
         l_inner = const.tile([P, CHUNKS, BASES], F32, name="l_inner")
         r_inner = const.tile([P, CHUNKS, BASES], F32, name="r_inner")
         r_first = const.tile([P, CHUNKS, 5], F32, name="r_first")
-        factor = inv[:, :, 0:KNOTS]
-        root_guess = const.tile([P, CHUNKS, KNOTS], F32, name="root_guess")
-
-        d4 = const.tile([P, CHUNKS, KNOTS - 4], F32, name="d4")
-        neg_d4 = const.tile([P, CHUNKS, KNOTS - 4], F32, name="neg_d4")
+        d1 = rest[:, :, 0:9]
 
         def knot_differences():
             nc.gpsimd.tensor_copy(out=g[:], in_=grid_bf[:])
-            nc.gpsimd.tensor_copy(out=gamma[:], in_=gamma_bf[:])
-            nc.gpsimd.tensor_copy(out=beta[:], in_=beta_bf[:])
-            d2 = const.tile([P, CHUNKS, KNOTS - 2], F32, name="d2")
-            d3 = const.tile([P, CHUNKS, KNOTS - 3], F32, name="d3")
-            nc.gpsimd.tensor_sub(out=den[:, :, 13:22], in0=g[:, :, 1:10], in1=g[:, :, 0:9])
+            nc.gpsimd.tensor_sub(out=d4[:], in0=g[:, :, 4:10], in1=g[:, :, 0:6])
+
+        def knot_products():
+            nc.gpsimd.tensor_sub(out=d1, in0=g[:, :, 1:10], in1=g[:, :, 0:9])
             nc.gpsimd.tensor_sub(out=d2[:], in0=g[:, :, 2:10], in1=g[:, :, 0:8])
             nc.gpsimd.tensor_sub(out=d3[:], in0=g[:, :, 3:10], in1=g[:, :, 0:7])
-            nc.gpsimd.tensor_sub(out=d4[:], in0=g[:, :, 4:10], in1=g[:, :, 0:6])
-            nc.gpsimd.tensor_sub(out=den[:, :, 23:25], in0=g[:, :, 7:10:2], in1=g[:, :, 3:6:2])
-            prod_a = const.tile([P, CHUNKS, 7], F32, name="prod_a")
-            prod_b = const.tile([P, CHUNKS, 7], F32, name="prod_b")
-            nc.gpsimd.tensor_mul(out=prod_b[:], in0=den[:, :, 15:22], in1=d2[:, :, 1:8])
-            nc.gpsimd.tensor_mul(out=prod_b[:], in0=prod_b[:], in1=d3[:])
-            nc.gpsimd.tensor_mul(out=prod_a[:], in0=den[:, :, 13:20], in1=d2[:, :, 0:7])
-            nc.gpsimd.tensor_mul(out=den[:, :, 0:6], in0=prod_a[:, :, 0:6], in1=d3[:, :, 0:6])
-            nc.gpsimd.tensor_mul(out=den[:, :, 6:9:2], in0=prod_b[:, :, 3:6:2], in1=den[:, :, 19:22:2])
-            nc.gpsimd.tensor_copy(out=den[:, :, 7:10:2], in_=prod_b[:, :, 4:7:2])
-            nc.gpsimd.tensor_copy(out=den[:, :, 10:13], in_=prod_b[:, :, 0:3])
-            nc.gpsimd.tensor_mul(out=den[:, :, 22:23], in0=prod_a[:, :, 6:7], in1=d3[:, :, 6:7])
+            nc.gpsimd.tensor_mul(out=d1d2_b[:], in0=d1[:, :, 2:9], in1=d2[:, :, 1:8])
+            nc.gpsimd.tensor_mul(out=d1d2[:], in0=d1[:, :, 0:7], in1=d2[:, :, 0:7])
+            nc.gpsimd.tensor_mul(out=cube_den[:, :, 0:6], in0=d1d2[:, :, 0:6], in1=d3[:, :, 0:6])
+            nc.gpsimd.tensor_mul(out=cube_den[:, :, 7:10:2], in0=d1d2_b[:, :, 4:7:2], in1=d3[:, :, 4:7:2])
+            nc.gpsimd.tensor_mul(out=b_paired[:], in0=d1d2_b[:, :, 3:6:2], in1=d3[:, :, 3:6:2])
+            nc.gpsimd.tensor_mul(out=d1_by_d4[:], in0=d1[:, :, 6:9:2], in1=inv_d4[:])
+            nc.gpsimd.tensor_mul(out=cube_den[:, :, 6:9:2], in0=b_paired[:], in1=d1_by_d4[:])
+            nc.gpsimd.tensor_copy(out=gamma[:], in_=gamma_bf[:])
+            nc.gpsimd.tensor_copy(out=beta[:], in_=beta_bf[:])
+            nc.gpsimd.tensor_mul(out=rest[:, :, 9:12], in0=d1d2_b[:, :, 0:3], in1=d3[:, :, 0:3])
+            nc.gpsimd.tensor_mul(out=rest[:, :, 12:13], in0=d1d2[:, :, 6:7], in1=d3[:, :, 6:7])
+            nc.gpsimd.tensor_sub(out=neg_d4[:], in0=g[:, :, 0:6], in1=g[:, :, 4:10])
 
         def knot_factors():
-            nc.vector.reciprocal(out=inv[:], in_=den[:])
-            nc.vector.tensor_mul(out=inv[:, :, 6:9:2], in0=inv[:, :, 6:9:2], in1=d4[:, :, 3:6:2])
-            nc.scalar.activation(out=root_guess[:], in_=factor, func=ACT.Sqrt)
+            nc.scalar.activation(out=root[:], in_=cube_den[:], func=ACT.Abs_reciprocal_sqrt)
 
         def knot_roots():
-            quotient = const.tile([P, CHUNKS, KNOTS], F32, name="quotient")
-            inv_guess = const.tile([P, CHUNKS, KNOTS], F32, name="inv_guess")
-            nc.vector.reciprocal(out=inv_guess[:], in_=root_guess[:])
+            nc.vector.tensor_mul(out=root_corr[:], in0=root[:], in1=root[:])
             nc.vector.scalar_tensor_tensor(
-                out=quotient[:], in0=factor, scalar=0.5, in1=inv_guess[:], op0=ALU.mult, op1=ALU.mult
+                out=root_corr[:], in0=root_corr[:], scalar=-0.5, in1=cube_den[:], op0=ALU.mult, op1=ALU.mult
             )
             nc.vector.scalar_tensor_tensor(
-                out=sq_scale[:], in0=root_guess[:], scalar=0.5, in1=quotient[:], op0=ALU.mult, op1=ALU.add
+                out=sq_scale[:], in0=root_corr[:], scalar=1.5, in1=root[:], op0=ALU.add, op1=ALU.mult
             )
             nc.vector.scalar_tensor_tensor(
                 out=sq_bias[:], in0=g[:], scalar=-1.0, in1=sq_scale[:], op0=ALU.mult, op1=ALU.mult
             )
 
         def knot_coefficients():
+            nc.vector.reciprocal(out=inv[:], in_=rest[:])
             ratio = const.tile([P, CHUNKS, 3], F32, name="ratio")
-            nc.gpsimd.tensor_mul(out=ratio[:], in0=inv[:, :, 10:13], in1=den[:, :, 3:6])
-            nc.gpsimd.tensor_sub(out=neg_d4[:], in0=g[:, :, 0:6], in1=g[:, :, 4:10])
-            nc.gpsimd.tensor_mul(out=r_inner[:], in0=neg_d4[:], in1=inv[:, :, 16:22])
+            nc.gpsimd.tensor_mul(out=ratio[:], in0=inv[:, :, 9:12], in1=cube_den[:, :, 3:6])
+            nc.gpsimd.tensor_mul(out=r_inner[:], in0=neg_d4[:], in1=inv[:, :, 3:9])
             nc.gpsimd.tensor_mul(out=r_inner[:, :, 0:3], in0=r_inner[:, :, 0:3], in1=ratio[:])
             nc.gpsimd.tensor_scalar_mul(out=r_first[:, :, 0:2], in0=ratio[:, :, 1:3], scalar1=-1.0)
-            nc.gpsimd.tensor_mul(out=r_first[:, :, 2:5:2], in0=den[:, :, 19:22:2], in1=inv[:, :, 23:25])
-            nc.gpsimd.tensor_scalar_mul(out=r_first[:, :, 2:5:2], in0=r_first[:, :, 2:5:2], scalar1=-1.0)
-            nc.gpsimd.tensor_mul(out=l_inner[:], in0=d4[:], in1=inv[:, :, 13:19])
+            nc.gpsimd.tensor_scalar_mul(out=r_first[:, :, 2:5:2], in0=d1_by_d4[:], scalar1=-1.0)
+            nc.gpsimd.tensor_mul(out=l_inner[:], in0=d4[:], in1=inv[:, :, 0:6])
             to_a6 = const.tile([P, CHUNKS, 1], F32, name="to_a6")
-            nc.gpsimd.tensor_mul(out=to_a6[:], in0=den[:, :, 6:7], in1=inv[:, :, 22:23])
-            nc.gpsimd.tensor_mul(out=to_a6[:], in0=to_a6[:], in1=inv[:, :, 23:24])
+            nc.gpsimd.tensor_mul(out=to_a6[:], in0=cube_den[:, :, 6:7], in1=inv[:, :, 12:13])
             nc.gpsimd.tensor_mul(out=l_inner[:, :, 5:6], in0=l_inner[:, :, 5:6], in1=to_a6[:])
 
         xn = keep.tile([P, HALVES, CHUNKS, HALF], F32, name="xn")
         neg_mean = keep.tile([P, HALVES, ROW_TILES], F32, name="neg_mean")
         var_eps = keep.tile([P, HALVES, ROW_TILES], F32, name="var_eps")
-        std = keep.tile([P, HALVES, ROW_TILES], F32, name="std")
+        rstd_guess = keep.tile([P, HALVES, ROW_TILES], F32, name="rstd_guess")
         rstd = keep.tile([P, HALVES, ROW_TILES], F32, name="rstd")
         shift = keep.tile([P, HALVES, ROW_TILES], F32, name="shift")
         z_tiles = {}
@@ -171,6 +174,7 @@ def tile_kanlinear_pa_kernel(tc, x, ln_gamma, ln_beta, base_weight, base_bias, s
                 nc.vector.bn_aggr(out=mean_var[:, t, :], in_=stats[:, t, :])
             nc.vector.tensor_scalar_add(out=var_eps[:, h, :], in0=mean_var[:, :, 1], scalar1=LN_EPS)
             nc.vector.tensor_scalar_mul(out=neg_mean[:, h, :], in0=mean_var[:, :, 0], scalar1=-1.0)
+            nc.vector.reciprocal(out=inv_d4[:], in_=d4[:, :, 3:6:2])
 
         sums = keep.tile([P, 2, ROW_TILES], F32, name="sums")
 
@@ -200,19 +204,18 @@ def tile_kanlinear_pa_kernel(tc, x, ln_gamma, ln_beta, base_weight, base_bias, s
                 out=var_eps[:, h, :], in0=sums[:, 1, :], scalar1=1.0 / FEATURES, scalar2=LN_EPS, op0=ALU.mult, op1=ALU.add
             )
 
-        def root(h):
-            nc.scalar.activation(out=std[:, h, :], in_=var_eps[:, h, :], func=ACT.Sqrt)
+        def row_root(h):
+            nc.scalar.activation(out=rstd_guess[:, h, :], in_=var_eps[:, h, :], func=ACT.Abs_reciprocal_sqrt)
 
         def reciprocal_root(h):
-            guess = work.tile([P, ROW_TILES], F32, name="guess")
-            nc.vector.reciprocal(out=guess[:], in_=std[:, h, :])
+            guess = rstd_guess[:, h, :]
             corr = work.tile([P, ROW_TILES], F32, name="corr")
-            nc.vector.tensor_mul(out=corr[:], in0=guess[:], in1=guess[:])
+            nc.vector.tensor_mul(out=corr[:], in0=guess, in1=guess)
             nc.vector.scalar_tensor_tensor(
                 out=corr[:], in0=corr[:], scalar=-0.5, in1=var_eps[:, h, :], op0=ALU.mult, op1=ALU.mult
             )
             nc.vector.scalar_tensor_tensor(
-                out=rstd[:, h, :], in0=corr[:], scalar=1.5, in1=guess[:], op0=ALU.add, op1=ALU.mult
+                out=rstd[:, h, :], in0=corr[:], scalar=1.5, in1=guess, op0=ALU.add, op1=ALU.mult
             )
             nc.vector.tensor_mul(out=shift[:, h, :], in0=neg_mean[:, h, :], in1=rstd[:, h, :])
 
@@ -262,15 +265,21 @@ def tile_kanlinear_pa_kernel(tc, x, ln_gamma, ln_beta, base_weight, base_bias, s
             nc.tensor.matmul(v[:], lhsT=ident[:], rhs=xn[:, h, c, :], start=True, stop=True)
             v_banks[(h, c)] = v
 
-        def regroup(planes, relu, shares):
-            grouped = work.tile([P, HALF, PACK], BF16, name="grouped", align_bytes=64, bufs=5)
-            dst_all = grouped[:].rearrange("p (c i) t -> p c t i", i=RUN)
-            src_all = planes.rearrange("p t (c i) -> p c t i", i=RUN)
+        def in_runs(planes, col0, col1):
+            return planes[:, :, col0:col1].rearrange("p t (c i) -> p c t i", i=RUN)
+
+        def words(grouped, col0, col1):
+            return grouped[:, col0:col1, :].rearrange("p (c i) t -> p c t i", i=RUN)
+
+        def new_grouped():
+            return work.tile([P, HALF, PACK], BF16, name="grouped", align_bytes=64, bufs=5)
+
+        def regroup(grouped, planes, relu, shares):
             for engine, col0, col1 in shares:
                 if col0 == col1:
                     continue
-                dst = dst_all[:, col0 // RUN : col1 // RUN]
-                src = src_all[:, col0 // RUN : col1 // RUN]
+                dst = words(grouped, col0, col1)
+                src = in_runs(planes, col0, col1)
                 if engine == "vector" and relu:
                     nc.vector.tensor_scalar_max(out=dst, in0=src, scalar1=0.0)
                 elif engine == "vector":
@@ -279,7 +288,6 @@ def tile_kanlinear_pa_kernel(tc, x, ln_gamma, ln_beta, base_weight, base_bias, s
                     nc.scalar.activation(out=dst, in_=src, func=ACT.Relu)
                 else:
                     nc.scalar.copy(out=dst, in_=src)
-            return grouped
 
         w_codes = keep.tile([P, SPLINE_PASSES + 1, UNITS], U32, name="w_codes", align_bytes=64)
         w_scales = keep.tile([P, SPLINE_PASSES + 1, UNITS], U8, name="w_scales", align_bytes=64)
@@ -336,17 +344,20 @@ def tile_kanlinear_pa_kernel(tc, x, ln_gamma, ln_beta, base_weight, base_bias, s
         weights = {}
 
         def regroup_weight(s, shares):
-            weights[s] = regroup(raw[:, s * PACK : (s + 1) * PACK, :], False, shares)
+            weights[s] = new_grouped()
+            regroup(weights[s], raw[:, s * PACK : (s + 1) * PACK, :], False, shares)
 
         def regroup_values(s, h, shares):
+            if (s, h) not in values:
+                values[(s, h)] = new_grouped()
             planes = xn[:, h] if s == BASE_PASS else sides[s][0][:]
-            values[(s, h)] = regroup(planes, True, shares)
+            regroup(values[(s, h)], planes, True, shares)
 
         def larger_side(s, cols=slice(0, HALF)):
             nc.vector.tensor_max(out=sides[s][0][:, :, cols], in0=sides[s][0][:, :, cols], in1=sides[s][1][:, :, cols])
 
-        def emit_squares(h, c, knots, squares):
-            for i in knots:
+        def emit_squares(h, c, squares):
+            for i in CUBE_ORDER:
                 square = work.tile([P, HALF], F32, name="square", bufs=KNOTS)
                 nc.scalar.activation(
                     out=square[:],
@@ -355,13 +366,13 @@ def tile_kanlinear_pa_kernel(tc, x, ln_gamma, ln_beta, base_weight, base_bias, s
                     scale=sq_scale[:, c, i : i + 1],
                     bias=sq_bias[:, c, i : i + 1],
                 )
-                squares.append(square)
+                squares[i] = square
 
         cube_banks = {}
 
         def emit_cubes(h, c, squares):
-            cubes = []
-            for i in range(KNOTS):
+            cubes = {}
+            for i in CUBE_ORDER:
                 cube = work.tile([P, HALF], F32, name="cube", bufs=2 * KNOTS)
                 nc.vector.scalar_tensor_tensor(
                     out=cube[:],
@@ -371,7 +382,7 @@ def tile_kanlinear_pa_kernel(tc, x, ln_gamma, ln_beta, base_weight, base_bias, s
                     op0=ALU.subtract,
                     op1=ALU.mult,
                 )
-                cubes.append(cube)
+                cubes[i] = cube
                 if (h, c) != (0, 0) and i in COPIED_CUBES:
                     copy = psum.tile([P, HALF], F32, name="copy", tag="cube%d" % i)
                     nc.tensor.matmul(copy[:], lhsT=ident[:], rhs=cube[:], start=True, stop=True)
@@ -422,23 +433,23 @@ def tile_kanlinear_pa_kernel(tc, x, ln_gamma, ln_beta, base_weight, base_bias, s
 
         knot_differences()
         moments_on_vector(0)
+        knot_products()
         sums_on_scalar(1, (0,))
-        root(0)
-        sums_on_scalar(1, (1, 2))
+        row_root(0)
+        sums_on_scalar(1, (1,))
         reciprocal_root(0)
-        knot_factors()
         normalise(0, (0, 1, 2), "vector")
+        knot_factors()
         normalise(0, (3,), "scalar")
         turn(0, 0)
-        sums_on_scalar(1, (3,))
+        knot_roots()
         scale_and_shift(0, 0)
         turn(0, 1)
-        knot_roots()
         knot_coefficients()
-        mean_of_sums(1)
         blocks = [(h, c) for h in range(HALVES) for c in range(CHUNKS)]
-        squares = []
-        emit_squares(0, 0, range(KNOTS), squares)
+        squares = {}
+        emit_squares(0, 0, squares)
+        sums_on_scalar(1, (2, 3))
         gate = const.tile([P, 1], F32, name="gate")
         passed = const.tile([P, 1], F32, name="passed")
         pending = []
@@ -446,8 +457,6 @@ def tile_kanlinear_pa_kernel(tc, x, ln_gamma, ln_beta, base_weight, base_bias, s
         def multiply_all(passes):
             for s, vh in passes:
                 multiply(s, vh, values[(s, vh)])
-                if s == SPLINE_PASSES - 1:
-                    store(vh, range(ROW_TILES))
 
         previous = None
         for b in range(len(blocks)):
@@ -471,20 +480,23 @@ def tile_kanlinear_pa_kernel(tc, x, ln_gamma, ln_beta, base_weight, base_bias, s
             if b + 2 < len(blocks):
                 turn(*blocks[b + 2])
             rights = {}
-            for j in INNER_RIGHTS:
-                rights[j] = emit_inner_right(c, j, cubes)
+            lefts = {}
+            for side, j in LAST_INNER_TERMS if last_block else INNER_TERMS:
+                if side == "right":
+                    rights[j] = emit_inner_right(c, j, cubes)
+                else:
+                    lefts[j] = emit_inner_left(c, j, cubes)
             for j in EARLY_RIGHTS:
                 emit_right(c, j, cubes, rights)
-            lefts = {}
-            for j in [j for j in range(BASES) if j not in lefts_by_gpsimd] + list(lefts_by_gpsimd):
-                lefts[j] = emit_inner_left(c, j, cubes)
             for s, vh in ready:
                 if s != BASE_PASS:
                     larger_side(s)
             multiply_all(pending)
+            if b == 0:
+                mean_of_sums(1)
             if b == 1:
                 reciprocal_root(1)
-            squares = []
+            squares = {}
             if b == 0:
                 deviations_on_scalar(1, range(ROW_TILES))
             if b == 1:
@@ -495,7 +507,7 @@ def tile_kanlinear_pa_kernel(tc, x, ln_gamma, ln_beta, base_weight, base_bias, s
                 regroup_values(s, vh, [("scalar", 0, share), ("vector", share, HALF)])
             emit_right(c, 1, cubes, rights)
             if not last_block:
-                emit_squares(*blocks[b + 1], range(KNOTS), squares)
+                emit_squares(*blocks[b + 1], squares)
             for s in REGROUP_WEIGHTS[b]:
                 regroup_weight(s, [("vector", 0, UNITS)])
             for j in range(BASES):
@@ -511,7 +523,9 @@ def tile_kanlinear_pa_kernel(tc, x, ln_gamma, ln_beta, base_weight, base_bias, s
                 quantise_weight(s, weights[s])
             if b == 0:
                 variance_of_sums(1)
-                root(1)
+                row_root(1)
+            if b == CHUNKS + 1:
+                store(0, range(ROW_TILES))
             if not last_block:
                 nc.vector.memset(gate[:], float(b))
                 nc.gpsimd.tensor_copy(out=passed[:], in_=gate[:])

@@ -27,19 +27,22 @@ SPLINE_PASSES = PLANES // PACK
 BASE_PASS = SPLINE_PASSES
 LN_EPS = 0.001
 RUN = 4
-VALUE_SCALAR_COLS = 256
-LAST_SCALAR_COLS = HALF
 TAIL_SCALAR_COLS = 96
 CUBE_ORDER = (6, 8, 7, 5, 9, 4, 3, 2, 1, 0)
 INNER_TERMS = (("right", 4), ("right", 2), ("left", 5), ("left", 4), ("right", 1), ("right", 0), ("left", 3), ("left", 2), ("left", 1), ("left", 0))
-LAST_INNER_TERMS = (("right", 4), ("right", 2), ("left", 5), ("left", 4), ("right", 1), ("right", 0), ("left", 1), ("left", 0), ("left", 3), ("left", 2))
+LAST_INNER_TERMS = (("left", 5), ("left", 4), ("right", 4), ("right", 2), ("right", 1), ("right", 0), ("left", 1), ("left", 0), ("left", 3), ("left", 2))
 EARLY_RIGHTS = (3, 5, 2, 4)
-GPSIMD_LEFTS = (5, 4, 3, 2, 1, 0)
+GPSIMD_PAIRS = (2, 1, 0)
 COPIED_CUBES = (6, 8)
 PAIRED_RIGHTS = (3, 5)
 COMPLETE = [[0], [1, 2], [3], [4, 5]]
-REGROUP_WEIGHTS = [[0, 1, 2], [3, 6], [4], [5], [], [], [], []]
+REGROUP_WEIGHTS = [[0], [2, 3], [6, 4], [5], [], [], [], []]
 
+SHARE = (0, 192, 192, 256, 256, 256, 256, 512)
+FIRST_CUBES = 2
+GPSIMD_WEIGHTS = (1,)
+OWN_PAIRS = ((), (), (), (), (), (), (2,), (2,))
+PROD_AT = (0, 1, 2, 3, 4, 5, 14, 11, 15, 13)
 FLOPS = 2 * ROWS * (FEATURES + FEATURES * BASES) * UNITS
 
 
@@ -52,6 +55,8 @@ def tile_kanlinear_pa_kernel(tc, x, ln_gamma, ln_beta, base_weight, base_bias, s
         psum = ctx.enter_context(tc.psum_pool(name="psum", bufs=1))
         ctx.enter_context(tc.manual_schedule())
 
+        grid_bf = const.tile([P, CHUNKS, KNOTS], BF16, name="grid_bf")
+        nc.sync.dma_start(out=grid_bf[:], in_=grid.rearrange("o (c p) t -> p (o c) t", p=P))
         x_bf = []
         for h in range(HALVES):
             x_half = keep.tile([P, ROW_TILES, FEATURES], BF16, name="x_half%d" % h)
@@ -59,8 +64,6 @@ def tile_kanlinear_pa_kernel(tc, x, ln_gamma, ln_beta, base_weight, base_bias, s
             for t in range(0, ROW_TILES, 2):
                 nc.sync.dma_start(out=x_half[:, t : t + 2, :], in_=rows[:, t : t + 2, :])
             x_bf.append(x_half)
-        grid_bf = const.tile([P, CHUNKS, KNOTS], BF16, name="grid_bf")
-        nc.scalar.dma_start(out=grid_bf[:], in_=grid.rearrange("o (c p) t -> p (o c) t", p=P))
         gamma_bf = const.tile([P, CHUNKS], BF16, name="gamma_bf")
         beta_bf = const.tile([P, CHUNKS], BF16, name="beta_bf")
         with nc.allow_non_contiguous_dma(reason="512 two-byte elements, one to a partition and chunk"):
@@ -85,77 +88,79 @@ def tile_kanlinear_pa_kernel(tc, x, ln_gamma, ln_beta, base_weight, base_bias, s
         nc.scalar.activation(out=warm[:], in_=one[:], func=ACT.Abs_reciprocal_sqrt)
 
         gamma = const.tile([P, CHUNKS], F32, name="gamma")
-        beta = const.tile([P, CHUNKS], F32, name="beta")
-        g = const.tile([P, CHUNKS, KNOTS], F32, name="g")
-        cube_den = const.tile([P, CHUNKS, KNOTS], F32, name="cube_den")
-        root = const.tile([P, CHUNKS, KNOTS], F32, name="root")
-        root_corr = const.tile([P, CHUNKS, KNOTS], F32, name="root_corr")
-        sq_scale = const.tile([P, CHUNKS, KNOTS], F32, name="sq_scale")
-        sq_bias = const.tile([P, CHUNKS, KNOTS], F32, name="sq_bias")
-        rest = const.tile([P, CHUNKS, 13], F32, name="rest")
-        inv = const.tile([P, CHUNKS, 13], F32, name="inv")
+        d1 = const.tile([P, CHUNKS, KNOTS - 1], F32, name="d1")
         d2 = const.tile([P, CHUNKS, KNOTS - 2], F32, name="d2")
         d3 = const.tile([P, CHUNKS, KNOTS - 3], F32, name="d3")
         d4 = const.tile([P, CHUNKS, KNOTS - 4], F32, name="d4")
-        neg_d4 = const.tile([P, CHUNKS, KNOTS - 4], F32, name="neg_d4")
+        inv_d1 = const.tile([P, CHUNKS, KNOTS - 1], F32, name="inv_d1")
         inv_d4 = const.tile([P, CHUNKS, 2], F32, name="inv_d4")
         d1_by_d4 = const.tile([P, CHUNKS, 2], F32, name="d1_by_d4")
-        d1d2 = const.tile([P, CHUNKS, 7], F32, name="d1d2")
+        d1d2_a = const.tile([P, CHUNKS, 7], F32, name="d1d2_a")
         d1d2_b = const.tile([P, CHUNKS, 7], F32, name="d1d2_b")
-        b_paired = const.tile([P, CHUNKS, 2], F32, name="b_paired")
+        prod = const.tile([P, CHUNKS, 16], F32, name="prod")
+        root = const.tile([P, CHUNKS, 16], F32, name="root")
+        root_corr = const.tile([P, CHUNKS, 16], F32, name="root_corr")
+        sq_scale = const.tile([P, CHUNKS, 16], F32, name="sq_scale")
+        sq_bias = const.tile([P, CHUNKS, KNOTS], F32, name="sq_bias")
+        inv_prod = const.tile([P, CHUNKS, 4], F32, name="inv_prod")
+        neg_ratio = const.tile([P, CHUNKS, 3], F32, name="neg_ratio")
         l_inner = const.tile([P, CHUNKS, BASES], F32, name="l_inner")
         r_inner = const.tile([P, CHUNKS, BASES], F32, name="r_inner")
-        r_first = const.tile([P, CHUNKS, 5], F32, name="r_first")
-        d1 = rest[:, :, 0:9]
+        r_paired = const.tile([P, CHUNKS, 2], F32, name="r_paired")
+        to_a6 = const.tile([P, CHUNKS, 1], F32, name="to_a6")
 
         def knot_differences():
-            nc.gpsimd.tensor_copy(out=g[:], in_=grid_bf[:])
-            nc.gpsimd.tensor_sub(out=d4[:], in0=g[:, :, 4:10], in1=g[:, :, 0:6])
+            nc.gpsimd.tensor_sub(out=d4[:], in0=grid_bf[:, :, 4:10], in1=grid_bf[:, :, 0:6])
+            nc.gpsimd.tensor_sub(out=d1[:], in0=grid_bf[:, :, 1:10], in1=grid_bf[:, :, 0:9])
+            nc.gpsimd.tensor_sub(out=d2[:], in0=grid_bf[:, :, 2:10], in1=grid_bf[:, :, 0:8])
+            nc.gpsimd.tensor_sub(out=d3[:], in0=grid_bf[:, :, 3:10], in1=grid_bf[:, :, 0:7])
+            nc.gpsimd.tensor_mul(out=d1d2_b[:], in0=d1[:, :, 2:9], in1=d2[:, :, 1:8])
+            nc.gpsimd.tensor_mul(out=d1d2_a[:], in0=d1[:, :, 0:7], in1=d2[:, :, 0:7])
+            nc.gpsimd.tensor_mul(out=prod[:, :, 7:14], in0=d1d2_b[:], in1=d3[:])
+            nc.gpsimd.tensor_mul(out=prod[:, :, 0:7], in0=d1d2_a[:], in1=d3[:])
+
+        def knot_inverses():
+            nc.vector.reciprocal(out=inv_d4[:], in_=d4[:, :, 3:6:2])
+            nc.vector.reciprocal(out=inv_d1[:], in_=d1[:])
 
         def knot_products():
-            nc.gpsimd.tensor_sub(out=d1, in0=g[:, :, 1:10], in1=g[:, :, 0:9])
-            nc.gpsimd.tensor_sub(out=d2[:], in0=g[:, :, 2:10], in1=g[:, :, 0:8])
-            nc.gpsimd.tensor_sub(out=d3[:], in0=g[:, :, 3:10], in1=g[:, :, 0:7])
-            nc.gpsimd.tensor_mul(out=d1d2_b[:], in0=d1[:, :, 2:9], in1=d2[:, :, 1:8])
-            nc.gpsimd.tensor_mul(out=d1d2[:], in0=d1[:, :, 0:7], in1=d2[:, :, 0:7])
-            nc.gpsimd.tensor_mul(out=cube_den[:, :, 0:6], in0=d1d2[:, :, 0:6], in1=d3[:, :, 0:6])
-            nc.gpsimd.tensor_mul(out=cube_den[:, :, 7:10:2], in0=d1d2_b[:, :, 4:7:2], in1=d3[:, :, 4:7:2])
-            nc.gpsimd.tensor_mul(out=b_paired[:], in0=d1d2_b[:, :, 3:6:2], in1=d3[:, :, 3:6:2])
             nc.gpsimd.tensor_mul(out=d1_by_d4[:], in0=d1[:, :, 6:9:2], in1=inv_d4[:])
-            nc.gpsimd.tensor_mul(out=cube_den[:, :, 6:9:2], in0=b_paired[:], in1=d1_by_d4[:])
+            nc.gpsimd.tensor_mul(out=prod[:, :, 14:16], in0=prod[:, :, 10:13:2], in1=d1_by_d4[:])
             nc.gpsimd.tensor_copy(out=gamma[:], in_=gamma_bf[:])
-            nc.gpsimd.tensor_copy(out=beta[:], in_=beta_bf[:])
-            nc.gpsimd.tensor_mul(out=rest[:, :, 9:12], in0=d1d2_b[:, :, 0:3], in1=d3[:, :, 0:3])
-            nc.gpsimd.tensor_mul(out=rest[:, :, 12:13], in0=d1d2[:, :, 6:7], in1=d3[:, :, 6:7])
-            nc.gpsimd.tensor_sub(out=neg_d4[:], in0=g[:, :, 0:6], in1=g[:, :, 4:10])
 
         def knot_factors():
-            nc.scalar.activation(out=root[:], in_=cube_den[:], func=ACT.Abs_reciprocal_sqrt)
+            nc.scalar.activation(out=root[:], in_=prod[:], func=ACT.Abs_reciprocal_sqrt)
 
         def knot_roots():
             nc.vector.tensor_mul(out=root_corr[:], in0=root[:], in1=root[:])
+            nc.vector.tensor_mul(out=r_inner[:], in0=d4[:], in1=inv_d1[:, :, 3:9])
             nc.vector.scalar_tensor_tensor(
-                out=root_corr[:], in0=root_corr[:], scalar=-0.5, in1=cube_den[:], op0=ALU.mult, op1=ALU.mult
+                out=root_corr[:], in0=root_corr[:], scalar=-0.5, in1=prod[:], op0=ALU.mult, op1=ALU.mult
             )
+            nc.vector.tensor_mul(out=l_inner[:], in0=d4[:], in1=inv_d1[:, :, 0:6])
             nc.vector.scalar_tensor_tensor(
                 out=sq_scale[:], in0=root_corr[:], scalar=1.5, in1=root[:], op0=ALU.add, op1=ALU.mult
             )
-            nc.vector.scalar_tensor_tensor(
-                out=sq_bias[:], in0=g[:], scalar=-1.0, in1=sq_scale[:], op0=ALU.mult, op1=ALU.mult
-            )
+            nc.vector.tensor_scalar_mul(out=r_paired[:], in0=d1_by_d4[:], scalar1=-1.0)
+            for knots, at in ((slice(6, 9, 2), slice(14, 16)), (slice(7, 10, 2), slice(11, 14, 2)), (slice(0, 6), slice(0, 6))):
+                nc.vector.scalar_tensor_tensor(
+                    out=sq_bias[:, :, knots],
+                    in0=grid_bf[:, :, knots],
+                    scalar=-1.0,
+                    in1=sq_scale[:, :, at],
+                    op0=ALU.mult,
+                    op1=ALU.mult,
+                )
 
         def knot_coefficients():
-            nc.vector.reciprocal(out=inv[:], in_=rest[:])
-            ratio = const.tile([P, CHUNKS, 3], F32, name="ratio")
-            nc.gpsimd.tensor_mul(out=ratio[:], in0=inv[:, :, 9:12], in1=cube_den[:, :, 3:6])
-            nc.gpsimd.tensor_mul(out=r_inner[:], in0=neg_d4[:], in1=inv[:, :, 3:9])
-            nc.gpsimd.tensor_mul(out=r_inner[:, :, 0:3], in0=r_inner[:, :, 0:3], in1=ratio[:])
-            nc.gpsimd.tensor_scalar_mul(out=r_first[:, :, 0:2], in0=ratio[:, :, 1:3], scalar1=-1.0)
-            nc.gpsimd.tensor_scalar_mul(out=r_first[:, :, 2:5:2], in0=d1_by_d4[:], scalar1=-1.0)
-            nc.gpsimd.tensor_mul(out=l_inner[:], in0=d4[:], in1=inv[:, :, 0:6])
-            to_a6 = const.tile([P, CHUNKS, 1], F32, name="to_a6")
-            nc.gpsimd.tensor_mul(out=to_a6[:], in0=cube_den[:, :, 6:7], in1=inv[:, :, 12:13])
-            nc.gpsimd.tensor_mul(out=l_inner[:, :, 5:6], in0=l_inner[:, :, 5:6], in1=to_a6[:])
+            nc.vector.tensor_mul(out=inv_prod[:], in0=sq_scale[:, :, 6:10], in1=sq_scale[:, :, 6:10])
+            nc.vector.tensor_scalar_mul(out=r_inner[:, :, 4:5], in0=r_inner[:, :, 4:5], scalar1=-1.0)
+            nc.vector.scalar_tensor_tensor(
+                out=neg_ratio[:], in0=inv_prod[:, :, 1:4], scalar=-1.0, in1=prod[:, :, 3:6], op0=ALU.mult, op1=ALU.mult
+            )
+            nc.vector.tensor_mul(out=to_a6[:], in0=inv_prod[:, :, 0:1], in1=prod[:, :, 14:15])
+            nc.vector.tensor_mul(out=r_inner[:, :, 0:3], in0=r_inner[:, :, 0:3], in1=neg_ratio[:])
+            nc.vector.tensor_mul(out=l_inner[:, :, 5:6], in0=l_inner[:, :, 5:6], in1=to_a6[:])
 
         xn = keep.tile([P, HALVES, CHUNKS, HALF], F32, name="xn")
         neg_mean = keep.tile([P, HALVES, ROW_TILES], F32, name="neg_mean")
@@ -174,7 +179,8 @@ def tile_kanlinear_pa_kernel(tc, x, ln_gamma, ln_beta, base_weight, base_bias, s
                 nc.vector.bn_aggr(out=mean_var[:, t, :], in_=stats[:, t, :])
             nc.vector.tensor_scalar_add(out=var_eps[:, h, :], in0=mean_var[:, :, 1], scalar1=LN_EPS)
             nc.vector.tensor_scalar_mul(out=neg_mean[:, h, :], in0=mean_var[:, :, 0], scalar1=-1.0)
-            nc.vector.reciprocal(out=inv_d4[:], in_=d4[:, :, 3:6:2])
+            if h == 0:
+                knot_inverses()
 
         sums = keep.tile([P, 2, ROW_TILES], F32, name="sums")
 
@@ -257,7 +263,7 @@ def tile_kanlinear_pa_kernel(tc, x, ln_gamma, ln_beta, base_weight, base_bias, s
                 in_=turned[(h, c)][:],
                 func=ACT.Identity,
                 scale=gamma[:, c : c + 1],
-                bias=beta[:, c : c + 1],
+                bias=beta_bf[:, c : c + 1],
             )
 
         def copy_to_psum(h, c):
@@ -282,6 +288,15 @@ def tile_kanlinear_pa_kernel(tc, x, ln_gamma, ln_beta, base_weight, base_bias, s
                 src = in_runs(planes, col0, col1)
                 if engine == "vector" and relu:
                     nc.vector.tensor_scalar_max(out=dst, in0=src, scalar1=0.0)
+                elif engine == "gpsimd":
+                    nc.gpsimd.tensor_scalar(
+                        out=grouped[:, col0:col1, :],
+                        in0=planes[:, :, col0:col1].rearrange("p t c -> p c t"),
+                        scalar1=1.0,
+                        scalar2=0.0,
+                        op0=ALU.mult,
+                        op1=ALU.add,
+                    )
                 elif engine == "vector":
                     nc.vector.tensor_copy(out=dst, in_=src)
                 elif relu:
@@ -363,40 +378,58 @@ def tile_kanlinear_pa_kernel(tc, x, ln_gamma, ln_beta, base_weight, base_bias, s
                     out=square[:],
                     in_=xn[:, h, c, :],
                     func=ACT.Square,
-                    scale=sq_scale[:, c, i : i + 1],
+                    scale=sq_scale[:, c, PROD_AT[i] : PROD_AT[i] + 1],
                     bias=sq_bias[:, c, i : i + 1],
                 )
                 squares[i] = square
 
         cube_banks = {}
+        gate = const.tile([P, 1], F32, name="gate")
+        passed = const.tile([P, 1], F32, name="passed")
 
         def emit_cubes(h, c, squares):
             cubes = {}
+            pairs = {}
             for i in CUBE_ORDER:
-                cube = work.tile([P, HALF], F32, name="cube", bufs=2 * KNOTS)
+                if i < BASES:
+                    if i // 2 not in pairs:
+                        cube_pair = work.tile([P, 2, HALF], F32, name="cube_pair", bufs=BASES)
+                        pairs[i // 2] = cube_pair
+                    cube = pairs[i // 2][:, i % 2, :]
+                else:
+                    right_cube = work.tile([P, HALF], F32, name="right_cube", bufs=2 * (KNOTS - BASES))
+                    cube = right_cube[:]
                 nc.vector.scalar_tensor_tensor(
-                    out=cube[:],
-                    in0=xn[:, h, c, :] if (h, c) == (0, 0) else v_banks[(h, c)][:],
-                    scalar=g[:, c, i : i + 1],
+                    out=cube,
+                    in0=xn[:, h, c, :] if (h, c) == (0, 0) and i in CUBE_ORDER[:FIRST_CUBES] else v_banks[(h, c)][:],
+                    scalar=grid_bf[:, c, i : i + 1],
                     in1=squares[i][:],
                     op0=ALU.subtract,
                     op1=ALU.mult,
                 )
                 cubes[i] = cube
+                if (h, c) == (0, 0) and i == CUBE_ORDER[FIRST_CUBES - 1]:
+                    nc.vector.memset(gate[:], -1.0)
+                    nc.gpsimd.tensor_copy(out=passed[:], in_=gate[:])
+                    for s in GPSIMD_WEIGHTS:
+                        regroup_weight(s, [("gpsimd", col, col + 256) for col in range(0, UNITS, 256)])
                 if (h, c) != (0, 0) and i in COPIED_CUBES:
                     copy = psum.tile([P, HALF], F32, name="copy", tag="cube%d" % i)
-                    nc.tensor.matmul(copy[:], lhsT=ident[:], rhs=cube[:], start=True, stop=True)
+                    nc.tensor.matmul(copy[:], lhsT=ident[:], rhs=cube, start=True, stop=True)
                     cube_banks[i] = copy
-            return cubes
+            return cubes, pairs
 
-        def emit_inner_left(c, j, cubes):
-            inner = work.tile([P, HALF], F32, name="inner_l", bufs=BASES)
-            nc.scalar.activation(out=inner[:], in_=cubes[j + 1][:], func=ACT.Relu, scale=l_inner[:, c, j : j + 1])
-            return inner
+        def emit_inner_left(c, j, cubes, inner_pairs):
+            if j // 2 not in inner_pairs:
+                inner_pair = work.tile([P, 2, HALF], F32, name="inner_l", bufs=BASES // 2)
+                inner_pairs[j // 2] = inner_pair
+            nc.scalar.activation(
+                out=inner_pairs[j // 2][:, j % 2, :], in_=cubes[j + 1], func=ACT.Relu, scale=l_inner[:, c, j : j + 1]
+            )
 
         def emit_inner_right(c, j, cubes):
             inner = work.tile([P, HALF], F32, name="inner_r", bufs=4)
-            nc.scalar.activation(out=inner[:], in_=cubes[j + 3][:], func=ACT.Relu, scale=r_inner[:, c, j : j + 1])
+            nc.scalar.activation(out=inner[:], in_=cubes[j + 3], func=ACT.Relu, scale=r_inner[:, c, j : j + 1])
             return inner
 
         def open_sides(c):
@@ -406,26 +439,25 @@ def tile_kanlinear_pa_kernel(tc, x, ln_gamma, ln_beta, base_weight, base_bias, s
                     right4 = work.tile([P, PACK, HALF], BF16, name="right4", bufs=4)
                     sides[s] = (left4, right4)
 
-        def side_slot(c, j, side):
+        def side_slot(c, j, side, planes=1):
             q = c * BASES + j
-            s = q // PACK
-            return sides[s][side][:, q % PACK, :]
+            return sides[q // PACK][side][:, q % PACK : q % PACK + planes, :]
 
-        def emit_left(c, j, cubes, inner, engine):
-            first = cubes[j] if engine is nc.gpsimd or j not in cube_banks else cube_banks[j]
-            engine.tensor_sub(out=side_slot(c, j, 0), in0=first[:], in1=inner[:])
+        def emit_left_pair(c, k, pairs, inner_pairs, engine):
+            engine.tensor_sub(out=side_slot(c, 2 * k, 0, 2), in0=pairs[k][:], in1=inner_pairs[k][:])
 
         def emit_right(c, j, cubes, inners):
+            side = side_slot(c, j, 1)[:, 0, :]
             if j in PAIRED_RIGHTS:
-                inner_cube = cube_banks[j + 3] if j + 3 in cube_banks else cubes[j + 3]
+                inner_cube = cube_banks[j + 3][:] if j + 3 in cube_banks else cubes[j + 3]
                 nc.vector.scalar_tensor_tensor(
-                    out=side_slot(c, j, 1), in0=inner_cube[:], scalar=0.0, in1=cubes[j + 4][:], op0=ALU.min, op1=ALU.subtract
+                    out=side, in0=inner_cube, scalar=0.0, in1=cubes[j + 4], op0=ALU.min, op1=ALU.subtract
                 )
                 return
             nc.vector.scalar_tensor_tensor(
-                out=side_slot(c, j, 1),
-                in0=cube_banks[j + 4][:] if j + 4 in cube_banks else cubes[j + 4][:],
-                scalar=r_first[:, c, j : j + 1],
+                out=side,
+                in0=cube_banks[j + 4][:] if j + 4 in cube_banks else cubes[j + 4],
+                scalar=r_paired[:, c, j // 2 - 1 : j // 2] if j + 4 in COPIED_CUBES else neg_ratio[:, c, j + 1 : j + 2],
                 in1=inners[j][:],
                 op0=ALU.mult,
                 op1=ALU.subtract,
@@ -444,14 +476,12 @@ def tile_kanlinear_pa_kernel(tc, x, ln_gamma, ln_beta, base_weight, base_bias, s
         turn(0, 0)
         knot_roots()
         scale_and_shift(0, 0)
+        copy_to_psum(0, 0)
         turn(0, 1)
         knot_coefficients()
         blocks = [(h, c) for h in range(HALVES) for c in range(CHUNKS)]
         squares = {}
         emit_squares(0, 0, squares)
-        sums_on_scalar(1, (2, 3))
-        gate = const.tile([P, 1], F32, name="gate")
-        passed = const.tile([P, 1], F32, name="passed")
         pending = []
 
         def multiply_all(passes):
@@ -462,30 +492,30 @@ def tile_kanlinear_pa_kernel(tc, x, ln_gamma, ln_beta, base_weight, base_bias, s
         for b in range(len(blocks)):
             h, c = blocks[b]
             last_block = b == len(blocks) - 1
-            lefts_by_gpsimd = () if last_block else GPSIMD_LEFTS
             ready = []
             if b > 0:
-                pc, p_cubes, p_lefts = previous
-                for j in GPSIMD_LEFTS:
-                    emit_left(pc, j, p_cubes, p_lefts[j], nc.gpsimd)
+                pc, p_pairs, p_lefts = previous
+                for k in GPSIMD_PAIRS:
+                    if k not in OWN_PAIRS[b - 1]:
+                        emit_left_pair(pc, k, p_pairs, p_lefts, nc.gpsimd)
                 ready = [(s, blocks[b - 1][0]) for s in COMPLETE[pc]]
                 if pc == 2:
                     ready.append((BASE_PASS, blocks[b - 1][0]))
             if not last_block:
                 scale_and_shift(*blocks[b + 1])
             open_sides(c)
-            cubes = emit_cubes(h, c, squares)
+            cubes, pairs = emit_cubes(h, c, squares)
             if not last_block:
                 copy_to_psum(*blocks[b + 1])
-            if b + 2 < len(blocks):
-                turn(*blocks[b + 2])
             rights = {}
             lefts = {}
             for side, j in LAST_INNER_TERMS if last_block else INNER_TERMS:
                 if side == "right":
                     rights[j] = emit_inner_right(c, j, cubes)
                 else:
-                    lefts[j] = emit_inner_left(c, j, cubes)
+                    emit_inner_left(c, j, cubes, lefts)
+            for k in OWN_PAIRS[b]:
+                emit_left_pair(c, k, pairs, lefts, nc.gpsimd)
             for j in EARLY_RIGHTS:
                 emit_right(c, j, cubes, rights)
             for s, vh in ready:
@@ -493,43 +523,48 @@ def tile_kanlinear_pa_kernel(tc, x, ln_gamma, ln_beta, base_weight, base_bias, s
                     larger_side(s)
             multiply_all(pending)
             if b == 0:
+                sums_on_scalar(1, (2, 3))
+            if b == 1:
                 mean_of_sums(1)
-            if b == 1:
-                reciprocal_root(1)
-            squares = {}
-            if b == 0:
                 deviations_on_scalar(1, range(ROW_TILES))
-            if b == 1:
+            if b == 2:
+                reciprocal_root(1)
                 normalise(1, range(ROW_TILES), "scalar")
+            if b + 2 < len(blocks):
+                turn(*blocks[b + 2])
+            squares = {}
             emit_right(c, 0, cubes, rights)
-            share = LAST_SCALAR_COLS if last_block else VALUE_SCALAR_COLS
             for s, vh in ready:
-                regroup_values(s, vh, [("scalar", 0, share), ("vector", share, HALF)])
+                regroup_values(s, vh, [("scalar", 0, SHARE[b]), ("vector", SHARE[b], HALF)])
             emit_right(c, 1, cubes, rights)
             if not last_block:
                 emit_squares(*blocks[b + 1], squares)
             for s in REGROUP_WEIGHTS[b]:
                 regroup_weight(s, [("vector", 0, UNITS)])
-            for j in range(BASES):
-                if j not in lefts_by_gpsimd:
-                    emit_left(c, j, cubes, lefts[j], nc.vector)
-                if last_block and j == 1:
-                    larger_side(4)
-                    regroup_values(4, h, [("scalar", 0, HALF)])
+            if last_block:
+                for k in range(BASES // 2):
+                    if k not in OWN_PAIRS[b]:
+                        emit_left_pair(c, k, pairs, lefts, nc.vector)
+                    if k == 0:
+                        larger_side(4)
+                        regroup_values(4, h, [("scalar", 0, HALF)])
             if last_block:
                 multiply_all(ready)
             pending = ready
             for s in REGROUP_WEIGHTS[b]:
                 quantise_weight(s, weights[s])
             if b == 0:
+                for s in GPSIMD_WEIGHTS:
+                    quantise_weight(s, weights[s])
+            if b == 1:
                 variance_of_sums(1)
                 row_root(1)
-            if b == CHUNKS + 1:
-                store(0, range(ROW_TILES))
             if not last_block:
                 nc.vector.memset(gate[:], float(b))
                 nc.gpsimd.tensor_copy(out=passed[:], in_=gate[:])
-            previous = (c, cubes, lefts)
+            if b == CHUNKS + 1:
+                store(0, range(ROW_TILES))
+            previous = (c, pairs, lefts)
         parts = [slice(0, HALF // 2), slice(HALF // 2, HALF)]
         for rows in parts:
             larger_side(5, rows)

@@ -56,26 +56,25 @@ def tile_kanlinear_pa_kernel(tc, x, ln_gamma, ln_beta, base_weight, base_bias, s
         ctx.enter_context(tc.manual_schedule())
 
         grid_bf = const.tile([P, CHUNKS, KNOTS], BF16, name="grid_bf")
-        nc.sync.dma_start(out=grid_bf[:], in_=grid.rearrange("o (c p) t -> p (o c) t", p=P))
+        nc.scalar.dma_start(out=grid_bf[:], in_=grid.rearrange("o (p c) t -> p (o c) t", c=CHUNKS))
         x_bf = []
         for h in range(HALVES):
             x_half = keep.tile([P, ROW_TILES, FEATURES], BF16, name="x_half%d" % h)
-            rows = x[h * HALF : (h + 1) * HALF, :].rearrange("(t p) f -> p t f", p=P)
+            rows = x[h * HALF : (h + 1) * HALF, :].rearrange("(p t) f -> p t f", t=ROW_TILES)
             for t in range(0, ROW_TILES, 2):
                 nc.sync.dma_start(out=x_half[:, t : t + 2, :], in_=rows[:, t : t + 2, :])
             x_bf.append(x_half)
         gamma_bf = const.tile([P, CHUNKS], BF16, name="gamma_bf")
         beta_bf = const.tile([P, CHUNKS], BF16, name="beta_bf")
-        with nc.allow_non_contiguous_dma(reason="512 two-byte elements, one to a partition and chunk"):
-            nc.scalar.dma_start(out=gamma_bf[:], in_=ln_gamma.rearrange("(c p) -> p c", p=P))
-            nc.scalar.dma_start(out=beta_bf[:], in_=ln_beta.rearrange("(c p) -> p c", p=P))
+        nc.scalar.dma_start(out=gamma_bf[:], in_=ln_gamma.rearrange("(p c) -> p c", c=CHUNKS))
+        nc.scalar.dma_start(out=beta_bf[:], in_=ln_beta.rearrange("(p c) -> p c", c=CHUNKS))
         raw = keep.tile([P, PLANES + PACK, UNITS], BF16, name="raw")
+        spline_rows = spline_weight.rearrange("(p q) u -> p q u", q=PLANES)
         for c in range(CHUNKS):
             if c == 2:
-                nc.sync.dma_start(out=raw[:, PLANES:, :], in_=base_weight.rearrange("(c p) u -> p c u", p=P))
+                nc.sync.dma_start(out=raw[:, PLANES:, :], in_=base_weight.rearrange("(p c) u -> p c u", c=CHUNKS))
             nc.sync.dma_start(
-                out=raw[:, c * BASES : (c + 1) * BASES, :].rearrange("p j u -> p (j u)"),
-                in_=spline_weight[c * P * BASES : (c + 1) * P * BASES, :].rearrange("(p j) u -> p (j u)", j=BASES),
+                out=raw[:, c * BASES : (c + 1) * BASES, :], in_=spline_rows[:, c * BASES : (c + 1) * BASES, :]
             )
         bias_bc = const.tile([P, UNITS], BF16, name="bias_bc")
         nc.sync.dma_start(out=bias_bc[:], in_=base_bias.partition_broadcast(P))
@@ -228,10 +227,12 @@ def tile_kanlinear_pa_kernel(tc, x, ln_gamma, ln_beta, base_weight, base_bias, s
         def normalise(h, tiles, engine):
             for t in tiles:
                 z = work.tile([P, FEATURES], F32, name="z", bufs=ROW_TILES)
+                dst = z[:].rearrange("p (c q) -> p c q", c=CHUNKS)
+                src = x_bf[h][:, t, :].rearrange("p (q c) -> p c q", c=CHUNKS)
                 if engine == "vector":
                     nc.vector.tensor_scalar(
-                        out=z[:],
-                        in0=x_bf[h][:, t, :],
+                        out=dst,
+                        in0=src,
                         scalar1=neg_mean[:, h, t : t + 1],
                         scalar2=rstd[:, h, t : t + 1],
                         op0=ALU.add,
@@ -239,8 +240,8 @@ def tile_kanlinear_pa_kernel(tc, x, ln_gamma, ln_beta, base_weight, base_bias, s
                     )
                 else:
                     nc.scalar.activation(
-                        out=z[:],
-                        in_=x_bf[h][:, t, :],
+                        out=dst,
+                        in_=src,
                         func=ACT.Identity,
                         scale=rstd[:, h, t : t + 1],
                         bias=shift[:, h, t : t + 1],
@@ -346,8 +347,8 @@ def tile_kanlinear_pa_kernel(tc, x, ln_gamma, ln_beta, base_weight, base_bias, s
             for m in row_tiles:
                 result = work.tile([P, UNITS], F32, name="result", bufs=4)
                 nc.vector.tensor_add(out=result[:], in0=acc[(h, m)][:], in1=bias_bc[:])
-                row0 = h * HALF + m * P
-                nc.sync.dma_start(out=out[row0 : row0 + P, :], in_=result[:])
+                rows = out[h * HALF : (h + 1) * HALF, :].rearrange("(p t) u -> p t u", t=ROW_TILES)
+                nc.sync.dma_start(out=rows[:, m, :], in_=result[:])
 
         def multiply(s, h, grouped):
             codes, scales = codes_and_scales()

@@ -27,6 +27,9 @@ SPLINE_PASSES = PLANES // PACK
 BASE_PASS = SPLINE_PASSES
 LN_EPS = 0.001
 RUN = 4
+VALUE_SCALAR_COLS = 256
+EARLY_SCALAR_COLS = 128
+LAST_SCALAR_COLS = HALF
 TAIL_SCALAR_COLS = 96
 CUBE_ORDER = (6, 8, 7, 5, 9, 4, 3, 2, 1, 0)
 INNER_TERMS = (("right", 4), ("right", 2), ("left", 5), ("left", 4), ("right", 1), ("right", 0), ("left", 3), ("left", 2), ("left", 1), ("left", 0))
@@ -36,11 +39,9 @@ GPSIMD_PAIRS = (2, 1, 0)
 COPIED_CUBES = (6, 8)
 PAIRED_RIGHTS = (3, 5)
 COMPLETE = [[0], [1, 2], [3], [4, 5]]
-REGROUP_WEIGHTS = [[0], [2, 3], [6, 4], [5], [], [], [], []]
+REGROUP_WEIGHTS = [[0], [3], [6, 4], [5], [], [], [], []]
 
-SHARE = (0, 192, 192, 256, 256, 256, 256, 512)
-FIRST_CUBES = 2
-GPSIMD_WEIGHTS = (1,)
+GPSIMD_WEIGHTS = ((1, UNITS), (2, UNITS // 2))
 OWN_PAIRS = ((), (), (), (), (), (), (2,), (2,))
 PROD_AT = (0, 1, 2, 3, 4, 5, 14, 11, 15, 13)
 FLOPS = 2 * ROWS * (FEATURES + FEATURES * BASES) * UNITS
@@ -61,8 +62,9 @@ def tile_kanlinear_pa_kernel(tc, x, ln_gamma, ln_beta, base_weight, base_bias, s
         for h in range(HALVES):
             x_half = keep.tile([P, ROW_TILES, FEATURES], BF16, name="x_half%d" % h)
             rows = x[h * HALF : (h + 1) * HALF, :].rearrange("(p t) f -> p t f", t=ROW_TILES)
-            for t in range(0, ROW_TILES, 2):
-                nc.sync.dma_start(out=x_half[:, t : t + 2, :], in_=rows[:, t : t + 2, :])
+            step = 1 if h == 0 else 2
+            for t in range(0, ROW_TILES, step):
+                nc.sync.dma_start(out=x_half[:, t : t + step, :], in_=rows[:, t : t + step, :])
             x_bf.append(x_half)
         gamma_bf = const.tile([P, CHUNKS], BF16, name="gamma_bf")
         beta_bf = const.tile([P, CHUNKS], BF16, name="beta_bf")
@@ -152,14 +154,13 @@ def tile_kanlinear_pa_kernel(tc, x, ln_gamma, ln_beta, base_weight, base_bias, s
                 )
 
         def knot_coefficients():
-            nc.vector.tensor_mul(out=inv_prod[:], in0=sq_scale[:, :, 6:10], in1=sq_scale[:, :, 6:10])
-            nc.vector.tensor_scalar_mul(out=r_inner[:, :, 4:5], in0=r_inner[:, :, 4:5], scalar1=-1.0)
-            nc.vector.scalar_tensor_tensor(
-                out=neg_ratio[:], in0=inv_prod[:, :, 1:4], scalar=-1.0, in1=prod[:, :, 3:6], op0=ALU.mult, op1=ALU.mult
-            )
-            nc.vector.tensor_mul(out=to_a6[:], in0=inv_prod[:, :, 0:1], in1=prod[:, :, 14:15])
-            nc.vector.tensor_mul(out=r_inner[:, :, 0:3], in0=r_inner[:, :, 0:3], in1=neg_ratio[:])
-            nc.vector.tensor_mul(out=l_inner[:, :, 5:6], in0=l_inner[:, :, 5:6], in1=to_a6[:])
+            nc.gpsimd.tensor_mul(out=inv_prod[:], in0=sq_scale[:, :, 6:10], in1=sq_scale[:, :, 6:10])
+            nc.gpsimd.tensor_mul(out=neg_ratio[:], in0=inv_prod[:, :, 1:4], in1=prod[:, :, 3:6])
+            nc.gpsimd.tensor_mul(out=to_a6[:], in0=inv_prod[:, :, 0:1], in1=prod[:, :, 14:15])
+            nc.gpsimd.tensor_scalar_mul(out=neg_ratio[:], in0=neg_ratio[:], scalar1=-1.0)
+            nc.gpsimd.tensor_scalar_mul(out=r_inner[:, :, 4:5], in0=r_inner[:, :, 4:5], scalar1=-1.0)
+            nc.gpsimd.tensor_mul(out=l_inner[:, :, 5:6], in0=l_inner[:, :, 5:6], in1=to_a6[:])
+            nc.gpsimd.tensor_mul(out=r_inner[:, :, 0:3], in0=r_inner[:, :, 0:3], in1=neg_ratio[:])
 
         xn = keep.tile([P, HALVES, CHUNKS, HALF], F32, name="xn")
         neg_mean = keep.tile([P, HALVES, ROW_TILES], F32, name="neg_mean")
@@ -252,24 +253,28 @@ def tile_kanlinear_pa_kernel(tc, x, ln_gamma, ln_beta, base_weight, base_bias, s
 
         turned = {}
 
-        def turn(h, c):
-            z_t = psum.tile([P, HALF], F32, name="z_t", tag="z_t")
-            for t in range(ROW_TILES):
+        ALL = slice(0, HALF)
+        FIRST = slice(0, HALF // 2)
+        SECOND = slice(HALF // 2, HALF)
+
+        def turn(h, c, rows=ALL, tag="z_t"):
+            z_t = psum.tile([P, HALF], F32, name="z_t", tag=tag)
+            for t in range(rows.start // P, rows.stop // P):
                 nc.tensor.transpose(z_t[:, t * P : (t + 1) * P], z_tiles[(h, t)][:, c * P : (c + 1) * P], ident[:])
             turned[(h, c)] = z_t
 
-        def scale_and_shift(h, c):
+        def scale_and_shift(h, c, rows=ALL):
             nc.scalar.activation(
-                out=xn[:, h, c, :],
-                in_=turned[(h, c)][:],
+                out=xn[:, h, c, rows],
+                in_=turned[(h, c)][:, rows],
                 func=ACT.Identity,
                 scale=gamma[:, c : c + 1],
                 bias=beta_bf[:, c : c + 1],
             )
 
-        def copy_to_psum(h, c):
-            v = psum.tile([P, HALF], F32, name="v", tag="v")
-            nc.tensor.matmul(v[:], lhsT=ident[:], rhs=xn[:, h, c, :], start=True, stop=True)
+        def copy_to_psum(h, c, rows=ALL, tag="v"):
+            v = psum.tile([P, HALF], F32, name="v", tag=tag)
+            nc.tensor.matmul(v[:, rows], lhsT=ident[:], rhs=xn[:, h, c, rows], start=True, stop=True)
             v_banks[(h, c)] = v
 
         def in_runs(planes, col0, col1):
@@ -343,10 +348,15 @@ def tile_kanlinear_pa_kernel(tc, x, ln_gamma, ln_beta, base_weight, base_bias, s
                     stop=(s == SPLINE_PASSES - 1),
                 )
 
-        def store(h, row_tiles):
+        def store(h, row_tiles, by_gpsimd=()):
             for m in row_tiles:
                 result = work.tile([P, UNITS], F32, name="result", bufs=4)
-                nc.vector.tensor_add(out=result[:], in0=acc[(h, m)][:], in1=bias_bc[:])
+                if m in by_gpsimd:
+                    total = work.tile([P, UNITS], F32, name="total", bufs=1)
+                    nc.scalar.copy(out=total[:], in_=acc[(h, m)][:])
+                    nc.gpsimd.tensor_add(out=result[:], in0=total[:], in1=bias_bc[:])
+                else:
+                    nc.vector.tensor_add(out=result[:], in0=acc[(h, m)][:], in1=bias_bc[:])
                 rows = out[h * HALF : (h + 1) * HALF, :].rearrange("(p t) u -> p t u", t=ROW_TILES)
                 nc.sync.dma_start(out=rows[:, m, :], in_=result[:])
 
@@ -360,7 +370,8 @@ def tile_kanlinear_pa_kernel(tc, x, ln_gamma, ln_beta, base_weight, base_bias, s
         weights = {}
 
         def regroup_weight(s, shares):
-            weights[s] = new_grouped()
+            if s not in weights:
+                weights[s] = new_grouped()
             regroup(weights[s], raw[:, s * PACK : (s + 1) * PACK, :], False, shares)
 
         def regroup_values(s, h, shares):
@@ -372,57 +383,62 @@ def tile_kanlinear_pa_kernel(tc, x, ln_gamma, ln_beta, base_weight, base_bias, s
         def larger_side(s, cols=slice(0, HALF)):
             nc.vector.tensor_max(out=sides[s][0][:, :, cols], in0=sides[s][0][:, :, cols], in1=sides[s][1][:, :, cols])
 
-        def emit_squares(h, c, squares):
+        def emit_squares(h, c, squares, rows=ALL):
             for i in CUBE_ORDER:
-                square = work.tile([P, HALF], F32, name="square", bufs=KNOTS)
+                if i not in squares:
+                    square = work.tile([P, HALF], F32, name="square", bufs=KNOTS)
+                    squares[i] = square
                 nc.scalar.activation(
-                    out=square[:],
-                    in_=xn[:, h, c, :],
+                    out=squares[i][:, rows],
+                    in_=xn[:, h, c, rows],
                     func=ACT.Square,
                     scale=sq_scale[:, c, PROD_AT[i] : PROD_AT[i] + 1],
                     bias=sq_bias[:, c, i : i + 1],
                 )
-                squares[i] = square
 
         cube_banks = {}
-        gate = const.tile([P, 1], F32, name="gate")
-        passed = const.tile([P, 1], F32, name="passed")
 
-        def emit_cubes(h, c, squares):
+        def cube_tiles():
             cubes = {}
             pairs = {}
             for i in CUBE_ORDER:
-                if i < BASES:
-                    if i // 2 not in pairs:
-                        cube_pair = work.tile([P, 2, HALF], F32, name="cube_pair", bufs=BASES)
-                        pairs[i // 2] = cube_pair
-                    cube = pairs[i // 2][:, i % 2, :]
-                else:
+                if i >= BASES:
                     right_cube = work.tile([P, HALF], F32, name="right_cube", bufs=2 * (KNOTS - BASES))
-                    cube = right_cube[:]
+                    cubes[i] = right_cube[:]
+                    continue
+                if i // 2 not in pairs:
+                    cube_pair = work.tile([P, 2, HALF], F32, name="cube_pair", bufs=BASES)
+                    pairs[i // 2] = cube_pair
+                cubes[i] = pairs[i // 2][:, i % 2, :]
+            return cubes, pairs
+
+        def emit_cubes(c, source, squares, cubes, rows=ALL):
+            for i in CUBE_ORDER:
                 nc.vector.scalar_tensor_tensor(
-                    out=cube,
-                    in0=xn[:, h, c, :] if (h, c) == (0, 0) and i in CUBE_ORDER[:FIRST_CUBES] else v_banks[(h, c)][:],
+                    out=cubes[i][:, rows],
+                    in0=source[:, rows],
                     scalar=grid_bf[:, c, i : i + 1],
-                    in1=squares[i][:],
+                    in1=squares[i][:, rows],
                     op0=ALU.subtract,
                     op1=ALU.mult,
                 )
-                cubes[i] = cube
-                if (h, c) == (0, 0) and i == CUBE_ORDER[FIRST_CUBES - 1]:
-                    nc.vector.memset(gate[:], -1.0)
-                    nc.gpsimd.tensor_copy(out=passed[:], in_=gate[:])
-                    for s in GPSIMD_WEIGHTS:
-                        regroup_weight(s, [("gpsimd", col, col + 256) for col in range(0, UNITS, 256)])
-                if (h, c) != (0, 0) and i in COPIED_CUBES:
-                    copy = psum.tile([P, HALF], F32, name="copy", tag="cube%d" % i)
-                    nc.tensor.matmul(copy[:], lhsT=ident[:], rhs=cube, start=True, stop=True)
-                    cube_banks[i] = copy
-            return cubes, pairs
+
+        def copy_cubes(cubes):
+            for i in COPIED_CUBES:
+                copy = psum.tile([P, HALF], F32, name="copy", tag="cube%d" % i)
+                nc.tensor.matmul(copy[:], lhsT=ident[:], rhs=cubes[i], start=True, stop=True)
+                cube_banks[i] = copy
+
+        gate = const.tile([P, 1], F32, name="gate")
+        passed = const.tile([P, 1], F32, name="passed")
+
+        def open_gate(number):
+            nc.vector.memset(gate[:], float(number))
+            nc.gpsimd.tensor_copy(out=passed[:], in_=gate[:])
 
         def emit_inner_left(c, j, cubes, inner_pairs):
             if j // 2 not in inner_pairs:
-                inner_pair = work.tile([P, 2, HALF], F32, name="inner_l", bufs=BASES // 2)
+                inner_pair = work.tile([P, 2, HALF], F32, name="inner_l", bufs=4)
                 inner_pairs[j // 2] = inner_pair
             nc.scalar.activation(
                 out=inner_pairs[j // 2][:, j % 2, :], in_=cubes[j + 1], func=ACT.Relu, scale=l_inner[:, c, j : j + 1]
@@ -471,19 +487,29 @@ def tile_kanlinear_pa_kernel(tc, x, ln_gamma, ln_beta, base_weight, base_bias, s
         row_root(0)
         sums_on_scalar(1, (1,))
         reciprocal_root(0)
-        normalise(0, (0, 1, 2), "vector")
+        normalise(0, (0, 1), "vector")
         knot_factors()
-        normalise(0, (3,), "scalar")
-        turn(0, 0)
+        turn(0, 0, FIRST)
         knot_roots()
-        scale_and_shift(0, 0)
-        copy_to_psum(0, 0)
-        turn(0, 1)
-        knot_coefficients()
+        scale_and_shift(0, 0, FIRST)
+        copy_to_psum(0, 0, FIRST)
+        first_v = v_banks[(0, 0)]
+        normalise(0, (2, 3), "vector")
+        turn(0, 0, SECOND, "acc0")
         blocks = [(h, c) for h in range(HALVES) for c in range(CHUNKS)]
         squares = {}
-        emit_squares(0, 0, squares)
+        emit_squares(0, 0, squares, FIRST)
+        knot_coefficients()
+        scale_and_shift(0, 0, SECOND)
+        copy_to_psum(0, 0, SECOND, "acc1")
+        turn(0, 1)
+        emit_squares(0, 0, squares, SECOND)
         pending = []
+
+        def keep_warm(count):
+            unread_bank = psum.tile([P, HALF], F32, name="unread_bank", tag="z_t")
+            for i in range(count):
+                nc.tensor.transpose(unread_bank[:, (i % ROW_TILES) * P : (i % ROW_TILES + 1) * P], ident[:], ident[:])
 
         def multiply_all(passes):
             for s, vh in passes:
@@ -505,7 +531,16 @@ def tile_kanlinear_pa_kernel(tc, x, ln_gamma, ln_beta, base_weight, base_bias, s
             if not last_block:
                 scale_and_shift(*blocks[b + 1])
             open_sides(c)
-            cubes, pairs = emit_cubes(h, c, squares)
+            cubes, pairs = cube_tiles()
+            if b == 0:
+                open_gate(-1)
+                for s, columns in GPSIMD_WEIGHTS:
+                    regroup_weight(s, [("gpsimd", col, col + UNITS // 2) for col in range(0, columns, UNITS // 2)])
+                emit_cubes(c, first_v, squares, cubes, FIRST)
+                emit_cubes(c, v_banks[(h, c)], squares, cubes, SECOND)
+            else:
+                emit_cubes(c, v_banks[(h, c)], squares, cubes)
+                copy_cubes(cubes)
             if not last_block:
                 copy_to_psum(*blocks[b + 1])
             rights = {}
@@ -523,6 +558,8 @@ def tile_kanlinear_pa_kernel(tc, x, ln_gamma, ln_beta, base_weight, base_bias, s
                 if s != BASE_PASS:
                     larger_side(s)
             multiply_all(pending)
+            if last_block:
+                keep_warm(16)
             if b == 0:
                 sums_on_scalar(1, (2, 3))
             if b == 1:
@@ -535,13 +572,17 @@ def tile_kanlinear_pa_kernel(tc, x, ln_gamma, ln_beta, base_weight, base_bias, s
                 turn(*blocks[b + 2])
             squares = {}
             emit_right(c, 0, cubes, rights)
+            share = LAST_SCALAR_COLS if last_block else EARLY_SCALAR_COLS if b in (1, 2) else VALUE_SCALAR_COLS
             for s, vh in ready:
-                regroup_values(s, vh, [("scalar", 0, SHARE[b]), ("vector", SHARE[b], HALF)])
+                regroup_values(s, vh, [("scalar", 0, share), ("vector", share, HALF)])
             emit_right(c, 1, cubes, rights)
             if not last_block:
                 emit_squares(*blocks[b + 1], squares)
             for s in REGROUP_WEIGHTS[b]:
                 regroup_weight(s, [("vector", 0, UNITS)])
+            if b == 0:
+                for s, columns in GPSIMD_WEIGHTS:
+                    regroup_weight(s, [("vector", columns, UNITS)])
             if last_block:
                 for k in range(BASES // 2):
                     if k not in OWN_PAIRS[b]:
@@ -555,14 +596,13 @@ def tile_kanlinear_pa_kernel(tc, x, ln_gamma, ln_beta, base_weight, base_bias, s
             for s in REGROUP_WEIGHTS[b]:
                 quantise_weight(s, weights[s])
             if b == 0:
-                for s in GPSIMD_WEIGHTS:
+                for s, columns in GPSIMD_WEIGHTS:
                     quantise_weight(s, weights[s])
             if b == 1:
                 variance_of_sums(1)
                 row_root(1)
             if not last_block:
-                nc.vector.memset(gate[:], float(b))
-                nc.gpsimd.tensor_copy(out=passed[:], in_=gate[:])
+                open_gate(b)
             if b == CHUNKS + 1:
                 store(0, range(ROW_TILES))
             previous = (c, pairs, lefts)
@@ -579,4 +619,4 @@ def tile_kanlinear_pa_kernel(tc, x, ln_gamma, ln_beta, base_weight, base_bias, s
         for rows in parts:
             quantise_values(values[(5, 1)], codes, scales, rows)
             accumulate(5, 1, codes, scales, range(rows.start // P, rows.stop // P))
-        store(1, range(ROW_TILES))
+        store(1, (1, 2, 3, 0), by_gpsimd=(0,))

@@ -28,9 +28,11 @@ BASE_PASS = SPLINE_PASSES
 LN_EPS = 0.001
 RUN = 4
 VALUE_SCALAR_COLS = 256
-EARLY_SCALAR_COLS = 128
+EARLY_SCALAR_COLS = 64
 LAST_SCALAR_COLS = HALF
-TAIL_SCALAR_COLS = 96
+HEAD_COLS = 128
+UNCOPIED = 4
+TAIL_SCALAR_COLS = 128
 CUBE_ORDER = (6, 8, 7, 5, 9, 4, 3, 2, 1, 0)
 INNER_TERMS = (("right", 4), ("right", 2), ("left", 5), ("left", 4), ("right", 1), ("right", 0), ("left", 3), ("left", 2), ("left", 1), ("left", 0))
 LAST_INNER_TERMS = (("left", 5), ("left", 4), ("right", 4), ("right", 2), ("right", 1), ("right", 0), ("left", 1), ("left", 0), ("left", 3), ("left", 2))
@@ -39,7 +41,7 @@ GPSIMD_PAIRS = (2, 1, 0)
 COPIED_CUBES = (6, 8)
 PAIRED_RIGHTS = (3, 5)
 COMPLETE = [[0], [1, 2], [3], [4, 5]]
-REGROUP_WEIGHTS = [[0], [3], [6, 4], [5], [], [], [], []]
+REGROUP_WEIGHTS = [[3], [6], [4], [5], [], [], [], []]
 
 GPSIMD_WEIGHTS = ((1, UNITS), (2, UNITS // 2))
 OWN_PAIRS = ((), (), (), (), (), (), (2,), (2,))
@@ -58,26 +60,34 @@ def tile_kanlinear_pa_kernel(tc, x, ln_gamma, ln_beta, base_weight, base_bias, s
 
         grid_bf = const.tile([P, CHUNKS, KNOTS], BF16, name="grid_bf")
         nc.scalar.dma_start(out=grid_bf[:], in_=grid.rearrange("o (p c) t -> p (o c) t", c=CHUNKS))
-        x_bf = []
-        for h in range(HALVES):
-            x_half = keep.tile([P, ROW_TILES, FEATURES], BF16, name="x_half%d" % h)
-            rows = x[h * HALF : (h + 1) * HALF, :].rearrange("(p t) f -> p t f", t=ROW_TILES)
-            step = 1 if h == 0 else 2
-            for t in range(0, ROW_TILES, step):
-                nc.sync.dma_start(out=x_half[:, t : t + step, :], in_=rows[:, t : t + step, :])
-            x_bf.append(x_half)
         gamma_bf = const.tile([P, CHUNKS], BF16, name="gamma_bf")
         beta_bf = const.tile([P, CHUNKS], BF16, name="beta_bf")
         nc.scalar.dma_start(out=gamma_bf[:], in_=ln_gamma.rearrange("(p c) -> p c", c=CHUNKS))
         nc.scalar.dma_start(out=beta_bf[:], in_=ln_beta.rearrange("(p c) -> p c", c=CHUNKS))
+        x_bf = []
+        for h in range(HALVES):
+            x_half = keep.tile([P, ROW_TILES, FEATURES], BF16, name="x_half%d" % h)
+            x_bf.append(x_half)
         raw = keep.tile([P, PLANES + PACK, UNITS], BF16, name="raw")
         spline_rows = spline_weight.rearrange("(p q) u -> p q u", q=PLANES)
-        for c in range(CHUNKS):
-            if c == 2:
-                nc.sync.dma_start(out=raw[:, PLANES:, :], in_=base_weight.rearrange("(p c) u -> p c u", c=CHUNKS))
-            nc.sync.dma_start(
-                out=raw[:, c * BASES : (c + 1) * BASES, :], in_=spline_rows[:, c * BASES : (c + 1) * BASES, :]
-            )
+
+        def load_x(h, step):
+            rows = x[h * HALF : (h + 1) * HALF, :].rearrange("(p t) f -> p t f", t=ROW_TILES)
+            for t in range(0, ROW_TILES, step):
+                nc.sync.dma_start(out=x_bf[h][:, t : t + step, :], in_=rows[:, t : t + step, :])
+
+        def load_weight(s):
+            planes = slice(s * PACK, (s + 1) * PACK)
+            if s == BASE_PASS:
+                nc.sync.dma_start(out=raw[:, planes, :], in_=base_weight.rearrange("(p c) u -> p c u", c=CHUNKS))
+            else:
+                nc.sync.dma_start(out=raw[:, planes, :], in_=spline_rows[:, planes, :])
+
+        load_x(0, 1)
+        load_weight(0)
+        load_x(1, 2)
+        for s in (1, 2, 3, BASE_PASS, 4, 5):
+            load_weight(s)
         bias_bc = const.tile([P, UNITS], BF16, name="bias_bc")
         nc.sync.dma_start(out=bias_bc[:], in_=base_bias.partition_broadcast(P))
 
@@ -163,36 +173,37 @@ def tile_kanlinear_pa_kernel(tc, x, ln_gamma, ln_beta, base_weight, base_bias, s
             nc.gpsimd.tensor_mul(out=r_inner[:, :, 0:3], in0=r_inner[:, :, 0:3], in1=neg_ratio[:])
 
         xn = keep.tile([P, HALVES, CHUNKS, HALF], F32, name="xn")
-        neg_mean = keep.tile([P, HALVES, ROW_TILES], F32, name="neg_mean")
+        neg_mean = keep.tile([P, ROW_TILES], F32, name="neg_mean")
         var_eps = keep.tile([P, HALVES, ROW_TILES], F32, name="var_eps")
         rstd_guess = keep.tile([P, HALVES, ROW_TILES], F32, name="rstd_guess")
         rstd = keep.tile([P, HALVES, ROW_TILES], F32, name="rstd")
-        shift = keep.tile([P, HALVES, ROW_TILES], F32, name="shift")
+        shift = keep.tile([P, ROW_TILES], F32, name="shift")
         z_tiles = {}
+
+        mean_var = keep.tile([P, ROW_TILES, 2], F32, name="mean_var")
 
         def moments_on_vector(h):
             stats = work.tile([P, ROW_TILES, 6], F32, name="stats")
-            mean_var = work.tile([P, ROW_TILES, 2], F32, name="mean_var")
             for t in range(ROW_TILES):
                 nc.vector.bn_stats(out=stats[:, t, :], in_=x_bf[h][:, t, :])
             for t in range(ROW_TILES):
                 nc.vector.bn_aggr(out=mean_var[:, t, :], in_=stats[:, t, :])
             nc.vector.tensor_scalar_add(out=var_eps[:, h, :], in0=mean_var[:, :, 1], scalar1=LN_EPS)
-            nc.vector.tensor_scalar_mul(out=neg_mean[:, h, :], in0=mean_var[:, :, 0], scalar1=-1.0)
             if h == 0:
                 knot_inverses()
 
-        sums = keep.tile([P, 2, ROW_TILES], F32, name="sums")
+        squares_sum = keep.tile([P, ROW_TILES], F32, name="squares_sum")
 
         def sums_on_scalar(h, tiles):
             for t in tiles:
                 unread = work.tile([P, FEATURES], BF16, name="unread", bufs=2)
                 nc.scalar.activation(
-                    out=unread[:], in_=x_bf[h][:, t, :], func=ACT.Identity, accum_out=sums[:, 0, t : t + 1]
+                    out=unread[:],
+                    in_=x_bf[h][:, t, :],
+                    func=ACT.Identity,
+                    scale=-1.0 / FEATURES,
+                    accum_out=neg_mean[:, t : t + 1],
                 )
-
-        def mean_of_sums(h):
-            nc.vector.tensor_scalar_mul(out=neg_mean[:, h, :], in0=sums[:, 0, :], scalar1=-1.0 / FEATURES)
 
         def deviations_on_scalar(h, tiles):
             for t in tiles:
@@ -201,17 +212,23 @@ def tile_kanlinear_pa_kernel(tc, x, ln_gamma, ln_beta, base_weight, base_bias, s
                     out=unread[:],
                     in_=x_bf[h][:, t, :],
                     func=ACT.Square,
-                    bias=neg_mean[:, h, t : t + 1],
-                    accum_out=sums[:, 1, t : t + 1],
+                    bias=neg_mean[:, t : t + 1],
+                    accum_out=squares_sum[:, t : t + 1],
                 )
 
         def variance_of_sums(h):
             nc.vector.tensor_scalar(
-                out=var_eps[:, h, :], in0=sums[:, 1, :], scalar1=1.0 / FEATURES, scalar2=LN_EPS, op0=ALU.mult, op1=ALU.add
+                out=var_eps[:, h, :], in0=squares_sum[:], scalar1=1.0 / FEATURES, scalar2=LN_EPS, op0=ALU.mult, op1=ALU.add
             )
 
         def row_root(h):
-            nc.scalar.activation(out=rstd_guess[:, h, :], in_=var_eps[:, h, :], func=ACT.Abs_reciprocal_sqrt)
+            nc.scalar.activation(
+                out=rstd_guess[:, h, :],
+                in_=mean_var[:, :, 1] if h == 0 else squares_sum[:],
+                func=ACT.Abs_reciprocal_sqrt,
+                scale=1.0 if h == 0 else 1.0 / FEATURES,
+                bias=LN_EPS,
+            )
 
         def reciprocal_root(h):
             guess = rstd_guess[:, h, :]
@@ -223,7 +240,8 @@ def tile_kanlinear_pa_kernel(tc, x, ln_gamma, ln_beta, base_weight, base_bias, s
             nc.vector.scalar_tensor_tensor(
                 out=rstd[:, h, :], in0=corr[:], scalar=1.5, in1=guess, op0=ALU.add, op1=ALU.mult
             )
-            nc.vector.tensor_mul(out=shift[:, h, :], in0=neg_mean[:, h, :], in1=rstd[:, h, :])
+            if h == 1:
+                nc.vector.tensor_mul(out=shift[:], in0=neg_mean[:], in1=rstd[:, h, :])
 
         def normalise(h, tiles, engine):
             for t in tiles:
@@ -234,9 +252,9 @@ def tile_kanlinear_pa_kernel(tc, x, ln_gamma, ln_beta, base_weight, base_bias, s
                     nc.vector.tensor_scalar(
                         out=dst,
                         in0=src,
-                        scalar1=neg_mean[:, h, t : t + 1],
+                        scalar1=mean_var[:, t, 0:1],
                         scalar2=rstd[:, h, t : t + 1],
-                        op0=ALU.add,
+                        op0=ALU.subtract,
                         op1=ALU.mult,
                     )
                 else:
@@ -245,7 +263,7 @@ def tile_kanlinear_pa_kernel(tc, x, ln_gamma, ln_beta, base_weight, base_bias, s
                         in_=src,
                         func=ACT.Identity,
                         scale=rstd[:, h, t : t + 1],
-                        bias=shift[:, h, t : t + 1],
+                        bias=shift[:, t : t + 1],
                     )
                 z_tiles[(h, t)] = z
 
@@ -348,15 +366,10 @@ def tile_kanlinear_pa_kernel(tc, x, ln_gamma, ln_beta, base_weight, base_bias, s
                     stop=(s == SPLINE_PASSES - 1),
                 )
 
-        def store(h, row_tiles, by_gpsimd=()):
+        def store(h, row_tiles):
             for m in row_tiles:
                 result = work.tile([P, UNITS], F32, name="result", bufs=4)
-                if m in by_gpsimd:
-                    total = work.tile([P, UNITS], F32, name="total", bufs=1)
-                    nc.scalar.copy(out=total[:], in_=acc[(h, m)][:])
-                    nc.gpsimd.tensor_add(out=result[:], in0=total[:], in1=bias_bc[:])
-                else:
-                    nc.vector.tensor_add(out=result[:], in0=acc[(h, m)][:], in1=bias_bc[:])
+                nc.vector.tensor_add(out=result[:], in0=acc[(h, m)][:], in1=bias_bc[:])
                 rows = out[h * HALF : (h + 1) * HALF, :].rearrange("(p t) u -> p t u", t=ROW_TILES)
                 nc.sync.dma_start(out=rows[:, m, :], in_=result[:])
 
@@ -412,8 +425,8 @@ def tile_kanlinear_pa_kernel(tc, x, ln_gamma, ln_beta, base_weight, base_bias, s
                 cubes[i] = pairs[i // 2][:, i % 2, :]
             return cubes, pairs
 
-        def emit_cubes(c, source, squares, cubes, rows=ALL):
-            for i in CUBE_ORDER:
+        def emit_cubes(c, source, squares, cubes, rows=ALL, knots=CUBE_ORDER):
+            for i in knots:
                 nc.vector.scalar_tensor_tensor(
                     out=cubes[i][:, rows],
                     in0=source[:, rows],
@@ -429,12 +442,12 @@ def tile_kanlinear_pa_kernel(tc, x, ln_gamma, ln_beta, base_weight, base_bias, s
                 nc.tensor.matmul(copy[:], lhsT=ident[:], rhs=cubes[i], start=True, stop=True)
                 cube_banks[i] = copy
 
-        gate = const.tile([P, 1], F32, name="gate")
-        passed = const.tile([P, 1], F32, name="passed")
+        passed = const.tile([P, 1], BF16, name="passed")
+        passed_word = const.tile([P, 1], U32, name="passed_word")
+        passed_float = const.tile([P, 1], F32, name="passed_float")
 
-        def open_gate(number):
-            nc.vector.memset(gate[:], float(number))
-            nc.gpsimd.tensor_copy(out=passed[:], in_=gate[:])
+        def open_gate(written, copied):
+            nc.gpsimd.tensor_copy(out=copied[:], in_=written)
 
         def emit_inner_left(c, j, cubes, inner_pairs):
             if j // 2 not in inner_pairs:
@@ -483,12 +496,13 @@ def tile_kanlinear_pa_kernel(tc, x, ln_gamma, ln_beta, base_weight, base_bias, s
         knot_differences()
         moments_on_vector(0)
         knot_products()
-        sums_on_scalar(1, (0,))
+        regroup_weight(0, [("scalar", 0, HEAD_COLS)])
         row_root(0)
-        sums_on_scalar(1, (1,))
+        regroup_weight(0, [("scalar", HEAD_COLS, UNITS)])
         reciprocal_root(0)
         normalise(0, (0, 1), "vector")
         knot_factors()
+        sums_on_scalar(1, (0,))
         turn(0, 0, FIRST)
         knot_roots()
         scale_and_shift(0, 0, FIRST)
@@ -533,10 +547,11 @@ def tile_kanlinear_pa_kernel(tc, x, ln_gamma, ln_beta, base_weight, base_bias, s
             open_sides(c)
             cubes, pairs = cube_tiles()
             if b == 0:
-                open_gate(-1)
+                emit_cubes(c, xn[:, h, c, :], squares, cubes, FIRST, CUBE_ORDER[:UNCOPIED])
+                open_gate(cubes[CUBE_ORDER[UNCOPIED - 1]][:, FIRST.stop - 1 : FIRST.stop], passed_float)
                 for s, columns in GPSIMD_WEIGHTS:
                     regroup_weight(s, [("gpsimd", col, col + UNITS // 2) for col in range(0, columns, UNITS // 2)])
-                emit_cubes(c, first_v, squares, cubes, FIRST)
+                emit_cubes(c, first_v, squares, cubes, FIRST, CUBE_ORDER[UNCOPIED:])
                 emit_cubes(c, v_banks[(h, c)], squares, cubes, SECOND)
             else:
                 emit_cubes(c, v_banks[(h, c)], squares, cubes)
@@ -561,9 +576,8 @@ def tile_kanlinear_pa_kernel(tc, x, ln_gamma, ln_beta, base_weight, base_bias, s
             if last_block:
                 keep_warm(16)
             if b == 0:
-                sums_on_scalar(1, (2, 3))
+                sums_on_scalar(1, (1, 2, 3))
             if b == 1:
-                mean_of_sums(1)
                 deviations_on_scalar(1, range(ROW_TILES))
             if b == 2:
                 reciprocal_root(1)
@@ -596,13 +610,17 @@ def tile_kanlinear_pa_kernel(tc, x, ln_gamma, ln_beta, base_weight, base_bias, s
             for s in REGROUP_WEIGHTS[b]:
                 quantise_weight(s, weights[s])
             if b == 0:
-                for s, columns in GPSIMD_WEIGHTS:
+                for s in range(3):
                     quantise_weight(s, weights[s])
             if b == 1:
                 variance_of_sums(1)
                 row_root(1)
             if not last_block:
-                open_gate(b)
+                if b == 0 or REGROUP_WEIGHTS[b]:
+                    last_pass = 2 if b == 0 else REGROUP_WEIGHTS[b][-1]
+                    open_gate(w_codes[:, last_pass, UNITS - 1 : UNITS], passed_word)
+                else:
+                    open_gate(side_slot(c, 1, 1)[:, 0, HALF - 1 : HALF], passed)
             if b == CHUNKS + 1:
                 store(0, range(ROW_TILES))
             previous = (c, pairs, lefts)
@@ -619,4 +637,4 @@ def tile_kanlinear_pa_kernel(tc, x, ln_gamma, ln_beta, base_weight, base_bias, s
         for rows in parts:
             quantise_values(values[(5, 1)], codes, scales, rows)
             accumulate(5, 1, codes, scales, range(rows.start // P, rows.stop // P))
-        store(1, (1, 2, 3, 0), by_gpsimd=(0,))
+        store(1, range(ROW_TILES))

from contextlib import ExitStack

import concourse.mybir as mybir
from concourse.masks import make_identity

F32 = mybir.dt.float32
BF16 = mybir.dt.bfloat16
U32 = mybir.dt.uint32
U8 = mybir.dt.uint8
FP8X4 = mybir.dt.float8_e4m3fn_x4
ALU = mybir.AluOpType
ACT = mybir.ActivationFunctionType

P = 128
PACK = 4
ROWS = 1024
FEATURES = 512
UNITS = 512
KNOTS = 10
BASES = 6
CHUNKS = FEATURES // P
HALF = 512
HALVES = ROWS // HALF
ROW_TILES = HALF // P
PLANES = CHUNKS * BASES
SPLINE_PASSES = PLANES // PACK
BASE_PASS = SPLINE_PASSES
LN_EPS = 0.001
RUN = 4
VALUE_SCALAR_COLS = 256
EARLY_SCALAR_COLS = 64
LAST_SCALAR_COLS = HALF
HEAD_COLS = 128
UNCOPIED = 4
TAIL_SCALAR_COLS = 128
CUBE_ORDER = (6, 8, 7, 5, 9, 4, 3, 2, 1, 0)
INNER_TERMS = (("right", 4), ("right", 2), ("left", 5), ("left", 4), ("right", 1), ("right", 0), ("left", 3), ("left", 2), ("left", 1), ("left", 0))
LAST_INNER_TERMS = (("left", 5), ("left", 4), ("right", 4), ("right", 2), ("right", 1), ("right", 0), ("left", 1), ("left", 0), ("left", 3), ("left", 2))
EARLY_RIGHTS = (3, 5, 2, 4)
GPSIMD_PAIRS = (2, 1, 0)
COPIED_CUBES = (6, 8)
PAIRED_RIGHTS = (3, 5)
COMPLETE = [[0], [1, 2], [3], [4, 5]]
REGROUP_WEIGHTS = [[3], [6], [4], [5], [], [], [], []]

GPSIMD_WEIGHTS = ((1, UNITS), (2, UNITS // 2))
OWN_PAIRS = ((), (), (), (), (), (), (2,), (2,))
PROD_AT = (0, 1, 2, 3, 4, 5, 14, 11, 15, 13)
FLOPS = 2 * ROWS * (FEATURES + FEATURES * BASES) * UNITS


def tile_kanlinear_pa_kernel(tc, x, ln_gamma, ln_beta, base_weight, base_bias, spline_weight, grid, out):
    nc = tc.nc
    with ExitStack() as ctx:
        const = ctx.enter_context(tc.tile_pool(name="const", bufs=1))
        keep = ctx.enter_context(tc.tile_pool(name="keep", bufs=1))
        work = ctx.enter_context(tc.tile_pool(name="work", bufs=2))
        psum = ctx.enter_context(tc.psum_pool(name="psum", bufs=1))
        ctx.enter_context(tc.manual_schedule())

        grid_bf = const.tile([P, CHUNKS, KNOTS], BF16, name="grid_bf")
        nc.scalar.dma_start(out=grid_bf[:], in_=grid.rearrange("o (p c) t -> p (o c) t", c=CHUNKS))
        gamma_bf = const.tile([P, CHUNKS], BF16, name="gamma_bf")
        beta_bf = const.tile([P, CHUNKS], BF16, name="beta_bf")
        nc.scalar.dma_start(out=gamma_bf[:], in_=ln_gamma.rearrange("(p c) -> p c", c=CHUNKS))
        nc.scalar.dma_start(out=beta_bf[:], in_=ln_beta.rearrange("(p c) -> p c", c=CHUNKS))
        x_bf = []
        for h in range(HALVES):
            x_half = keep.tile([P, ROW_TILES, FEATURES], BF16, name="x_half%d" % h)
            x_bf.append(x_half)
        raw = keep.tile([P, PLANES + PACK, UNITS], BF16, name="raw")
        spline_rows = spline_weight.rearrange("(p q) u -> p q u", q=PLANES)

        def load_x(h, step):
            rows = x[h * HALF : (h + 1) * HALF, :].rearrange("(p t) f -> p t f", t=ROW_TILES)
            for t in range(0, ROW_TILES, step):
                nc.sync.dma_start(out=x_bf[h][:, t : t + step, :], in_=rows[:, t : t + step, :])

        def load_weight(s):
            planes = slice(s * PACK, (s + 1) * PACK)
            if s == BASE_PASS:
                nc.sync.dma_start(out=raw[:, planes, :], in_=base_weight.rearrange("(p c) u -> p c u", c=CHUNKS))
            else:
                nc.sync.dma_start(out=raw[:, planes, :], in_=spline_rows[:, planes, :])

        load_x(0, 1)
        load_weight(0)
        load_x(1, 2)
        for s in (1, 2, 3, BASE_PASS, 4, 5):
            load_weight(s)
        bias_bc = const.tile([P, UNITS], BF16, name="bias_bc")
        nc.sync.dma_start(out=bias_bc[:], in_=base_bias.partition_broadcast(P))

        ident = const.tile([P, P], F32, name="ident")
        make_identity(nc, ident[:])
        one = const.tile([P, 1], F32, name="one")
        nc.vector.memset(one[:], 1.0)
        warm = const.tile([P, 1], F32, name="warm")
        nc.scalar.activation(out=warm[:], in_=one[:], func=ACT.Abs_reciprocal_sqrt)

        gamma = const.tile([P, CHUNKS], F32, name="gamma")
        d1 = const.tile([P, CHUNKS, KNOTS - 1], F32, name="d1")
        d2 = const.tile([P, CHUNKS, KNOTS - 2], F32, name="d2")
        d3 = const.tile([P, CHUNKS, KNOTS - 3], F32, name="d3")
        d4 = const.tile([P, CHUNKS, KNOTS - 4], F32, name="d4")
        inv_d1 = const.tile([P, CHUNKS, KNOTS - 1], F32, name="inv_d1")
        inv_d4 = const.tile([P, CHUNKS, 2], F32, name="inv_d4")
        d1_by_d4 = const.tile([P, CHUNKS, 2], F32, name="d1_by_d4")
        d1d2_a = const.tile([P, CHUNKS, 7], F32, name="d1d2_a")
        d1d2_b = const.tile([P, CHUNKS, 7], F32, name="d1d2_b")
        prod = const.tile([P, CHUNKS, 16], F32, name="prod")
        root = const.tile([P, CHUNKS, 16], F32, name="root")
        root_corr = const.tile([P, CHUNKS, 16], F32, name="root_corr")
        sq_scale = const.tile([P, CHUNKS, 16], F32, name="sq_scale")
        sq_bias = const.tile([P, CHUNKS, KNOTS], F32, name="sq_bias")
        inv_prod = const.tile([P, CHUNKS, 4], F32, name="inv_prod")
        neg_ratio = const.tile([P, CHUNKS, 3], F32, name="neg_ratio")
        l_inner = const.tile([P, CHUNKS, BASES], F32, name="l_inner")
        r_inner = const.tile([P, CHUNKS, BASES], F32, name="r_inner")
        r_paired = const.tile([P, CHUNKS, 2], F32, name="r_paired")
        to_a6 = const.tile([P, CHUNKS, 1], F32, name="to_a6")

        def knot_differences():
            nc.gpsimd.tensor_sub(out=d4[:], in0=grid_bf[:, :, 4:10], in1=grid_bf[:, :, 0:6])
            nc.gpsimd.tensor_sub(out=d1[:], in0=grid_bf[:, :, 1:10], in1=grid_bf[:, :, 0:9])
            nc.gpsimd.tensor_sub(out=d2[:], in0=grid_bf[:, :, 2:10], in1=grid_bf[:, :, 0:8])
            nc.gpsimd.tensor_sub(out=d3[:], in0=grid_bf[:, :, 3:10], in1=grid_bf[:, :, 0:7])
            nc.gpsimd.tensor_mul(out=d1d2_b[:], in0=d1[:, :, 2:9], in1=d2[:, :, 1:8])
            nc.gpsimd.tensor_mul(out=d1d2_a[:], in0=d1[:, :, 0:7], in1=d2[:, :, 0:7])
            nc.gpsimd.tensor_mul(out=prod[:, :, 7:14], in0=d1d2_b[:], in1=d3[:])
            nc.gpsimd.tensor_mul(out=prod[:, :, 0:7], in0=d1d2_a[:], in1=d3[:])

        def knot_inverses():
            nc.vector.reciprocal(out=inv_d4[:], in_=d4[:, :, 3:6:2])
            nc.vector.reciprocal(out=inv_d1[:], in_=d1[:])

        def knot_products():
            nc.gpsimd.tensor_mul(out=d1_by_d4[:], in0=d1[:, :, 6:9:2], in1=inv_d4[:])
            nc.gpsimd.tensor_mul(out=prod[:, :, 14:16], in0=prod[:, :, 10:13:2], in1=d1_by_d4[:])
            nc.gpsimd.tensor_copy(out=gamma[:], in_=gamma_bf[:])

        def knot_factors():
            nc.scalar.activation(out=root[:], in_=prod[:], func=ACT.Abs_reciprocal_sqrt)

        def knot_roots():
            nc.vector.tensor_mul(out=root_corr[:], in0=root[:], in1=root[:])
            nc.vector.tensor_mul(out=r_inner[:], in0=d4[:], in1=inv_d1[:, :, 3:9])
            nc.vector.scalar_tensor_tensor(
                out=root_corr[:], in0=root_corr[:], scalar=-0.5, in1=prod[:], op0=ALU.mult, op1=ALU.mult
            )
            nc.vector.tensor_mul(out=l_inner[:], in0=d4[:], in1=inv_d1[:, :, 0:6])
            nc.vector.scalar_tensor_tensor(
                out=sq_scale[:], in0=root_corr[:], scalar=1.5, in1=root[:], op0=ALU.add, op1=ALU.mult
            )
            nc.vector.tensor_scalar_mul(out=r_paired[:], in0=d1_by_d4[:], scalar1=-1.0)
            for knots, at in ((slice(6, 9, 2), slice(14, 16)), (slice(7, 10, 2), slice(11, 14, 2)), (slice(0, 6), slice(0, 6))):
                nc.vector.scalar_tensor_tensor(
                    out=sq_bias[:, :, knots],
                    in0=grid_bf[:, :, knots],
                    scalar=-1.0,
                    in1=sq_scale[:, :, at],
                    op0=ALU.mult,
                    op1=ALU.mult,
                )

        def knot_coefficients():
            nc.gpsimd.tensor_mul(out=inv_prod[:], in0=sq_scale[:, :, 6:10], in1=sq_scale[:, :, 6:10])
            nc.gpsimd.tensor_mul(out=neg_ratio[:], in0=inv_prod[:, :, 1:4], in1=prod[:, :, 3:6])
            nc.gpsimd.tensor_mul(out=to_a6[:], in0=inv_prod[:, :, 0:1], in1=prod[:, :, 14:15])
            nc.gpsimd.tensor_scalar_mul(out=neg_ratio[:], in0=neg_ratio[:], scalar1=-1.0)
            nc.gpsimd.tensor_scalar_mul(out=r_inner[:, :, 4:5], in0=r_inner[:, :, 4:5], scalar1=-1.0)
            nc.gpsimd.tensor_mul(out=l_inner[:, :, 5:6], in0=l_inner[:, :, 5:6], in1=to_a6[:])
            nc.gpsimd.tensor_mul(out=r_inner[:, :, 0:3], in0=r_inner[:, :, 0:3], in1=neg_ratio[:])

        xn = keep.tile([P, HALVES, CHUNKS, HALF], F32, name="xn")
        neg_mean = keep.tile([P, ROW_TILES], F32, name="neg_mean")
        var_eps = keep.tile([P, HALVES, ROW_TILES], F32, name="var_eps")
        rstd_guess = keep.tile([P, HALVES, ROW_TILES], F32, name="rstd_guess")
        rstd = keep.tile([P, HALVES, ROW_TILES], F32, name="rstd")
        shift = keep.tile([P, ROW_TILES], F32, name="shift")
        z_tiles = {}

        mean_var = keep.tile([P, ROW_TILES, 2], F32, name="mean_var")

        def moments_on_vector(h):
            stats = work.tile([P, ROW_TILES, 6], F32, name="stats")
            for t in range(ROW_TILES):
                nc.vector.bn_stats(out=stats[:, t, :], in_=x_bf[h][:, t, :])
            for t in range(ROW_TILES):
                nc.vector.bn_aggr(out=mean_var[:, t, :], in_=stats[:, t, :])
            nc.vector.tensor_scalar_add(out=var_eps[:, h, :], in0=mean_var[:, :, 1], scalar1=LN_EPS)
            if h == 0:
                knot_inverses()

        squares_sum = keep.tile([P, ROW_TILES], F32, name="squares_sum")

        def sums_on_scalar(h, tiles):
            for t in tiles:
                unread = work.tile([P, FEATURES], BF16, name="unread", bufs=2)
                nc.scalar.activation(
                    out=unread[:],
                    in_=x_bf[h][:, t, :],
                    func=ACT.Identity,
                    scale=-1.0 / FEATURES,
                    accum_out=neg_mean[:, t : t + 1],
                )

        def deviations_on_scalar(h, tiles):
            for t in tiles:
                unread = work.tile([P, FEATURES], BF16, name="unread", bufs=2)
                nc.scalar.activation(
                    out=unread[:],
                    in_=x_bf[h][:, t, :],
                    func=ACT.Square,
                    bias=neg_mean[:, t : t + 1],
                    accum_out=squares_sum[:, t : t + 1],
                )

        def variance_of_sums(h):
            nc.vector.tensor_scalar(
                out=var_eps[:, h, :], in0=squares_sum[:], scalar1=1.0 / FEATURES, scalar2=LN_EPS, op0=ALU.mult, op1=ALU.add
            )

        def row_root(h):
            nc.scalar.activation(
                out=rstd_guess[:, h, :],
                in_=mean_var[:, :, 1] if h == 0 else squares_sum[:],
                func=ACT.Abs_reciprocal_sqrt,
                scale=1.0 if h == 0 else 1.0 / FEATURES,
                bias=LN_EPS,
            )

        def reciprocal_root(h):
            guess = rstd_guess[:, h, :]
            corr = work.tile([P, ROW_TILES], F32, name="corr")
            nc.vector.tensor_mul(out=corr[:], in0=guess, in1=guess)
            nc.vector.scalar_tensor_tensor(
                out=corr[:], in0=corr[:], scalar=-0.5, in1=var_eps[:, h, :], op0=ALU.mult, op1=ALU.mult
            )
            nc.vector.scalar_tensor_tensor(
                out=rstd[:, h, :], in0=corr[:], scalar=1.5, in1=guess, op0=ALU.add, op1=ALU.mult
            )
            if h == 1:
                nc.vector.tensor_mul(out=shift[:], in0=neg_mean[:], in1=rstd[:, h, :])

        def normalise(h, tiles, engine):
            for t in tiles:
                z = work.tile([P, FEATURES], F32, name="z", bufs=ROW_TILES)
                dst = z[:].rearrange("p (c q) -> p c q", c=CHUNKS)
                src = x_bf[h][:, t, :].rearrange("p (q c) -> p c q", c=CHUNKS)
                if engine == "vector":
                    nc.vector.tensor_scalar(
                        out=dst,
                        in0=src,
                        scalar1=mean_var[:, t, 0:1],
                        scalar2=rstd[:, h, t : t + 1],
                        op0=ALU.subtract,
                        op1=ALU.mult,
                    )
                else:
                    nc.scalar.activation(
                        out=dst,
                        in_=src,
                        func=ACT.Identity,
                        scale=rstd[:, h, t : t + 1],
                        bias=shift[:, t : t + 1],
                    )
                z_tiles[(h, t)] = z

        v_banks = {}

        turned = {}

        ALL = slice(0, HALF)
        FIRST = slice(0, HALF // 2)
        SECOND = slice(HALF // 2, HALF)

        def turn(h, c, rows=ALL, tag="z_t"):
            z_t = psum.tile([P, HALF], F32, name="z_t", tag=tag)
            for t in range(rows.start // P, rows.stop // P):
                nc.tensor.transpose(z_t[:, t * P : (t + 1) * P], z_tiles[(h, t)][:, c * P : (c + 1) * P], ident[:])
            turned[(h, c)] = z_t

        def scale_and_shift(h, c, rows=ALL):
            nc.scalar.activation(
                out=xn[:, h, c, rows],
                in_=turned[(h, c)][:, rows],
                func=ACT.Identity,
                scale=gamma[:, c : c + 1],
                bias=beta_bf[:, c : c + 1],
            )

        def copy_to_psum(h, c, rows=ALL, tag="v"):
            v = psum.tile([P, HALF], F32, name="v", tag=tag)
            nc.tensor.matmul(v[:, rows], lhsT=ident[:], rhs=xn[:, h, c, rows], start=True, stop=True)
            v_banks[(h, c)] = v

        def in_runs(planes, col0, col1):
            return planes[:, :, col0:col1].rearrange("p t (c i) -> p c t i", i=RUN)

        def words(grouped, col0, col1):
            return grouped[:, col0:col1, :].rearrange("p (c i) t -> p c t i", i=RUN)

        def new_grouped():
            return work.tile([P, HALF, PACK], BF16, name="grouped", align_bytes=64, bufs=5)

        def regroup(grouped, planes, relu, shares):
            for engine, col0, col1 in shares:
                if col0 == col1:
                    continue
                dst = words(grouped, col0, col1)
                src = in_runs(planes, col0, col1)
                if engine == "vector" and relu:
                    nc.vector.tensor_scalar_max(out=dst, in0=src, scalar1=0.0)
                elif engine == "gpsimd":
                    nc.gpsimd.tensor_scalar(
                        out=grouped[:, col0:col1, :],
                        in0=planes[:, :, col0:col1].rearrange("p t c -> p c t"),
                        scalar1=1.0,
                        scalar2=0.0,
                        op0=ALU.mult,
                        op1=ALU.add,
                    )
                elif engine == "vector":
                    nc.vector.tensor_copy(out=dst, in_=src)
                elif relu:
                    nc.scalar.activation(out=dst, in_=src, func=ACT.Relu)
                else:
                    nc.scalar.copy(out=dst, in_=src)

        w_codes = keep.tile([P, SPLINE_PASSES + 1, UNITS], U32, name="w_codes", align_bytes=64)
        w_scales = keep.tile([P, SPLINE_PASSES + 1, UNITS], U8, name="w_scales", align_bytes=64)

        def quantise_weight(s, grouped):
            nc.vector.quantize_mx(
                out=w_codes[:, s, :].bitcast(FP8X4),
                scales=w_scales[:, s, :],
                in_=grouped[:].rearrange("p u t -> p (u t)"),
            )

        acc = {}

        def quantise_values(grouped, codes, scales, rows):
            nc.vector.quantize_mx(
                out=codes[:, rows].bitcast(FP8X4),
                scales=scales[:, rows],
                in_=grouped[:, rows, :].rearrange("p n t -> p (n t)"),
            )

        def codes_and_scales():
            codes = work.tile([P, HALF], U32, name="codes", align_bytes=64, bufs=3)
            scales = work.tile([P, HALF], U8, name="scales", align_bytes=64, bufs=3)
            return codes, scales

        def accumulate(s, h, codes, scales, row_tiles):
            for m in row_tiles:
                if s == 0:
                    acc[(h, m)] = psum.tile([P, UNITS], F32, name="acc", tag="acc%d" % m)
                nc.tensor.matmul_mx(
                    out=acc[(h, m)][:],
                    lhsT=codes[:, m * P : (m + 1) * P].bitcast(FP8X4),
                    lhsT_scale=scales[:, m * P : (m + 1) * P],
                    rhs=w_codes[:, s, :].bitcast(FP8X4),
                    rhs_scale=w_scales[:, s, :],
                    start=(s == 0),
                    stop=(s == SPLINE_PASSES - 1),
                )

        def store(h, row_tiles):
            for m in row_tiles:
                result = work.tile([P, UNITS], F32, name="result", bufs=4)
                nc.vector.tensor_add(out=result[:], in0=acc[(h, m)][:], in1=bias_bc[:])
                rows = out[h * HALF : (h + 1) * HALF, :].rearrange("(p t) u -> p t u", t=ROW_TILES)
                nc.sync.dma_start(out=rows[:, m, :], in_=result[:])

        def multiply(s, h, grouped):
            codes, scales = codes_and_scales()
            quantise_values(grouped, codes, scales, slice(0, HALF))
            accumulate(s, h, codes, scales, range(ROW_TILES))

        sides = {}
        values = {}
        weights = {}

        def regroup_weight(s, shares):
            if s not in weights:
                weights[s] = new_grouped()
            regroup(weights[s], raw[:, s * PACK : (s + 1) * PACK, :], False, shares)

        def regroup_values(s, h, shares):
            if (s, h) not in values:
                values[(s, h)] = new_grouped()
            planes = xn[:, h] if s == BASE_PASS else sides[s][0][:]
            regroup(values[(s, h)], planes, True, shares)

        def larger_side(s, cols=slice(0, HALF)):
            nc.vector.tensor_max(out=sides[s][0][:, :, cols], in0=sides[s][0][:, :, cols], in1=sides[s][1][:, :, cols])

        def emit_squares(h, c, squares, rows=ALL):
            for i in CUBE_ORDER:
                if i not in squares:
                    square = work.tile([P, HALF], F32, name="square", bufs=KNOTS)
                    squares[i] = square
                nc.scalar.activation(
                    out=squares[i][:, rows],
                    in_=xn[:, h, c, rows],
                    func=ACT.Square,
                    scale=sq_scale[:, c, PROD_AT[i] : PROD_AT[i] + 1],
                    bias=sq_bias[:, c, i : i + 1],
                )

        cube_banks = {}

        def cube_tiles():
            cubes = {}
            pairs = {}
            for i in CUBE_ORDER:
                if i >= BASES:
                    right_cube = work.tile([P, HALF], F32, name="right_cube", bufs=2 * (KNOTS - BASES))
                    cubes[i] = right_cube[:]
                    continue
                if i // 2 not in pairs:
                    cube_pair = work.tile([P, 2, HALF], F32, name="cube_pair", bufs=BASES)
                    pairs[i // 2] = cube_pair
                cubes[i] = pairs[i // 2][:, i % 2, :]
            return cubes, pairs

        def emit_cubes(c, source, squares, cubes, rows=ALL, knots=CUBE_ORDER):
            for i in knots:
                nc.vector.scalar_tensor_tensor(
                    out=cubes[i][:, rows],
                    in0=source[:, rows],
                    scalar=grid_bf[:, c, i : i + 1],
                    in1=squares[i][:, rows],
                    op0=ALU.subtract,
                    op1=ALU.mult,
                )

        def copy_cubes(cubes):
            for i in COPIED_CUBES:
                copy = psum.tile([P, HALF], F32, name="copy", tag="cube%d" % i)
                nc.tensor.matmul(copy[:], lhsT=ident[:], rhs=cubes[i], start=True, stop=True)
                cube_banks[i] = copy

        passed = const.tile([P, 1], BF16, name="passed")
        passed_word = const.tile([P, 1], U32, name="passed_word")
        passed_float = const.tile([P, 1], F32, name="passed_float")

        def open_gate(written, copied):
            nc.gpsimd.tensor_copy(out=copied[:], in_=written)

        def emit_inner_left(c, j, cubes, inner_pairs):
            if j // 2 not in inner_pairs:
                inner_pair = work.tile([P, 2, HALF], F32, name="inner_l", bufs=4)
                inner_pairs[j // 2] = inner_pair
            nc.scalar.activation(
                out=inner_pairs[j // 2][:, j % 2, :], in_=cubes[j + 1], func=ACT.Relu, scale=l_inner[:, c, j : j + 1]
            )

        def emit_inner_right(c, j, cubes):
            inner = work.tile([P, HALF], F32, name="inner_r", bufs=4)
            nc.scalar.activation(out=inner[:], in_=cubes[j + 3], func=ACT.Relu, scale=r_inner[:, c, j : j + 1])
            return inner

        def open_sides(c):
            for s in range(SPLINE_PASSES):
                if s * PACK // BASES == c:
                    left4 = work.tile([P, PACK, HALF], BF16, name="left4", bufs=4)
                    right4 = work.tile([P, PACK, HALF], BF16, name="right4", bufs=4)
                    sides[s] = (left4, right4)

        def side_slot(c, j, side, planes=1):
            q = c * BASES + j
            return sides[q // PACK][side][:, q % PACK : q % PACK + planes, :]

        def emit_left_pair(c, k, pairs, inner_pairs, engine):
            engine.tensor_sub(out=side_slot(c, 2 * k, 0, 2), in0=pairs[k][:], in1=inner_pairs[k][:])

        def emit_right(c, j, cubes, inners):
            side = side_slot(c, j, 1)[:, 0, :]
            if j in PAIRED_RIGHTS:
                inner_cube = cube_banks[j + 3][:] if j + 3 in cube_banks else cubes[j + 3]
                nc.vector.scalar_tensor_tensor(
                    out=side, in0=inner_cube, scalar=0.0, in1=cubes[j + 4], op0=ALU.min, op1=ALU.subtract
                )
                return
            nc.vector.scalar_tensor_tensor(
                out=side,
                in0=cube_banks[j + 4][:] if j + 4 in cube_banks else cubes[j + 4],
                scalar=r_paired[:, c, j // 2 - 1 : j // 2] if j + 4 in COPIED_CUBES else neg_ratio[:, c, j + 1 : j + 2],
                in1=inners[j][:],
                op0=ALU.mult,
                op1=ALU.subtract,
            )

        knot_differences()
        moments_on_vector(0)
        knot_products()
        regroup_weight(0, [("scalar", 0, HEAD_COLS)])
        row_root(0)
        regroup_weight(0, [("scalar", HEAD_COLS, UNITS)])
        reciprocal_root(0)
        normalise(0, (0, 1), "vector")
        knot_factors()
        sums_on_scalar(1, (0,))
        turn(0, 0, FIRST)
        knot_roots()
        scale_and_shift(0, 0, FIRST)
        copy_to_psum(0, 0, FIRST)
        first_v = v_banks[(0, 0)]
        normalise(0, (2, 3), "vector")
        turn(0, 0, SECOND, "acc0")
        blocks = [(h, c) for h in range(HALVES) for c in range(CHUNKS)]
        squares = {}
        emit_squares(0, 0, squares, FIRST)
        knot_coefficients()
        scale_and_shift(0, 0, SECOND)
        copy_to_psum(0, 0, SECOND, "acc1")
        turn(0, 1)
        emit_squares(0, 0, squares, SECOND)
        pending = []

        def keep_warm(count):
            unread_bank = psum.tile([P, HALF], F32, name="unread_bank", tag="z_t")
            for i in range(count):
                nc.tensor.transpose(unread_bank[:, (i % ROW_TILES) * P : (i % ROW_TILES + 1) * P], ident[:], ident[:])

        def multiply_all(passes):
            for s, vh in passes:
                multiply(s, vh, values[(s, vh)])

        previous = None
        for b in range(len(blocks)):
            h, c = blocks[b]
            last_block = b == len(blocks) - 1
            ready = []
            if b > 0:
                pc, p_pairs, p_lefts = previous
                for k in GPSIMD_PAIRS:
                    if k not in OWN_PAIRS[b - 1]:
                        emit_left_pair(pc, k, p_pairs, p_lefts, nc.gpsimd)
                ready = [(s, blocks[b - 1][0]) for s in COMPLETE[pc]]
                if pc == 2:
                    ready.append((BASE_PASS, blocks[b - 1][0]))
            if not last_block:
                scale_and_shift(*blocks[b + 1])
            open_sides(c)
            cubes, pairs = cube_tiles()
            if b == 0:
                emit_cubes(c, xn[:, h, c, :], squares, cubes, FIRST, CUBE_ORDER[:UNCOPIED])
                open_gate(cubes[CUBE_ORDER[UNCOPIED - 1]][:, FIRST.stop - 1 : FIRST.stop], passed_float)
                for s, columns in GPSIMD_WEIGHTS:
                    regroup_weight(s, [("gpsimd", col, col + UNITS // 2) for col in range(0, columns, UNITS // 2)])
                emit_cubes(c, first_v, squares, cubes, FIRST, CUBE_ORDER[UNCOPIED:])
                emit_cubes(c, v_banks[(h, c)], squares, cubes, SECOND)
            else:
                emit_cubes(c, v_banks[(h, c)], squares, cubes)
                copy_cubes(cubes)
            if not last_block:
                copy_to_psum(*blocks[b + 1])
            rights = {}
            lefts = {}
            for side, j in LAST_INNER_TERMS if last_block else INNER_TERMS:
                if side == "right":
                    rights[j] = emit_inner_right(c, j, cubes)
                else:
                    emit_inner_left(c, j, cubes, lefts)
            for k in OWN_PAIRS[b]:
                emit_left_pair(c, k, pairs, lefts, nc.gpsimd)
            for j in EARLY_RIGHTS:
                emit_right(c, j, cubes, rights)
            for s, vh in ready:
                if s != BASE_PASS:
                    larger_side(s)
            multiply_all(pending)
            if last_block:
                keep_warm(16)
            if b == 0:
                sums_on_scalar(1, (1, 2, 3))
            if b == 1:
                deviations_on_scalar(1, range(ROW_TILES))
            if b == 2:
                reciprocal_root(1)
                normalise(1, range(ROW_TILES), "scalar")
            if b + 2 < len(blocks):
                turn(*blocks[b + 2])
            squares = {}
            emit_right(c, 0, cubes, rights)
            share = LAST_SCALAR_COLS if last_block else EARLY_SCALAR_COLS if b in (1, 2) else VALUE_SCALAR_COLS
            for s, vh in ready:
                regroup_values(s, vh, [("scalar", 0, share), ("vector", share, HALF)])
            emit_right(c, 1, cubes, rights)
            if not last_block:
                emit_squares(*blocks[b + 1], squares)
            for s in REGROUP_WEIGHTS[b]:
                regroup_weight(s, [("vector", 0, UNITS)])
            if b == 0:
                for s, columns in GPSIMD_WEIGHTS:
                    regroup_weight(s, [("vector", columns, UNITS)])
            if last_block:
                for k in range(BASES // 2):
                    if k not in OWN_PAIRS[b]:
                        emit_left_pair(c, k, pairs, lefts, nc.vector)
                    if k == 0:
                        larger_side(4)
                        regroup_values(4, h, [("scalar", 0, HALF)])
            if last_block:
                multiply_all(ready)
            pending = ready
            for s in REGROUP_WEIGHTS[b]:
                quantise_weight(s, weights[s])
            if b == 0:
                for s in range(3):
                    quantise_weight(s, weights[s])
            if b == 1:
                variance_of_sums(1)
                row_root(1)
            if not last_block:
                if b == 0 or REGROUP_WEIGHTS[b]:
                    last_pass = 2 if b == 0 else REGROUP_WEIGHTS[b][-1]
                    open_gate(w_codes[:, last_pass, UNITS - 1 : UNITS], passed_word)
                else:
                    open_gate(side_slot(c, 1, 1)[:, 0, HALF - 1 : HALF], passed)
            if b == CHUNKS + 1:
                store(0, range(ROW_TILES))
            previous = (c, pairs, lefts)
        parts = [slice(0, HALF // 2), slice(HALF // 2, HALF)]
        for rows in parts:
            larger_side(5, rows)
        shares = []
        for rows in parts:
            cut = rows.start + TAIL_SCALAR_COLS
            shares = shares + [("scalar", rows.start, cut), ("vector", cut, rows.stop)]
        multiply(4, 1, values[(4, 1)])
        codes, scales = codes_and_scales()
        regroup_values(5, 1, shares)
        for rows in parts:
            quantise_values(values[(5, 1)], codes, scales, rows)
            accumulate(5, 1, codes, scales, range(rows.start // P, rows.stop // P))
        store(1, range(ROW_TILES))
